import numpy as np
import ml_dtypes


def mxq(x, axis, fmt="e4m3"):
    dtype, down = {"e4m3": (ml_dtypes.float8_e4m3fn, 7), "e5m2": (ml_dtypes.float8_e5m2, 14)}[fmt]
    v = np.moveaxis(np.asarray(x, np.float32).astype(ml_dtypes.bfloat16).astype(np.float64), axis, -1)
    blocks = v.reshape(v.shape[:-1] + (-1, 32))
    amax = np.abs(blocks).max(-1, keepdims=True)
    byte = np.maximum(np.where(amax > 0, np.frexp(amax)[1] - 1 + 127, 0) - down, 1)
    scale = np.exp2(byte - 127.0)
    codes = (blocks / scale).astype(np.float32).astype(dtype).astype(np.float64)
    return np.moveaxis((codes * scale).reshape(v.shape), -1, axis)


WIDE = False


def mx_kscale(k):
    if not WIDE:
        return np.ones(k)
    levels = np.array([10, -10, 5, -5, 0])
    a = np.random.permutation(np.resize(levels, k // 512 * 4)).reshape(k // 512, 4)
    idx = np.arange(k)
    return np.exp2(a[idx // 512, idx % 128 // 32])


BF16 = ml_dtypes.bfloat16


def bf(x):
    return np.asarray(x, np.float32).astype(BF16)


def f64(x):
    return np.asarray(x).astype(np.float64)


B, D, O, NC = 16384, 256, 128, 8
DEGREE = 3
X_MIN, X_MAX = -1.0, 1.0
K = D * NC


def bspline_basis(x, knots, degree):
    M = knots.shape[0]
    xe = x[..., None]
    N = np.where((xe >= knots[:-1]) & (xe < knots[1:]), 1.0, 0.0)
    for k in range(1, degree + 1):
        d1 = knots[k:M - 1] - knots[:M - k - 1]
        d2 = knots[k + 1:M] - knots[1:M - k]
        inv1 = np.where(d1 != 0, 1.0 / np.where(d1 != 0, d1, 1.0), 0.0)
        inv2 = np.where(d2 != 0, 1.0 / np.where(d2 != 0, d2, 1.0), 0.0)
        N = ((xe - knots[:M - k - 1]) * inv1 * N[..., :M - k - 1]
             + (knots[k + 1:M] - xe) * inv2 * N[..., 1:M - k])
    return N[..., :M - degree - 1]


def setup_inputs():
    h = (X_MAX - X_MIN) / (NC - DEGREE)
    grid = X_MIN + h * (np.arange(NC + DEGREE + 1) - DEGREE)
    s = mx_kscale(K)
    w = float(s.max() / s.min())
    G = 32 // NC
    hot = ((np.arange(D) // G) % 4 == 3) & (w > 1.0)
    x = np.random.standard_normal((B, D))
    x[:, hot] = X_MIN + 0.625 * h * np.random.random((B, int(hot.sum())))
    f = np.ones((D, NC))
    f[hot, DEGREE + 1:] = w
    f[hot, :DEGREE + 1] = 1.0 / w
    return {"x": bf(x),
            "coeff": bf(np.random.standard_normal((O, D, NC)) * 1.2 / np.sqrt(D) * f[None]),
            "bias": bf(np.random.standard_normal(O) * 0.3),
            "knots": bf(grid + 0.25 * h * (np.random.random(NC + DEGREE + 1) - 0.5))}


def reference(x, coeff, bias, knots):
    xc = np.clip(f64(x), X_MIN, X_MAX)
    basis = bspline_basis(xc, f64(knots), DEGREE)
    out = (mxq(basis.reshape(B, K), 1, "e4m3") @ mxq(f64(coeff).reshape(O, K), 1, "e4m3").T) + f64(bias)[None, :]
    return out

@@ -1,0 +1,198 @@
+from contextlib import ExitStack
+
+import concourse.mybir as mybir
+from concourse.masks import make_identity
+
+F32 = mybir.dt.float32
+BF16 = mybir.dt.bfloat16
+U32 = mybir.dt.uint32
+U8 = mybir.dt.uint8
+FP8X4 = mybir.dt.float8_e4m3fn_x4
+ALU = mybir.AluOpType
+ACT = mybir.ActivationFunctionType
+
+B, D, O, NC = 16384, 256, 128, 8
+K = D * NC
+FLOPS = 2 * B * K * O
+P = 128
+PASSES = 4
+NB = 1024
+NT = NB // P
+CHUNKS = B // NB
+
+
+def tile_kanlayerbspline_kernel(tc, x, coeff, bias, knots, out):
+    nc = tc.nc
+    with ExitStack() as ctx:
+        const = ctx.enter_context(tc.tile_pool(name="const", bufs=1))
+        xin = ctx.enter_context(tc.tile_pool(name="xin", bufs=2))
+        work = ctx.enter_context(tc.tile_pool(name="work", bufs=2))
+        mxp = ctx.enter_context(tc.tile_pool(name="mxp", bufs=2))
+        ps_t = ctx.enter_context(tc.psum_pool(name="ps_t", bufs=2))
+        ps_o = ctx.enter_context(tc.psum_pool(name="ps_o", bufs=2))
+
+        ident = const.tile([P, P], BF16)
+        make_identity(nc, ident[:])
+
+        kn_bf = const.tile([P, 8], BF16)
+        nc.sync.dma_start(out=kn_bf[0:P:2, :], in_=knots[0:8].partition_broadcast(64))
+        nc.sync.dma_start(out=kn_bf[1:P:2, :], in_=knots[4:12].partition_broadcast(64))
+        w_nat = const.tile([P, K], BF16)
+        nc.sync.dma_start(out=w_nat[:], in_=coeff.rearrange("o d m -> o (d m)"))
+        bias_bf = const.tile([P, O], BF16)
+        nc.sync.dma_start(out=bias_bf[:], in_=bias.partition_broadcast(P))
+
+        kn = const.tile([P, 8], F32)
+        nc.vector.tensor_copy(out=kn[:], in_=kn_bf[:])
+        negt = const.tile([P, 8], F32)
+        nc.vector.tensor_scalar_mul(out=negt[:], in0=kn[:], scalar1=-1.0)
+
+        def diff(a, b, nm):
+            d = const.tile([P, 4], F32, name=nm)
+            nc.vector.tensor_sub(out=d[:], in0=kn[:, a:a + 4], in1=kn[:, b:b + 4])
+            return d
+
+        d10 = diff(1, 0, "d10")
+        d20 = diff(2, 0, "d20")
+        d30 = diff(3, 0, "d30")
+        d40 = diff(4, 0, "d40")
+        d21 = diff(2, 1, "d21")
+        d31 = diff(3, 1, "d31")
+        d41 = diff(4, 1, "d41")
+        d32 = diff(3, 2, "d32")
+        d42 = diff(4, 2, "d42")
+        d43 = diff(4, 3, "d43")
+
+        def weight(factors, top, sign, nm):
+            prod = const.tile([P, 4], F32, name=nm + "_p")
+            nc.vector.tensor_mul(out=prod[:], in0=factors[0][:], in1=factors[1][:])
+            for f in factors[2:]:
+                nc.vector.tensor_mul(out=prod[:], in0=prod[:], in1=f[:])
+            w = const.tile([P, 4], F32, name=nm)
+            nc.vector.reciprocal(out=w[:], in_=prod[:])
+            if top is not None:
+                nc.vector.tensor_mul(out=w[:], in0=w[:], in1=top[:])
+            if sign < 0:
+                nc.vector.tensor_scalar_mul(out=w[:], in0=w[:], scalar1=-1.0)
+            return w
+
+        w0 = weight([d10, d20, d30], None, 1, "w0")
+        w1 = weight([d10, d21, d31, d41], d40, 1, "w1")
+        negw3 = weight([d30, d31, d32, d43], d40, -1, "negw3")
+        negw4 = weight([d41, d42, d43], None, -1, "negw4")
+
+        bias_f = const.tile([P, O], F32)
+        nc.vector.tensor_copy(out=bias_f[:], in_=bias_bf[:])
+
+        w_perm = const.tile([P, PASSES, 4, P], BF16)
+        nc.vector.tensor_copy(
+            out=w_perm[:], in_=w_nat[:].rearrange("o (c p t) -> o c t p", c=PASSES, t=4)
+        )
+        w_grp = const.tile([P, PASSES, O, 4], BF16, align_bytes=64)
+        for c in range(PASSES):
+            wT = ps_t.tile([P, 4, P], BF16, tag="uT")
+            for t in range(4):
+                nc.tensor.transpose(wT[:, t, :], w_perm[:, c, t, :], ident[:])
+            nc.vector.tensor_copy(out=w_grp[:, c, :, :], in_=wT[:].rearrange("p t o -> p o t"))
+        w_codes = const.tile([P, PASSES * O], U32, align_bytes=64)
+        w_scales = const.tile([P, PASSES * O], U8, align_bytes=64)
+        nc.vector.quantize_mx(
+            out=w_codes[:].bitcast(FP8X4),
+            scales=w_scales[:],
+            in_=w_grp[:].rearrange("p c o t -> p (c o t)"),
+        )
+
+        for ch in range(CHUNKS):
+            rows = slice(ch * NB, (ch + 1) * NB)
+            x_nat = xin.tile([P, NT, D], BF16)
+            nc.sync.dma_start(out=x_nat[:], in_=x[rows, :].rearrange("(p n) d -> p n d", n=NT))
+            x_clip = xin.tile([P, NT, D], BF16)
+            nc.vector.tensor_scalar(
+                out=x_clip[:], in0=x_nat[:], scalar1=-1.0, scalar2=1.0, op0=ALU.max, op1=ALU.min
+            )
+            x_dup = xin.tile([P, NT, D, 2], BF16)
+            nc.scalar.copy(
+                out=x_dup[:], in_=x_clip[:].unsqueeze(3).to_broadcast([P, NT, D, 2])
+            )
+
+            codes = mxp.tile([P, PASSES, NB], U32, align_bytes=64)
+            scales = mxp.tile([P, PASSES, NB], U8, align_bytes=64)
+
+            for c in range(PASSES):
+                uT = ps_t.tile([P, NB], BF16, tag="uT")
+                for n in range(NT):
+                    nc.tensor.transpose(
+                        uT[:, n * P:(n + 1) * P],
+                        x_dup[:, n, c * 64:(c + 1) * 64, :].rearrange("p d h -> p (d h)"),
+                        ident[:],
+                    )
+                u = work.tile([P, NB], BF16, tag="u", bufs=3)
+                nc.scalar.copy(out=u[:], in_=uT[:])
+
+                fl = work.tile([P, 4, NB], BF16, tag="fl")
+                fr = work.tile([P, 4, NB], BF16, tag="fr")
+                d3s = []
+                rms = []
+                for i in range(8):
+                    sq = work.tile([P, NB], F32, tag="sq", bufs=3)
+                    nc.scalar.activation(
+                        out=sq[:], in_=u[:], func=ACT.Square, bias=negt[:, i:i + 1], scale=1.0
+                    )
+                    d3 = work.tile([P, NB], F32, tag="d3", bufs=4)
+                    nc.vector.scalar_tensor_tensor(
+                        out=d3[:], in0=u[:], scalar=kn[:, i:i + 1], in1=sq[:],
+                        op0=ALU.subtract, op1=ALU.mult,
+                    )
+                    d3s.append(d3)
+                    if 1 <= i <= 4:
+                        rp = work.tile([P, NB], F32, tag="rp", bufs=2)
+                        nc.scalar.activation(
+                            out=rp[:], in_=d3[:], func=ACT.Relu, scale=w1[:, i - 1:i]
+                        )
+                        nc.vector.scalar_tensor_tensor(
+                            out=fl[:, i - 1, :], in0=d3s[i - 1][:], scalar=w0[:, i - 1:i], in1=rp[:],
+                            op0=ALU.mult, op1=ALU.subtract,
+                        )
+                    if i >= 4:
+                        nc.vector.scalar_tensor_tensor(
+                            out=fr[:, i - 4, :], in0=d3[:], scalar=negw4[:, i - 4:i - 3],
+                            in1=rms[i - 4][:], op0=ALU.mult, op1=ALU.subtract,
+                        )
+                    if 3 <= i <= 6:
+                        rm = work.tile([P, NB], F32, tag="rm", bufs=3)
+                        nc.scalar.activation(
+                            out=rm[:], in_=d3[:], func=ACT.Relu, scale=negw3[:, i - 3:i - 2]
+                        )
+                        rms.append(rm)
+
+                grouped = work.tile([P, NB, 4], BF16, tag="grouped", align_bytes=64)
+                nc.vector.scalar_tensor_tensor(
+                    out=grouped[:], in0=fl[:].rearrange("p t b -> p b t"), scalar=0.0,
+                    in1=fr[:].rearrange("p t b -> p b t"), op0=ALU.max, op1=ALU.max,
+                )
+                nc.vector.quantize_mx(
+                    out=codes[:, c, :].bitcast(FP8X4),
+                    scales=scales[:, c, :],
+                    in_=grouped[:].rearrange("p b t -> p (b t)"),
+                )
+
+            out_sb = xin.tile([P, NT, O], F32)
+            for g in range(NT // 4):
+                acc = ps_o.tile([P, 4, O], F32)
+                for j in range(4):
+                    n = g * 4 + j
+                    for c in range(PASSES):
+                        nc.tensor.matmul_mx(
+                            out=acc[:, j, :],
+                            lhsT=codes[:, c, n * P:(n + 1) * P].bitcast(FP8X4),
+                            lhsT_scale=scales[:, c, n * P:(n + 1) * P],
+                            rhs=w_codes[:, c * O:(c + 1) * O].bitcast(FP8X4),
+                            rhs_scale=w_scales[:, c * O:(c + 1) * O],
+                            start=(c == 0),
+                            stop=(c == PASSES - 1),
+                        )
+                nc.vector.tensor_tensor(
+                    out=out_sb[:, g * 4:(g + 1) * 4, :], in0=acc[:],
+                    in1=bias_f[:].unsqueeze(1).to_broadcast([P, 4, O]), op=ALU.add,
+                )
+            nc.sync.dma_start(out=out[rows, :].rearrange("(p n) o -> p n o", n=NT), in_=out_sb[:])

@@ -16,9 +16,11 @@ K = D * NC
 FLOPS = 2 * B * K * O
 P = 128
 PASSES = 4
-NB = 1024
-NT = NB // P
-CHUNKS = B // NB
+NBIG = 8
+NT = 2
+N = NT * D
+G = N // 4
+V_RELU_RM = True
 
 
 def tile_kanlayerbspline_kernel(tc, x, coeff, bias, knots, out):
@@ -26,30 +28,31 @@ def tile_kanlayerbspline_kernel(tc, x, coeff, bias, knots, out):
     with ExitStack() as ctx:
         const = ctx.enter_context(tc.tile_pool(name="const", bufs=1))
         xin = ctx.enter_context(tc.tile_pool(name="xin", bufs=2))
-        work = ctx.enter_context(tc.tile_pool(name="work", bufs=2))
+        sets = ctx.enter_context(tc.tile_pool(name="sets", bufs=2))
+        work = ctx.enter_context(tc.tile_pool(name="work", bufs=3))
         mxp = ctx.enter_context(tc.tile_pool(name="mxp", bufs=2))
-        ps_t = ctx.enter_context(tc.psum_pool(name="ps_t", bufs=2))
+        ps_l = ctx.enter_context(tc.psum_pool(name="ps_l", bufs=3))
+        ps_r = ctx.enter_context(tc.psum_pool(name="ps_r", bufs=3))
         ps_o = ctx.enter_context(tc.psum_pool(name="ps_o", bufs=2))
 
         ident = const.tile([P, P], BF16)
         make_identity(nc, ident[:])
+        identf = const.tile([P, P], F32)
+        make_identity(nc, identf[:])
 
-        kn_bf = const.tile([P, 8], BF16)
-        nc.sync.dma_start(out=kn_bf[0:P:2, :], in_=knots[0:8].partition_broadcast(64))
-        nc.sync.dma_start(out=kn_bf[1:P:2, :], in_=knots[4:12].partition_broadcast(64))
+        kn_bf = const.tile([P, 12], BF16)
+        nc.sync.dma_start(out=kn_bf[:], in_=knots.partition_broadcast(P))
         w_nat = const.tile([P, K], BF16)
         nc.sync.dma_start(out=w_nat[:], in_=coeff.rearrange("o d m -> o (d m)"))
         bias_bf = const.tile([P, O], BF16)
         nc.sync.dma_start(out=bias_bf[:], in_=bias.partition_broadcast(P))
 
-        kn = const.tile([P, 8], F32)
+        kn = const.tile([P, 12], F32)
         nc.vector.tensor_copy(out=kn[:], in_=kn_bf[:])
-        negt = const.tile([P, 8], F32)
-        nc.vector.tensor_scalar_mul(out=negt[:], in0=kn[:], scalar1=-1.0)
 
         def diff(a, b, nm):
-            d = const.tile([P, 4], F32, name=nm)
-            nc.vector.tensor_sub(out=d[:], in0=kn[:, a:a + 4], in1=kn[:, b:b + 4])
+            d = const.tile([P, 8], F32, name=nm)
+            nc.vector.tensor_sub(out=d[:], in0=kn[:, a:a + 8], in1=kn[:, b:b + 8])
             return d
 
         d10 = diff(1, 0, "d10")
@@ -63,34 +66,62 @@ def tile_kanlayerbspline_kernel(tc, x, coeff, bias, knots, out):
         d42 = diff(4, 2, "d42")
         d43 = diff(4, 3, "d43")
 
-        def weight(factors, top, sign, nm):
-            prod = const.tile([P, 4], F32, name=nm + "_p")
+        def weight(factors, top, nm):
+            prod = const.tile([P, 8], F32, name=nm + "_p")
             nc.vector.tensor_mul(out=prod[:], in0=factors[0][:], in1=factors[1][:])
             for f in factors[2:]:
                 nc.vector.tensor_mul(out=prod[:], in0=prod[:], in1=f[:])
-            w = const.tile([P, 4], F32, name=nm)
+            w = const.tile([P, 8], F32, name=nm)
             nc.vector.reciprocal(out=w[:], in_=prod[:])
             if top is not None:
                 nc.vector.tensor_mul(out=w[:], in0=w[:], in1=top[:])
-            if sign < 0:
-                nc.vector.tensor_scalar_mul(out=w[:], in0=w[:], scalar1=-1.0)
             return w
 
-        w0 = weight([d10, d20, d30], None, 1, "w0")
-        w1 = weight([d10, d21, d31, d41], d40, 1, "w1")
-        negw3 = weight([d30, d31, d32, d43], d40, -1, "negw3")
-        negw4 = weight([d41, d42, d43], None, -1, "negw4")
+        w0 = weight([d10, d20, d30], None, "w0")
+        w4 = weight([d41, d42, d43], None, "w4")
+        w1 = weight([d10, d21, d31, d41], d40, "w1")
+        w3 = weight([d30, d31, d32, d43], d40, "w3")
+
+        wsig = const.tile([P, 12], F32)
+        nc.vector.tensor_copy(out=wsig[:, 0:8], in_=w0[:])
+        nc.vector.tensor_copy(out=wsig[:, 8:12], in_=w4[:, 4:8])
+        sig0 = const.tile([P, 12], F32)
+        nc.scalar.activation(out=sig0[:], in_=wsig[:], func=ACT.Sqrt)
+        sig = const.tile([P, 12], F32)
+        nc.vector.reciprocal(out=sig[:], in_=sig0[:])
+        nc.vector.tensor_mul(out=sig[:], in0=sig[:], in1=wsig[:])
+        nc.vector.tensor_add(out=sig[:], in0=sig[:], in1=sig0[:])
+        nc.vector.tensor_scalar_mul(out=sig[:], in0=sig[:], scalar1=0.5)
+        beta = const.tile([P, 12], F32)
+        nc.vector.tensor_mul(out=beta[:], in0=sig[:], in1=kn[:])
+        nc.vector.tensor_scalar_mul(out=beta[:], in0=beta[:], scalar1=-1.0)
+        rweff = const.tile([P, 12], F32)
+        nc.vector.tensor_mul(out=rweff[:], in0=sig[:], in1=sig[:])
+        nc.vector.reciprocal(out=rweff[:], in_=rweff[:])
+        rp_s = const.tile([P, 8], F32)
+        nc.vector.tensor_mul(out=rp_s[:], in0=w1[:], in1=rweff[:, 1:9])
+        nc.vector.tensor_scalar_mul(out=rp_s[:, 0:7], in0=rp_s[:, 0:7], scalar1=-1.0)
+        rm_s = const.tile([P, 8], F32)
+        nc.vector.tensor_mul(out=rm_s[:], in0=w3[:], in1=rweff[:, 3:11])
+        nc.vector.tensor_scalar_mul(out=rm_s[:, 5:8], in0=rm_s[:, 5:8], scalar1=-1.0)
+        a4_s = const.tile([P, 4], F32)
+        nc.vector.tensor_mul(out=a4_s[:], in0=w4[:, 0:4], in1=rweff[:, 4:8])
+        nc.vector.tensor_scalar_mul(out=a4_s[:], in0=a4_s[:], scalar1=-1.0)
 
         bias_f = const.tile([P, O], F32)
         nc.vector.tensor_copy(out=bias_f[:], in_=bias_bf[:])
 
         w_perm = const.tile([P, PASSES, 4, P], BF16)
-        nc.vector.tensor_copy(
-            out=w_perm[:], in_=w_nat[:].rearrange("o (c p t) -> o c t p", c=PASSES, t=4)
-        )
+        wv = w_nat[:].rearrange("o (c q l h t) -> o c t q h l", c=PASSES, q=16, l=4, h=2, t=4)
+        for c in range(PASSES):
+            for t in range(4):
+                nc.vector.tensor_copy(
+                    out=w_perm[:, c, t, :].rearrange("o (q h l) -> o q h l", q=16, h=2),
+                    in_=wv[:, c, t],
+                )
         w_grp = const.tile([P, PASSES, O, 4], BF16, align_bytes=64)
         for c in range(PASSES):
-            wT = ps_t.tile([P, 4, P], BF16, tag="uT")
+            wT = ps_l.tile([P, 4, P], BF16, tag="L")
             for t in range(4):
                 nc.tensor.transpose(wT[:, t, :], w_perm[:, c, t, :], ident[:])
             nc.vector.tensor_copy(out=w_grp[:, c, :, :], in_=wT[:].rearrange("p t o -> p o t"))
@@ -102,88 +133,110 @@ def tile_kanlayerbspline_kernel(tc, x, coeff, bias, knots, out):
             in_=w_grp[:].rearrange("p c o t -> p (c o t)"),
         )
 
-        for ch in range(CHUNKS):
-            rows = slice(ch * NB, (ch + 1) * NB)
-            x_nat = xin.tile([P, NT, D], BF16)
-            nc.sync.dma_start(out=x_nat[:], in_=x[rows, :].rearrange("(p n) d -> p n d", n=NT))
-            x_clip = xin.tile([P, NT, D], BF16)
+        def plane(s, m):
+            return s[:, m % 4, :, m // 4, :]
+
+        def scaled(eng_v, dst, src, sc, relu):
+            if eng_v:
+                if relu:
+                    nc.vector.tensor_scalar(
+                        out=dst, in0=src, scalar1=sc, scalar2=0.0, op0=ALU.mult, op1=ALU.max
+                    )
+                else:
+                    nc.vector.tensor_scalar_mul(out=dst, in0=src, scalar1=sc)
+            else:
+                nc.scalar.activation(
+                    out=dst, in_=src, func=(ACT.Relu if relu else ACT.Copy), scale=sc
+                )
+
+        for big in range(B // (NBIG * P)):
+            rows = slice(big * NBIG * P, (big + 1) * NBIG * P)
+            x_nat = xin.tile([P, NBIG, D], BF16)
+            nc.sync.dma_start(out=x_nat[:], in_=x[rows, :].rearrange("(p n) d -> p n d", n=NBIG))
+            x_pos = xin.tile([P, NBIG, D], BF16)
             nc.vector.tensor_scalar(
-                out=x_clip[:], in0=x_nat[:], scalar1=-1.0, scalar2=1.0, op0=ALU.max, op1=ALU.min
+                out=x_pos[:], in0=x_nat[:], scalar1=-1.0, scalar2=1.0, op0=ALU.max, op1=ALU.min
             )
-            x_dup = xin.tile([P, NT, D, 2], BF16)
-            nc.scalar.copy(
-                out=x_dup[:], in_=x_clip[:].unsqueeze(3).to_broadcast([P, NT, D, 2])
-            )
+            x_neg = xin.tile([P, NBIG, D], BF16)
+            nc.vector.tensor_scalar_mul(out=x_neg[:], in0=x_pos[:], scalar1=-1.0)
+            out_sb = xin.tile([P, NBIG, O], F32)
 
-            codes = mxp.tile([P, PASSES, NB], U32, align_bytes=64)
-            scales = mxp.tile([P, PASSES, NB], U8, align_bytes=64)
+            for sub in range(NBIG // NT):
+                n0 = sub * NT
+                upos = x_pos[:, n0:n0 + NT, :].rearrange("p n (g l) -> p (n g) l", l=4)
+                uneg = x_neg[:, n0:n0 + NT, :].rearrange("p n (g l) -> p (n g) l", l=4)
+                uflat = x_pos[:, n0:n0 + NT, :].rearrange("p n d -> p (n d)")
+                s_a = sets.tile([P, 4, G, 2, 4], F32, tag="A")
+                s_rp = sets.tile([P, 4, G, 2, 4], F32, tag="RP")
+                s_a4 = sets.tile([P, 4, G, 2, 4], F32, tag="A4")
+                s_rm = sets.tile([P, 4, G, 2, 4], F32, tag="RM")
 
-            for c in range(PASSES):
-                uT = ps_t.tile([P, NB], BF16, tag="uT")
-                for n in range(NT):
-                    nc.tensor.transpose(
-                        uT[:, n * P:(n + 1) * P],
-                        x_dup[:, n, c * 64:(c + 1) * 64, :].rearrange("p d h -> p (d h)"),
-                        ident[:],
-                    )
-                u = work.tile([P, NB], BF16, tag="u", bufs=3)
-                nc.scalar.copy(out=u[:], in_=uT[:])
-
-                fl = work.tile([P, 4, NB], BF16, tag="fl")
-                fr = work.tile([P, 4, NB], BF16, tag="fr")
-                d3s = []
-                rms = []
-                for i in range(8):
-                    sq = work.tile([P, NB], F32, tag="sq", bufs=3)
+                for i in range(12):
+                    sq = work.tile([P, N], F32, tag="sq")
                     nc.scalar.activation(
-                        out=sq[:], in_=u[:], func=ACT.Square, bias=negt[:, i:i + 1], scale=1.0
+                        out=sq[:], in_=uflat, func=ACT.Square,
+                        bias=beta[:, i:i + 1], scale=sig[:, i:i + 1],
                     )
-                    d3 = work.tile([P, NB], F32, tag="d3", bufs=4)
-                    nc.vector.scalar_tensor_tensor(
-                        out=d3[:], in0=u[:], scalar=kn[:, i:i + 1], in1=sq[:],
-                        op0=ALU.subtract, op1=ALU.mult,
-                    )
-                    d3s.append(d3)
-                    if 1 <= i <= 4:
-                        rp = work.tile([P, NB], F32, tag="rp", bufs=2)
+                    sqv = sq[:].rearrange("p (g l) -> p g l", l=4)
+                    if i < 8:
+                        src = plane(s_a, i)
+                        nc.vector.scalar_tensor_tensor(
+                            out=src, in0=uneg, scalar=kn[:, i:i + 1], in1=sqv,
+                            op0=ALU.add, op1=ALU.mult,
+                        )
+                    else:
+                        src = plane(s_a4, i - 4)
+                        nc.vector.scalar_tensor_tensor(
+                            out=src, in0=upos, scalar=kn[:, i:i + 1], in1=sqv,
+                            op0=ALU.subtract, op1=ALU.mult,
+                        )
+                    if 1 <= i <= 8:
+                        scaled(False, plane(s_rp, i - 1), src, rp_s[:, i - 1:i], True)
+                    if 3 <= i <= 10:
+                        scaled(True, plane(s_rm, i - 3), src, rm_s[:, i - 3:i - 2], True)
+                    if 4 <= i <= 7:
+                        scaled(True, plane(s_a4, i - 4), src, a4_s[:, i - 4:i - 3], False)
+
+                codes = mxp.tile([P, PASSES, NT * P], U32, align_bytes=64)
+                scales = mxp.tile([P, PASSES, NT * P], U8, align_bytes=64)
+                for c in range(PASSES):
+                    grouped = work.tile([P, NT, P, 4], BF16, tag="grouped", align_bytes=64)
+                    for n in range(NT):
+                        g0 = n * 64 + c * 16
+                        ps_left = ps_l.tile([P, 4, P], F32, tag="L")
+                        ps_right = ps_r.tile([P, 4, P], F32, tag="R")
+                        for bank, first, second in ((ps_left, s_a, s_rp), (ps_right, s_a4, s_rm)):
+                            for t in range(4):
+                                nc.tensor.matmul(
+                                    out=bank[:, t, :],
+                                    lhsT=first[:, t, g0:g0 + 16, :, :].rearrange("p g h l -> p (g h l)"),
+                                    rhs=identf[:], is_transpose=True, start=True, stop=False,
+                                )
+                                nc.tensor.matmul(
+                                    out=bank[:, t, :],
+                                    lhsT=second[:, t, g0:g0 + 16, :, :].rearrange("p g h l -> p (g h l)"),
+                                    rhs=identf[:], is_transpose=True, start=False, stop=True,
+                                )
+                        rfr = work.tile([P, P, 4], BF16, tag="rfr")
                         nc.scalar.activation(
-                            out=rp[:], in_=d3[:], func=ACT.Relu, scale=w1[:, i - 1:i]
+                            out=rfr[:], in_=ps_right[:].rearrange("p t b -> p b t"),
+                            func=ACT.Relu, scale=-1.0,
                         )
                         nc.vector.scalar_tensor_tensor(
-                            out=fl[:, i - 1, :], in0=d3s[i - 1][:], scalar=w0[:, i - 1:i], in1=rp[:],
-                            op0=ALU.mult, op1=ALU.subtract,
+                            out=grouped[:, n, :, :], in0=ps_left[:].rearrange("p t b -> p b t"),
+                            scalar=-1.0, in1=rfr[:], op0=ALU.mult, op1=ALU.max,
                         )
-                    if i >= 4:
-                        nc.vector.scalar_tensor_tensor(
-                            out=fr[:, i - 4, :], in0=d3[:], scalar=negw4[:, i - 4:i - 3],
-                            in1=rms[i - 4][:], op0=ALU.mult, op1=ALU.subtract,
-                        )
-                    if 3 <= i <= 6:
-                        rm = work.tile([P, NB], F32, tag="rm", bufs=3)
-                        nc.scalar.activation(
-                            out=rm[:], in_=d3[:], func=ACT.Relu, scale=negw3[:, i - 3:i - 2]
-                        )
-                        rms.append(rm)
+                    nc.vector.quantize_mx(
+                        out=codes[:, c, :].bitcast(FP8X4),
+                        scales=scales[:, c, :],
+                        in_=grouped[:].rearrange("p n b t -> p (n b t)"),
+                    )
 
-                grouped = work.tile([P, NB, 4], BF16, tag="grouped", align_bytes=64)
-                nc.vector.scalar_tensor_tensor(
-                    out=grouped[:], in0=fl[:].rearrange("p t b -> p b t"), scalar=0.0,
-                    in1=fr[:].rearrange("p t b -> p b t"), op0=ALU.max, op1=ALU.max,
-                )
-                nc.vector.quantize_mx(
-                    out=codes[:, c, :].bitcast(FP8X4),
-                    scales=scales[:, c, :],
-                    in_=grouped[:].rearrange("p b t -> p (b t)"),
-                )
-
-            out_sb = xin.tile([P, NT, O], F32)
-            for g in range(NT // 4):
-                acc = ps_o.tile([P, 4, O], F32)
-                for j in range(4):
-                    n = g * 4 + j
+                acc = ps_o.tile([P, NT, O], F32)
+                for n in range(NT):
                     for c in range(PASSES):
                         nc.tensor.matmul_mx(
-                            out=acc[:, j, :],
+                            out=acc[:, n, :],
                             lhsT=codes[:, c, n * P:(n + 1) * P].bitcast(FP8X4),
                             lhsT_scale=scales[:, c, n * P:(n + 1) * P],
                             rhs=w_codes[:, c * O:(c + 1) * O].bitcast(FP8X4),
@@ -192,7 +245,7 @@ def tile_kanlayerbspline_kernel(tc, x, coeff, bias, knots, out):
                             stop=(c == PASSES - 1),
                         )
                 nc.vector.tensor_tensor(
-                    out=out_sb[:, g * 4:(g + 1) * 4, :], in0=acc[:],
-                    in1=bias_f[:].unsqueeze(1).to_broadcast([P, 4, O]), op=ALU.add,
+                    out=out_sb[:, n0:n0 + NT, :], in0=acc[:],
+                    in1=bias_f[:].unsqueeze(1).to_broadcast([P, NT, O]), op=ALU.add,
                 )
-            nc.sync.dma_start(out=out[rows, :].rearrange("(p n) o -> p n o", n=NT), in_=out_sb[:])
+            nc.sync.dma_start(out=out[rows, :].rearrange("(p n) o -> p n o", n=NBIG), in_=out_sb[:])

@@ -16,23 +16,18 @@ K = D * NC
 FLOPS = 2 * B * K * O
 P = 128
 PASSES = 4
-NBIG = 8
-NT = 2
+NT = 4
 N = NT * D
 G = N // 4
-V_RELU_RM = True
+ROUNDS = B // (NT * P)
+A4_ON_SCALAR = (0, 1)
 
 
 def tile_kanlayerbspline_kernel(tc, x, coeff, bias, knots, out):
     nc = tc.nc
     with ExitStack() as ctx:
         const = ctx.enter_context(tc.tile_pool(name="const", bufs=1))
-        xin = ctx.enter_context(tc.tile_pool(name="xin", bufs=2))
-        sets = ctx.enter_context(tc.tile_pool(name="sets", bufs=2))
-        work = ctx.enter_context(tc.tile_pool(name="work", bufs=3))
-        mxp = ctx.enter_context(tc.tile_pool(name="mxp", bufs=2))
-        ps_l = ctx.enter_context(tc.psum_pool(name="ps_l", bufs=3))
-        ps_r = ctx.enter_context(tc.psum_pool(name="ps_r", bufs=3))
+        ps_s = ctx.enter_context(tc.psum_pool(name="ps_s", bufs=6))
         ps_o = ctx.enter_context(tc.psum_pool(name="ps_o", bufs=2))
 
         ident = const.tile([P, P], BF16)
@@ -42,11 +37,6 @@ def tile_kanlayerbspline_kernel(tc, x, coeff, bias, knots, out):
 
         kn_bf = const.tile([P, 12], BF16)
         nc.sync.dma_start(out=kn_bf[:], in_=knots.partition_broadcast(P))
-        w_nat = const.tile([P, K], BF16)
-        nc.sync.dma_start(out=w_nat[:], in_=coeff.rearrange("o d m -> o (d m)"))
-        bias_bf = const.tile([P, O], BF16)
-        nc.sync.dma_start(out=bias_bf[:], in_=bias.partition_broadcast(P))
-
         kn = const.tile([P, 12], F32)
         nc.vector.tensor_copy(out=kn[:], in_=kn_bf[:])
 
@@ -100,152 +90,157 @@ def tile_kanlayerbspline_kernel(tc, x, coeff, bias, knots, out):
         nc.vector.reciprocal(out=rweff[:], in_=rweff[:])
         rp_s = const.tile([P, 8], F32)
         nc.vector.tensor_mul(out=rp_s[:], in0=w1[:], in1=rweff[:, 1:9])
-        nc.vector.tensor_scalar_mul(out=rp_s[:, 0:7], in0=rp_s[:, 0:7], scalar1=-1.0)
+        nc.vector.tensor_scalar_mul(out=rp_s[:], in0=rp_s[:], scalar1=-1.0)
         rm_s = const.tile([P, 8], F32)
         nc.vector.tensor_mul(out=rm_s[:], in0=w3[:], in1=rweff[:, 3:11])
-        nc.vector.tensor_scalar_mul(out=rm_s[:, 5:8], in0=rm_s[:, 5:8], scalar1=-1.0)
+        nc.vector.tensor_scalar_mul(out=rm_s[:], in0=rm_s[:], scalar1=-1.0)
         a4_s = const.tile([P, 4], F32)
         nc.vector.tensor_mul(out=a4_s[:], in0=w4[:, 0:4], in1=rweff[:, 4:8])
-        nc.vector.tensor_scalar_mul(out=a4_s[:], in0=a4_s[:], scalar1=-1.0)
 
         bias_f = const.tile([P, O], F32)
-        nc.vector.tensor_copy(out=bias_f[:], in_=bias_bf[:])
-
-        w_perm = const.tile([P, PASSES, 4, P], BF16)
-        wv = w_nat[:].rearrange("o (c q l h t) -> o c t q h l", c=PASSES, q=16, l=4, h=2, t=4)
-        for c in range(PASSES):
-            for t in range(4):
-                nc.vector.tensor_copy(
-                    out=w_perm[:, c, t, :].rearrange("o (q h l) -> o q h l", q=16, h=2),
-                    in_=wv[:, c, t],
-                )
-        w_grp = const.tile([P, PASSES, O, 4], BF16, align_bytes=64)
-        for c in range(PASSES):
-            wT = ps_l.tile([P, 4, P], BF16, tag="L")
-            for t in range(4):
-                nc.tensor.transpose(wT[:, t, :], w_perm[:, c, t, :], ident[:])
-            nc.vector.tensor_copy(out=w_grp[:, c, :, :], in_=wT[:].rearrange("p t o -> p o t"))
         w_codes = const.tile([P, PASSES * O], U32, align_bytes=64)
         w_scales = const.tile([P, PASSES * O], U8, align_bytes=64)
-        nc.vector.quantize_mx(
-            out=w_codes[:].bitcast(FP8X4),
-            scales=w_scales[:],
-            in_=w_grp[:].rearrange("p c o t -> p (c o t)"),
-        )
 
-        def plane(s, m):
-            return s[:, m % 4, :, m // 4, :]
-
-        def scaled(eng_v, dst, src, sc, relu):
-            if eng_v:
-                if relu:
-                    nc.vector.tensor_scalar(
-                        out=dst, in0=src, scalar1=sc, scalar2=0.0, op0=ALU.mult, op1=ALU.max
+        with tc.tile_pool(name="prep", bufs=1) as prep:
+            w_nat = prep.tile([P, K], BF16)
+            nc.sync.dma_start(out=w_nat[:], in_=coeff.rearrange("o d m -> o (d m)"))
+            bias_bf = prep.tile([P, O], BF16)
+            nc.sync.dma_start(out=bias_bf[:], in_=bias.partition_broadcast(P))
+            nc.vector.tensor_copy(out=bias_f[:], in_=bias_bf[:])
+            w_perm = prep.tile([P, PASSES, 4, P], BF16)
+            wv = w_nat[:].rearrange("o (c q l h t) -> o c t q h l", c=PASSES, q=16, l=4, h=2, t=4)
+            for c in range(PASSES):
+                for t in range(4):
+                    nc.vector.tensor_copy(
+                        out=w_perm[:, c, t, :].rearrange("o (q h l) -> o q h l", q=16, h=2),
+                        in_=wv[:, c, t],
                     )
-                else:
-                    nc.vector.tensor_scalar_mul(out=dst, in0=src, scalar1=sc)
-            else:
-                nc.scalar.activation(
-                    out=dst, in_=src, func=(ACT.Relu if relu else ACT.Copy), scale=sc
-                )
-
-        for big in range(B // (NBIG * P)):
-            rows = slice(big * NBIG * P, (big + 1) * NBIG * P)
-            x_nat = xin.tile([P, NBIG, D], BF16)
-            nc.sync.dma_start(out=x_nat[:], in_=x[rows, :].rearrange("(p n) d -> p n d", n=NBIG))
-            x_pos = xin.tile([P, NBIG, D], BF16)
-            nc.vector.tensor_scalar(
-                out=x_pos[:], in0=x_nat[:], scalar1=-1.0, scalar2=1.0, op0=ALU.max, op1=ALU.min
+            w_grp = prep.tile([P, PASSES, O, 4], BF16, align_bytes=64)
+            for c in range(PASSES):
+                wT = ps_s.tile([P, 4, P], BF16, tag="S")
+                for t in range(4):
+                    nc.tensor.transpose(wT[:, t, :], w_perm[:, c, t, :], ident[:])
+                nc.vector.tensor_copy(out=w_grp[:, c, :, :], in_=wT[:].rearrange("p t o -> p o t"))
+            nc.vector.quantize_mx(
+                out=w_codes[:].bitcast(FP8X4),
+                scales=w_scales[:],
+                in_=w_grp[:].rearrange("p c o t -> p (c o t)"),
             )
-            x_neg = xin.tile([P, NBIG, D], BF16)
-            nc.vector.tensor_scalar_mul(out=x_neg[:], in0=x_pos[:], scalar1=-1.0)
-            out_sb = xin.tile([P, NBIG, O], F32)
 
-            for sub in range(NBIG // NT):
-                n0 = sub * NT
-                upos = x_pos[:, n0:n0 + NT, :].rearrange("p n (g l) -> p (n g) l", l=4)
-                uneg = x_neg[:, n0:n0 + NT, :].rearrange("p n (g l) -> p (n g) l", l=4)
-                uflat = x_pos[:, n0:n0 + NT, :].rearrange("p n d -> p (n d)")
-                s_a = sets.tile([P, 4, G, 2, 4], F32, tag="A")
-                s_rp = sets.tile([P, 4, G, 2, 4], F32, tag="RP")
-                s_a4 = sets.tile([P, 4, G, 2, 4], F32, tag="A4")
-                s_rm = sets.tile([P, 4, G, 2, 4], F32, tag="RM")
+        xin = ctx.enter_context(tc.tile_pool(name="xin", bufs=2))
+        rise = ctx.enter_context(tc.tile_pool(name="rise", bufs=2))
+        sets = ctx.enter_context(tc.tile_pool(name="sets", bufs=1))
+        sqp = ctx.enter_context(tc.tile_pool(name="sqp", bufs=3))
+        grp = ctx.enter_context(tc.tile_pool(name="grp", bufs=6))
+        mxp = ctx.enter_context(tc.tile_pool(name="mxp", bufs=5))
 
-                for i in range(12):
-                    sq = work.tile([P, N], F32, tag="sq")
-                    nc.scalar.activation(
-                        out=sq[:], in_=uflat, func=ACT.Square,
-                        bias=beta[:, i:i + 1], scale=sig[:, i:i + 1],
-                    )
-                    sqv = sq[:].rearrange("p (g l) -> p g l", l=4)
-                    if i < 8:
-                        src = plane(s_a, i)
-                        nc.vector.scalar_tensor_tensor(
-                            out=src, in0=uneg, scalar=kn[:, i:i + 1], in1=sqv,
-                            op0=ALU.add, op1=ALU.mult,
-                        )
-                    else:
-                        src = plane(s_a4, i - 4)
-                        nc.vector.scalar_tensor_tensor(
-                            out=src, in0=upos, scalar=kn[:, i:i + 1], in1=sqv,
-                            op0=ALU.subtract, op1=ALU.mult,
-                        )
-                    if 1 <= i <= 8:
-                        scaled(False, plane(s_rp, i - 1), src, rp_s[:, i - 1:i], True)
-                    if 3 <= i <= 10:
-                        scaled(True, plane(s_rm, i - 3), src, rm_s[:, i - 3:i - 2], True)
-                    if 4 <= i <= 7:
-                        scaled(True, plane(s_a4, i - 4), src, a4_s[:, i - 4:i - 3], False)
+        def rows_of(r):
+            return slice(r * NT * P, (r + 1) * NT * P)
 
-                codes = mxp.tile([P, PASSES, NT * P], U32, align_bytes=64)
-                scales = mxp.tile([P, PASSES, NT * P], U8, align_bytes=64)
-                for c in range(PASSES):
-                    grouped = work.tile([P, NT, P, 4], BF16, tag="grouped", align_bytes=64)
-                    for n in range(NT):
-                        g0 = n * 64 + c * 16
-                        ps_left = ps_l.tile([P, 4, P], F32, tag="L")
-                        ps_right = ps_r.tile([P, 4, P], F32, tag="R")
-                        for bank, first, second in ((ps_left, s_a, s_rp), (ps_right, s_a4, s_rm)):
-                            for t in range(4):
-                                nc.tensor.matmul(
-                                    out=bank[:, t, :],
-                                    lhsT=first[:, t, g0:g0 + 16, :, :].rearrange("p g h l -> p (g h l)"),
-                                    rhs=identf[:], is_transpose=True, start=True, stop=False,
-                                )
-                                nc.tensor.matmul(
-                                    out=bank[:, t, :],
-                                    lhsT=second[:, t, g0:g0 + 16, :, :].rearrange("p g h l -> p (g h l)"),
-                                    rhs=identf[:], is_transpose=True, start=False, stop=True,
-                                )
-                        rfr = work.tile([P, P, 4], BF16, tag="rfr")
-                        nc.scalar.activation(
-                            out=rfr[:], in_=ps_right[:].rearrange("p t b -> p b t"),
-                            func=ACT.Relu, scale=-1.0,
-                        )
-                        nc.vector.scalar_tensor_tensor(
-                            out=grouped[:, n, :, :], in0=ps_left[:].rearrange("p t b -> p b t"),
-                            scalar=-1.0, in1=rfr[:], op0=ALU.mult, op1=ALU.max,
-                        )
-                    nc.vector.quantize_mx(
-                        out=codes[:, c, :].bitcast(FP8X4),
-                        scales=scales[:, c, :],
-                        in_=grouped[:].rearrange("p n b t -> p (n b t)"),
-                    )
+        def prepare(r):
+            x_nat = xin.tile([P, NT, D], BF16, name="x_nat")
+            nc.sync.dma_start(out=x_nat[:], in_=x[rows_of(r), :].rearrange("(p n) d -> p n d", n=NT))
+            x_cl = xin.tile([P, NT, D], BF16, name="x_cl")
+            nc.vector.tensor_scalar(
+                out=x_cl[:], in0=x_nat[:], scalar1=-1.0, scalar2=1.0, op0=ALU.max, op1=ALU.min
+            )
+            return x_cl
 
-                acc = ps_o.tile([P, NT, O], F32)
-                for n in range(NT):
-                    for c in range(PASSES):
-                        nc.tensor.matmul_mx(
-                            out=acc[:, n, :],
-                            lhsT=codes[:, c, n * P:(n + 1) * P].bitcast(FP8X4),
-                            lhsT_scale=scales[:, c, n * P:(n + 1) * P],
-                            rhs=w_codes[:, c * O:(c + 1) * O].bitcast(FP8X4),
-                            rhs_scale=w_scales[:, c * O:(c + 1) * O],
-                            start=(c == 0),
-                            stop=(c == PASSES - 1),
-                        )
-                nc.vector.tensor_tensor(
-                    out=out_sb[:, n0:n0 + NT, :], in0=acc[:],
-                    in1=bias_f[:].unsqueeze(1).to_broadcast([P, NT, O]), op=ALU.add,
+        ready = prepare(0)
+        for r in range(ROUNDS):
+            x_cl = ready
+            if r + 1 < ROUNDS:
+                ready = prepare(r + 1)
+            xf = x_cl[:].rearrange("p n d -> p (n d)")
+            uv = x_cl[:].rearrange("p n (g l) -> p (n g) l", l=4)
+
+            s_a = [rise.tile([P, G, 2, 4], F32, name="A%d" % t) for t in range(4)]
+            s_rp = [sets.tile([P, G, 2, 4], F32, name="RP%d" % t) for t in range(4)]
+            s_a4 = [sets.tile([P, G, 2, 4], F32, name="F%d" % t) for t in range(4)]
+            s_rm = [sets.tile([P, G, 2, 4], F32, name="RM%d" % t) for t in range(4)]
+
+            def plane(s, m):
+                return s[m % 4][:, :, m // 4, :]
+
+            def cube(i):
+                sq = sqp.tile([P, N], F32, name="sq")
+                nc.scalar.activation(
+                    out=sq[:], in_=xf, func=ACT.Square, bias=beta[:, i:i + 1], scale=sig[:, i:i + 1]
                 )
-            nc.sync.dma_start(out=out[rows, :].rearrange("(p n) o -> p n o", n=NBIG), in_=out_sb[:])
+                dst = plane(s_a, i) if i < 8 else plane(s_a4, i - 4)
+                nc.vector.scalar_tensor_tensor(
+                    out=dst, in0=uv, scalar=kn[:, i:i + 1],
+                    in1=sq[:].rearrange("p (g l) -> p g l", l=4), op0=ALU.subtract, op1=ALU.mult,
+                )
+                return dst
+
+            cubes = []
+            for i in range(9):
+                cubes.append(cube(i))
+                if i >= 1:
+                    nc.vector.tensor_scalar(
+                        out=plane(s_rp, i - 1), in0=cubes[i], scalar1=rp_s[:, i - 1:i], scalar2=0.0,
+                        op0=ALU.mult, op1=ALU.min,
+                    )
+            for i in range(9, 12):
+                cubes.append(cube(i))
+            for m in range(8):
+                if m in A4_ON_SCALAR:
+                    nc.scalar.activation(
+                        out=plane(s_a4, m), in_=cubes[m + 4], func=ACT.Copy, scale=a4_s[:, m:m + 1]
+                    )
+                elif m < 4:
+                    nc.vector.tensor_scalar_mul(
+                        out=plane(s_a4, m), in0=cubes[m + 4], scalar1=a4_s[:, m:m + 1]
+                    )
+                nc.scalar.activation(
+                    out=plane(s_rm, m), in_=cubes[m + 3], func=ACT.Relu, scale=rm_s[:, m:m + 1]
+                )
+
+            def side(first, second, c, n):
+                g0 = n * 64 + c * 16
+                bank = ps_s.tile([P, 4, P], F32, tag="S", name="bank")
+                for t in range(4):
+                    for s, lead in ((first, True), (second, False)):
+                        nc.tensor.matmul(
+                            out=bank[:, t, :],
+                            lhsT=s[t][:, g0:g0 + 16, :, :].rearrange("p g h l -> p (g h l)"),
+                            rhs=identf[:], is_transpose=True, start=lead, stop=not lead,
+                        )
+                return bank[:].rearrange("p t b -> p b t")
+
+            grouped = [grp.tile([P, NT, P, 4], BF16, name="grouped", align_bytes=64) for c in range(PASSES)]
+            for c in range(PASSES):
+                for n in range(NT):
+                    nc.scalar.activation(out=grouped[c][:, n], in_=side(s_a, s_rp, c, n), func=ACT.Relu)
+            acc = ps_o.tile([P, NT, O], F32, name="acc")
+            codes = []
+            for c in range(PASSES):
+                for n in range(NT):
+                    nc.vector.scalar_tensor_tensor(
+                        out=grouped[c][:, n], in0=side(s_a4, s_rm, c, n), scalar=-1.0,
+                        in1=grouped[c][:, n], op0=ALU.mult, op1=ALU.max,
+                    )
+                code = mxp.tile([P, NT * P], U32, name="code", align_bytes=64)
+                scale = mxp.tile([P, NT * P], U8, name="scale", align_bytes=64)
+                nc.vector.quantize_mx(
+                    out=code[:].bitcast(FP8X4), scales=scale[:],
+                    in_=grouped[c][:].rearrange("p n b t -> p (n b t)"),
+                )
+                codes.append((code, scale))
+            for n in range(NT):
+                cols = slice(n * P, (n + 1) * P)
+                for c in range(PASSES):
+                    code, scale = codes[c]
+                    nc.tensor.matmul_mx(
+                        out=acc[:, n, :],
+                        lhsT=code[:, cols].bitcast(FP8X4), lhsT_scale=scale[:, cols],
+                        rhs=w_codes[:, c * O:(c + 1) * O].bitcast(FP8X4),
+                        rhs_scale=w_scales[:, c * O:(c + 1) * O],
+                        start=(c == 0), stop=(c == PASSES - 1),
+                    )
+            out_sb = xin.tile([P, NT, O], F32, name="out_sb")
+            nc.vector.tensor_tensor(
+                out=out_sb[:], in0=acc[:], in1=bias_f[:].unsqueeze(1).to_broadcast([P, NT, O]), op=ALU.add
+            )
+            nc.sync.dma_start(out=out[rows_of(r), :].rearrange("(p n) o -> p n o", n=NT), in_=out_sb[:])

@@ -20,6 +20,8 @@ NT = 4
 N = NT * D
 G = N // 4
 ROUNDS = B // (NT * P)
+HT = NT // 2
+HG = HT * 64
 A4_ON_SCALAR = (0, 1)
 
 
@@ -27,7 +29,7 @@ def tile_kanlayerbspline_kernel(tc, x, coeff, bias, knots, out):
     nc = tc.nc
     with ExitStack() as ctx:
         const = ctx.enter_context(tc.tile_pool(name="const", bufs=1))
-        ps_s = ctx.enter_context(tc.psum_pool(name="ps_s", bufs=6))
+        ps_s = ctx.enter_context(tc.psum_pool(name="ps_s", bufs=3))
         ps_o = ctx.enter_context(tc.psum_pool(name="ps_o", bufs=2))
 
         ident = const.tile([P, P], BF16)
@@ -117,7 +119,7 @@ def tile_kanlayerbspline_kernel(tc, x, coeff, bias, knots, out):
                     )
             w_grp = prep.tile([P, PASSES, O, 4], BF16, align_bytes=64)
             for c in range(PASSES):
-                wT = ps_s.tile([P, 4, P], BF16, tag="S")
+                wT = ps_s.tile([P, 4, P], BF16, tag="L")
                 for t in range(4):
                     nc.tensor.transpose(wT[:, t, :], w_perm[:, c, t, :], ident[:])
                 nc.vector.tensor_copy(out=w_grp[:, c, :, :], in_=wT[:].rearrange("p t o -> p o t"))
@@ -128,11 +130,10 @@ def tile_kanlayerbspline_kernel(tc, x, coeff, bias, knots, out):
             )
 
         xin = ctx.enter_context(tc.tile_pool(name="xin", bufs=2))
-        rise = ctx.enter_context(tc.tile_pool(name="rise", bufs=2))
-        sets = ctx.enter_context(tc.tile_pool(name="sets", bufs=1))
-        sqp = ctx.enter_context(tc.tile_pool(name="sqp", bufs=3))
-        grp = ctx.enter_context(tc.tile_pool(name="grp", bufs=6))
-        mxp = ctx.enter_context(tc.tile_pool(name="mxp", bufs=5))
+        cub = ctx.enter_context(tc.tile_pool(name="cub", bufs=2))
+        sets = ctx.enter_context(tc.tile_pool(name="sets", bufs=2))
+        work = ctx.enter_context(tc.tile_pool(name="work", bufs=2))
+        mxp = ctx.enter_context(tc.tile_pool(name="mxp", bufs=2))
 
         def rows_of(r):
             return slice(r * NT * P, (r + 1) * NT * P)
@@ -140,11 +141,10 @@ def tile_kanlayerbspline_kernel(tc, x, coeff, bias, knots, out):
         def prepare(r):
             x_nat = xin.tile([P, NT, D], BF16, name="x_nat")
             nc.sync.dma_start(out=x_nat[:], in_=x[rows_of(r), :].rearrange("(p n) d -> p n d", n=NT))
-            x_cl = xin.tile([P, NT, D], BF16, name="x_cl")
             nc.vector.tensor_scalar(
-                out=x_cl[:], in0=x_nat[:], scalar1=-1.0, scalar2=1.0, op0=ALU.max, op1=ALU.min
+                out=x_nat[:], in0=x_nat[:], scalar1=-1.0, scalar2=1.0, op0=ALU.max, op1=ALU.min
             )
-            return x_cl
+            return x_nat
 
         ready = prepare(0)
         for r in range(ROUNDS):
@@ -154,16 +154,15 @@ def tile_kanlayerbspline_kernel(tc, x, coeff, bias, knots, out):
             xf = x_cl[:].rearrange("p n d -> p (n d)")
             uv = x_cl[:].rearrange("p n (g l) -> p (n g) l", l=4)
 
-            s_a = [rise.tile([P, G, 2, 4], F32, name="A%d" % t) for t in range(4)]
-            s_rp = [sets.tile([P, G, 2, 4], F32, name="RP%d" % t) for t in range(4)]
-            s_a4 = [sets.tile([P, G, 2, 4], F32, name="F%d" % t) for t in range(4)]
-            s_rm = [sets.tile([P, G, 2, 4], F32, name="RM%d" % t) for t in range(4)]
+            s_a = [cub.tile([P, G, 2, 4], F32, name="A%d" % t) for t in range(4)]
+            s_a4 = [cub.tile([P, G, 2, 4], F32, name="F%d" % t) for t in range(4)]
 
             def plane(s, m):
                 return s[m % 4][:, :, m // 4, :]
 
-            def cube(i):
-                sq = sqp.tile([P, N], F32, name="sq")
+            cubes = []
+            for i in range(12):
+                sq = work.tile([P, N], F32, name="sq")
                 nc.scalar.activation(
                     out=sq[:], in_=xf, func=ACT.Square, bias=beta[:, i:i + 1], scale=sig[:, i:i + 1]
                 )
@@ -172,75 +171,74 @@ def tile_kanlayerbspline_kernel(tc, x, coeff, bias, knots, out):
                     out=dst, in0=uv, scalar=kn[:, i:i + 1],
                     in1=sq[:].rearrange("p (g l) -> p g l", l=4), op0=ALU.subtract, op1=ALU.mult,
                 )
-                return dst
-
-            cubes = []
-            for i in range(9):
-                cubes.append(cube(i))
-                if i >= 1:
-                    nc.vector.tensor_scalar(
-                        out=plane(s_rp, i - 1), in0=cubes[i], scalar1=rp_s[:, i - 1:i], scalar2=0.0,
-                        op0=ALU.mult, op1=ALU.min,
-                    )
-            for i in range(9, 12):
-                cubes.append(cube(i))
-            for m in range(8):
+                cubes.append(dst)
+            for m in range(4):
                 if m in A4_ON_SCALAR:
                     nc.scalar.activation(
                         out=plane(s_a4, m), in_=cubes[m + 4], func=ACT.Copy, scale=a4_s[:, m:m + 1]
                     )
-                elif m < 4:
+                else:
                     nc.vector.tensor_scalar_mul(
                         out=plane(s_a4, m), in0=cubes[m + 4], scalar1=a4_s[:, m:m + 1]
                     )
-                nc.scalar.activation(
-                    out=plane(s_rm, m), in_=cubes[m + 3], func=ACT.Relu, scale=rm_s[:, m:m + 1]
-                )
 
-            def side(first, second, c, n):
-                g0 = n * 64 + c * 16
-                bank = ps_s.tile([P, 4, P], F32, tag="S", name="bank")
-                for t in range(4):
-                    for s, lead in ((first, True), (second, False)):
-                        nc.tensor.matmul(
-                            out=bank[:, t, :],
-                            lhsT=s[t][:, g0:g0 + 16, :, :].rearrange("p g h l -> p (g h l)"),
-                            rhs=identf[:], is_transpose=True, start=lead, stop=not lead,
-                        )
-                return bank[:].rearrange("p t b -> p b t")
-
-            grouped = [grp.tile([P, NT, P, 4], BF16, name="grouped", align_bytes=64) for c in range(PASSES)]
-            for c in range(PASSES):
-                for n in range(NT):
-                    nc.scalar.activation(out=grouped[c][:, n], in_=side(s_a, s_rp, c, n), func=ACT.Relu)
-            acc = ps_o.tile([P, NT, O], F32, name="acc")
-            codes = []
-            for c in range(PASSES):
-                for n in range(NT):
-                    nc.vector.scalar_tensor_tensor(
-                        out=grouped[c][:, n], in0=side(s_a4, s_rm, c, n), scalar=-1.0,
-                        in1=grouped[c][:, n], op0=ALU.mult, op1=ALU.max,
+            for half in range(2):
+                gh = slice(half * HG, (half + 1) * HG)
+                s_rp = [sets.tile([P, HG, 2, 4], F32, name="RP%d" % t) for t in range(4)]
+                s_rm = [sets.tile([P, HG, 2, 4], F32, name="RM%d" % t) for t in range(4)]
+                for m in range(8):
+                    nc.vector.tensor_scalar(
+                        out=plane(s_rp, m), in0=cubes[m + 1][:, gh], scalar1=rp_s[:, m:m + 1], scalar2=0.0,
+                        op0=ALU.mult, op1=ALU.min,
                     )
-                code = mxp.tile([P, NT * P], U32, name="code", align_bytes=64)
-                scale = mxp.tile([P, NT * P], U8, name="scale", align_bytes=64)
-                nc.vector.quantize_mx(
-                    out=code[:].bitcast(FP8X4), scales=scale[:],
-                    in_=grouped[c][:].rearrange("p n b t -> p (n b t)"),
-                )
-                codes.append((code, scale))
-            for n in range(NT):
-                cols = slice(n * P, (n + 1) * P)
+                    nc.scalar.activation(
+                        out=plane(s_rm, m), in_=cubes[m + 3][:, gh], func=ACT.Relu, scale=rm_s[:, m:m + 1]
+                    )
+
+                def side(first, second, g0, tag):
+                    bank = ps_s.tile([P, 4, P], F32, tag=tag, name="bank")
+                    for t in range(4):
+                        for s, g, lead in ((first, half * HG + g0, True), (second, g0, False)):
+                            nc.tensor.matmul(
+                                out=bank[:, t, :],
+                                lhsT=s[t][:, g:g + 16, :, :].rearrange("p g h l -> p (g h l)"),
+                                rhs=identf[:], is_transpose=True, start=lead, stop=not lead,
+                            )
+                    return bank[:].rearrange("p t b -> p b t")
+
+                codes = mxp.tile([P, PASSES, HT * P], U32, name="codes", align_bytes=64)
+                scales = mxp.tile([P, PASSES, HT * P], U8, name="scales", align_bytes=64)
                 for c in range(PASSES):
-                    code, scale = codes[c]
-                    nc.tensor.matmul_mx(
-                        out=acc[:, n, :],
-                        lhsT=code[:, cols].bitcast(FP8X4), lhsT_scale=scale[:, cols],
-                        rhs=w_codes[:, c * O:(c + 1) * O].bitcast(FP8X4),
-                        rhs_scale=w_scales[:, c * O:(c + 1) * O],
-                        start=(c == 0), stop=(c == PASSES - 1),
+                    grouped = work.tile([P, HT, P, 4], BF16, name="grouped", align_bytes=64)
+                    for n in range(HT):
+                        left = work.tile([P, P, 4], BF16, name="left", bufs=3)
+                        nc.scalar.activation(
+                            out=left[:], in_=side(s_a, s_rp, n * 64 + c * 16, "L"), func=ACT.Relu
+                        )
+                        nc.vector.scalar_tensor_tensor(
+                            out=grouped[:, n], in0=side(s_a4, s_rm, n * 64 + c * 16, "R"), scalar=-1.0,
+                            in1=left[:], op0=ALU.mult, op1=ALU.max,
+                        )
+                    nc.vector.quantize_mx(
+                        out=codes[:, c, :].bitcast(FP8X4), scales=scales[:, c, :],
+                        in_=grouped[:].rearrange("p n b t -> p (n b t)"),
                     )
-            out_sb = xin.tile([P, NT, O], F32, name="out_sb")
-            nc.vector.tensor_tensor(
-                out=out_sb[:], in0=acc[:], in1=bias_f[:].unsqueeze(1).to_broadcast([P, NT, O]), op=ALU.add
-            )
-            nc.sync.dma_start(out=out[rows_of(r), :].rearrange("(p n) o -> p n o", n=NT), in_=out_sb[:])
+                acc = ps_o.tile([P, HT, O], F32, name="acc")
+                for n in range(HT):
+                    cols = slice(n * P, (n + 1) * P)
+                    for c in range(PASSES):
+                        nc.tensor.matmul_mx(
+                            out=acc[:, n, :],
+                            lhsT=codes[:, c, cols].bitcast(FP8X4), lhsT_scale=scales[:, c, cols],
+                            rhs=w_codes[:, c * O:(c + 1) * O].bitcast(FP8X4),
+                            rhs_scale=w_scales[:, c * O:(c + 1) * O],
+                            start=(c == 0), stop=(c == PASSES - 1),
+                        )
+                out_sb = xin.tile([P, HT, O], F32, name="out_sb")
+                nc.vector.tensor_tensor(
+                    out=out_sb[:], in0=acc[:], in1=bias_f[:].unsqueeze(1).to_broadcast([P, HT, O]), op=ALU.add
+                )
+                nc.sync.dma_start(
+                    out=out[rows_of(r), :].rearrange("(p n) o -> p n o", n=NT)[:, half * HT:(half + 1) * HT, :],
+                    in_=out_sb[:],
+                )

@@ -22,7 +22,6 @@ G = N // 4
 ROUNDS = B // (NT * P)
 HT = NT // 2
 HG = HT * 64
-A4_ON_SCALAR = (0, 1)
 
 
 def tile_kanlayerbspline_kernel(tc, x, coeff, bias, knots, out):
@@ -132,113 +131,210 @@ def tile_kanlayerbspline_kernel(tc, x, coeff, bias, knots, out):
         xin = ctx.enter_context(tc.tile_pool(name="xin", bufs=2))
         cub = ctx.enter_context(tc.tile_pool(name="cub", bufs=2))
         sets = ctx.enter_context(tc.tile_pool(name="sets", bufs=2))
-        work = ctx.enter_context(tc.tile_pool(name="work", bufs=2))
+        work = ctx.enter_context(tc.tile_pool(name="work", bufs=3))
         mxp = ctx.enter_context(tc.tile_pool(name="mxp", bufs=2))
+        ctx.enter_context(tc.manual_schedule())
 
         def rows_of(r):
             return slice(r * NT * P, (r + 1) * NT * P)
 
-        def prepare(r):
-            x_nat = xin.tile([P, NT, D], BF16, name="x_nat")
-            nc.sync.dma_start(out=x_nat[:], in_=x[rows_of(r), :].rearrange("(p n) d -> p n d", n=NT))
+        def plane(s, m):
+            return s[m % 4][:, :, m // 4, :]
+
+        xs = {}
+        squares = {}
+        cubes = {}
+        relus = {}
+        lefts = {}
+        groups = {}
+        coded = {}
+        accs = {}
+
+        def load(r):
+            t = xin.tile([P, NT, D], BF16, name="x_nat")
+            nc.sync.dma_start(out=t[:], in_=x[rows_of(r), :].rearrange("(p n) d -> p n d", n=NT))
+            xs[r] = t
+
+        def clip(r):
             nc.vector.tensor_scalar(
-                out=x_nat[:], in0=x_nat[:], scalar1=-1.0, scalar2=1.0, op0=ALU.max, op1=ALU.min
+                out=xs[r][:], in0=xs[r][:], scalar1=-1.0, scalar2=1.0, op0=ALU.max, op1=ALU.min
             )
-            return x_nat
 
-        ready = prepare(0)
-        for r in range(ROUNDS):
-            x_cl = ready
-            if r + 1 < ROUNDS:
-                ready = prepare(r + 1)
-            xf = x_cl[:].rearrange("p n d -> p (n d)")
-            uv = x_cl[:].rearrange("p n (g l) -> p (n g) l", l=4)
+        def square(r, i):
+            t = work.tile([P, N], F32, name="sq")
+            nc.scalar.activation(
+                out=t[:], in_=xs[r][:].rearrange("p n d -> p (n d)"), func=ACT.Square,
+                bias=beta[:, i:i + 1], scale=sig[:, i:i + 1],
+            )
+            squares[i] = t
 
+        def open_cubes(r):
             s_a = [cub.tile([P, G, 2, 4], F32, name="A%d" % t) for t in range(4)]
-            s_a4 = [cub.tile([P, G, 2, 4], F32, name="F%d" % t) for t in range(4)]
+            s_f = [cub.tile([P, G, 2, 4], F32, name="F%d" % t) for t in range(4)]
+            cubes[r] = (s_a, s_f)
 
-            def plane(s, m):
-                return s[m % 4][:, :, m // 4, :]
+        def cube_of(r, i):
+            s_a, s_f = cubes[r]
+            return plane(s_a, i) if i < 8 else plane(s_f, i - 4)
 
-            cubes = []
-            for i in range(12):
-                sq = work.tile([P, N], F32, name="sq")
+        def cube(r, i):
+            nc.vector.scalar_tensor_tensor(
+                out=cube_of(r, i), in0=xs[r][:].rearrange("p n (g l) -> p (n g) l", l=4),
+                scalar=kn[:, i:i + 1], in1=squares[i][:].rearrange("p (g l) -> p g l", l=4),
+                op0=ALU.subtract, op1=ALU.mult,
+            )
+
+        def fall_lead(r, m, on_scalar):
+            dst = plane(cubes[r][1], m)
+            if on_scalar:
                 nc.scalar.activation(
-                    out=sq[:], in_=xf, func=ACT.Square, bias=beta[:, i:i + 1], scale=sig[:, i:i + 1]
+                    out=dst, in_=cube_of(r, m + 4), func=ACT.Copy, scale=a4_s[:, m:m + 1]
                 )
-                dst = plane(s_a, i) if i < 8 else plane(s_a4, i - 4)
-                nc.vector.scalar_tensor_tensor(
-                    out=dst, in0=uv, scalar=kn[:, i:i + 1],
-                    in1=sq[:].rearrange("p (g l) -> p g l", l=4), op0=ALU.subtract, op1=ALU.mult,
-                )
-                cubes.append(dst)
-            for m in range(4):
-                if m in A4_ON_SCALAR:
-                    nc.scalar.activation(
-                        out=plane(s_a4, m), in_=cubes[m + 4], func=ACT.Copy, scale=a4_s[:, m:m + 1]
-                    )
-                else:
-                    nc.vector.tensor_scalar_mul(
-                        out=plane(s_a4, m), in0=cubes[m + 4], scalar1=a4_s[:, m:m + 1]
-                    )
+            else:
+                nc.vector.tensor_scalar_mul(out=dst, in0=cube_of(r, m + 4), scalar1=a4_s[:, m:m + 1])
 
-            for half in range(2):
-                gh = slice(half * HG, (half + 1) * HG)
-                s_rp = [sets.tile([P, HG, 2, 4], F32, name="RP%d" % t) for t in range(4)]
-                s_rm = [sets.tile([P, HG, 2, 4], F32, name="RM%d" % t) for t in range(4)]
-                for m in range(8):
-                    nc.vector.tensor_scalar(
-                        out=plane(s_rp, m), in0=cubes[m + 1][:, gh], scalar1=rp_s[:, m:m + 1], scalar2=0.0,
-                        op0=ALU.mult, op1=ALU.min,
-                    )
-                    nc.scalar.activation(
-                        out=plane(s_rm, m), in_=cubes[m + 3][:, gh], func=ACT.Relu, scale=rm_s[:, m:m + 1]
-                    )
+        def open_relus(h):
+            s_rp = [sets.tile([P, HG, 2, 4], F32, name="RP%d" % t) for t in range(4)]
+            s_rm = [sets.tile([P, HG, 2, 4], F32, name="RM%d" % t) for t in range(4)]
+            relus[h] = (s_rp, s_rm)
 
-                def side(first, second, g0, tag):
-                    bank = ps_s.tile([P, 4, P], F32, tag=tag, name="bank")
-                    for t in range(4):
-                        for s, g, lead in ((first, half * HG + g0, True), (second, g0, False)):
-                            nc.tensor.matmul(
-                                out=bank[:, t, :],
-                                lhsT=s[t][:, g:g + 16, :, :].rearrange("p g h l -> p (g h l)"),
-                                rhs=identf[:], is_transpose=True, start=lead, stop=not lead,
-                            )
-                    return bank[:].rearrange("p t b -> p b t")
+        def half_of(h):
+            return h // 2, slice((h % 2) * HG, (h % 2 + 1) * HG)
 
+        def relu_rise(h, m):
+            r, gh = half_of(h)
+            nc.vector.tensor_scalar(
+                out=plane(relus[h][0], m), in0=cube_of(r, m + 1)[:, gh], scalar1=rp_s[:, m:m + 1],
+                scalar2=0.0, op0=ALU.mult, op1=ALU.min,
+            )
+
+        def relu_fall(h, m):
+            r, gh = half_of(h)
+            nc.scalar.activation(
+                out=plane(relus[h][1], m), in_=cube_of(r, m + 3)[:, gh], func=ACT.Relu,
+                scale=rm_s[:, m:m + 1],
+            )
+
+        banks = {}
+
+        def sums(h, j):
+            r = h // 2
+            c, n = j // HT, j % HT
+            g0 = n * 64 + c * 16
+            pair = []
+            for side in range(2):
+                bank = ps_s.tile([P, 4, P], F32, tag="LR"[side], name="bank")
+                for t in range(4):
+                    for s, g, lead in (
+                        (cubes[r][side], (h % 2) * HG + g0, True), (relus[h][side], g0, False)
+                    ):
+                        nc.tensor.matmul(
+                            out=bank[:, t, :],
+                            lhsT=s[t][:, g:g + 16, :, :].rearrange("p g h l -> p (g h l)"),
+                            rhs=identf[:], is_transpose=True, start=lead, stop=not lead,
+                        )
+                pair.append(bank[:].rearrange("p t b -> p b t"))
+            banks[(h, j)] = pair
+
+        def read_left(h, j):
+            t = work.tile([P, P, 4], BF16, name="left")
+            nc.scalar.activation(out=t[:], in_=banks[(h, j)][0], func=ACT.Relu)
+            lefts[(h, j)] = t
+
+        def read_right(h, j):
+            c, n = j // HT, j % HT
+            if n == 0:
+                groups[(h, c)] = work.tile([P, HT, P, 4], BF16, name="grouped", align_bytes=64)
+            nc.vector.scalar_tensor_tensor(
+                out=groups[(h, c)][:, n], in0=banks[(h, j)][1], scalar=-1.0, in1=lefts[(h, j)][:],
+                op0=ALU.mult, op1=ALU.max,
+            )
+
+        def quantise(h, c):
+            if c == 0:
                 codes = mxp.tile([P, PASSES, HT * P], U32, name="codes", align_bytes=64)
                 scales = mxp.tile([P, PASSES, HT * P], U8, name="scales", align_bytes=64)
+                coded[h] = (codes, scales)
+            codes, scales = coded[h]
+            nc.vector.quantize_mx(
+                out=codes[:, c, :].bitcast(FP8X4), scales=scales[:, c, :],
+                in_=groups[(h, c)][:].rearrange("p n b t -> p (n b t)"),
+            )
+
+        def multiply(h):
+            codes, scales = coded[h]
+            acc = ps_o.tile([P, HT, O], F32, name="acc")
+            for n in range(HT):
+                cols = slice(n * P, (n + 1) * P)
                 for c in range(PASSES):
-                    grouped = work.tile([P, HT, P, 4], BF16, name="grouped", align_bytes=64)
-                    for n in range(HT):
-                        left = work.tile([P, P, 4], BF16, name="left", bufs=3)
-                        nc.scalar.activation(
-                            out=left[:], in_=side(s_a, s_rp, n * 64 + c * 16, "L"), func=ACT.Relu
-                        )
-                        nc.vector.scalar_tensor_tensor(
-                            out=grouped[:, n], in0=side(s_a4, s_rm, n * 64 + c * 16, "R"), scalar=-1.0,
-                            in1=left[:], op0=ALU.mult, op1=ALU.max,
-                        )
-                    nc.vector.quantize_mx(
-                        out=codes[:, c, :].bitcast(FP8X4), scales=scales[:, c, :],
-                        in_=grouped[:].rearrange("p n b t -> p (n b t)"),
+                    nc.tensor.matmul_mx(
+                        out=acc[:, n, :],
+                        lhsT=codes[:, c, cols].bitcast(FP8X4), lhsT_scale=scales[:, c, cols],
+                        rhs=w_codes[:, c * O:(c + 1) * O].bitcast(FP8X4),
+                        rhs_scale=w_scales[:, c * O:(c + 1) * O],
+                        start=(c == 0), stop=(c == PASSES - 1),
                     )
-                acc = ps_o.tile([P, HT, O], F32, name="acc")
-                for n in range(HT):
-                    cols = slice(n * P, (n + 1) * P)
-                    for c in range(PASSES):
-                        nc.tensor.matmul_mx(
-                            out=acc[:, n, :],
-                            lhsT=codes[:, c, cols].bitcast(FP8X4), lhsT_scale=scales[:, c, cols],
-                            rhs=w_codes[:, c * O:(c + 1) * O].bitcast(FP8X4),
-                            rhs_scale=w_scales[:, c * O:(c + 1) * O],
-                            start=(c == 0), stop=(c == PASSES - 1),
-                        )
-                out_sb = xin.tile([P, HT, O], F32, name="out_sb")
-                nc.vector.tensor_tensor(
-                    out=out_sb[:], in0=acc[:], in1=bias_f[:].unsqueeze(1).to_broadcast([P, HT, O]), op=ALU.add
-                )
-                nc.sync.dma_start(
-                    out=out[rows_of(r), :].rearrange("(p n) o -> p n o", n=NT)[:, half * HT:(half + 1) * HT, :],
-                    in_=out_sb[:],
-                )
+            accs[h] = acc
+
+        def finish(h):
+            out_sb = xin.tile([P, HT, O], F32, name="out_sb")
+            nc.vector.tensor_tensor(
+                out=out_sb[:], in0=accs[h][:], in1=bias_f[:].unsqueeze(1).to_broadcast([P, HT, O]),
+                op=ALU.add,
+            )
+            n0 = (h % 2) * HT
+            nc.sync.dma_start(
+                out=out[rows_of(h // 2), :].rearrange("(p n) o -> p n o", n=NT)[:, n0:n0 + HT, :],
+                in_=out_sb[:],
+            )
+
+        CH = PASSES * HT
+        halves = 2 * ROUNDS
+        load(0)
+        clip(0)
+        for k in range(-1, ROUNDS + 1):
+            nxt = k + 1
+            more = nxt < ROUNDS
+            if nxt + 1 < ROUNDS:
+                load(nxt + 1)
+            for s in range(2 * CH):
+                h, j = 2 * k + s // CH, s % CH
+                here = 0 <= h < halves
+                hp, jp = (h, j - 1) if j > 0 else (h - 1, CH - 1)
+                hq, jq = (h, j - 3) if j > 2 else (h - 1, j + CH - 3)
+                if here:
+                    sums(h, j)
+                if 0 <= hp < halves:
+                    read_left(hp, jp)
+                if j == 0 and 0 <= h + 1 < halves:
+                    open_relus(h + 1)
+                if 0 <= h + 1 < halves:
+                    relu_fall(h + 1, j)
+                if more:
+                    if s == 1:
+                        open_cubes(nxt)
+                    if 1 <= s <= 6 or 8 <= s <= 13:
+                        square(nxt, s - 1 if s <= 6 else s - 2)
+                    if s == 7:
+                        fall_lead(nxt, 0, True)
+                    if s == 14:
+                        fall_lead(nxt, 2, True)
+                    if 2 <= s <= 7 or 9 <= s <= 14:
+                        cube(nxt, s - 2 if s <= 7 else s - 3)
+                if 0 <= h + 1 < halves:
+                    relu_rise(h + 1, j)
+                if 0 <= hq < halves and jq % HT == HT - 1:
+                    quantise(hq, jq // HT)
+                if more:
+                    if s == 8:
+                        fall_lead(nxt, 1, False)
+                    if s == 15:
+                        fall_lead(nxt, 3, False)
+                if 0 <= hp < halves:
+                    read_right(hp, jp)
+                if j == 3 and 0 <= h - 1 < halves:
+                    multiply(h - 1)
+                if j == 5 and 0 <= h - 1 < halves:
+                    finish(h - 1)
+                if s == 15 and nxt + 1 < ROUNDS:
+                    clip(nxt + 1)

@@ -10,6 +10,7 @@ U8 = mybir.dt.uint8
 FP8X4 = mybir.dt.float8_e4m3fn_x4
 ALU = mybir.AluOpType
 ACT = mybir.ActivationFunctionType
+AX = mybir.AxisListType
 
 B, D, O, NC = 16384, 256, 128, 8
 K = D * NC
@@ -17,28 +18,62 @@ FLOPS = 2 * B * K * O
 P = 128
 PASSES = 4
 NT = 4
+HT = NT // 2
 N = NT * D
 G = N // 4
+HG = G // 2
+KN = 12
 ROUNDS = B // (NT * P)
-HT = NT // 2
-HG = HT * 64
 
 
 def tile_kanlayerbspline_kernel(tc, x, coeff, bias, knots, out):
     nc = tc.nc
     with ExitStack() as ctx:
         const = ctx.enter_context(tc.tile_pool(name="const", bufs=1))
+        xin = ctx.enter_context(tc.tile_pool(name="xin", bufs=2))
+        cub = ctx.enter_context(tc.tile_pool(name="cub", bufs=2))
+        sets = ctx.enter_context(tc.tile_pool(name="sets", bufs=2))
+        work = ctx.enter_context(tc.tile_pool(name="work", bufs=3))
+        mxp = ctx.enter_context(tc.tile_pool(name="mxp", bufs=2))
         ps_s = ctx.enter_context(tc.psum_pool(name="ps_s", bufs=3))
         ps_o = ctx.enter_context(tc.psum_pool(name="ps_o", bufs=2))
+        ctx.enter_context(tc.manual_schedule())
 
+        def rows_of(r):
+            return slice(r * NT * P, (r + 1) * NT * P)
+
+        xs = {}
+        us = {}
+
+        def load(r):
+            t = xin.tile([P, NT, D], BF16, name="x_nat")
+            nc.sync.dma_start(out=t[:], in_=x[rows_of(r), :].rearrange("(p n) d -> p n d", n=NT))
+            xs[r] = t
+
+        def clip(r):
+            t = xin.tile([P, NT, D], BF16, name="u")
+            dst = t[:].rearrange("p n (e t v z) -> p (n e) t v z", e=2, t=4, v=2)
+            src = xs[r][:].rearrange("p n (e v t z) -> p (n e) v t z", e=2, v=2, t=4)
+            for v in range(2):
+                nc.vector.tensor_scalar(
+                    out=dst[:, :, :, v, :], in0=src[:, :, v], scalar1=-1.0, scalar2=1.0,
+                    op0=ALU.max, op1=ALU.min,
+                )
+            us[r] = t
+
+        kn_bf = const.tile([P, KN], BF16)
+        nc.sync.dma_start(out=kn_bf[:], in_=knots.partition_broadcast(P))
+        load(0)
+        w_nat = const.tile([P, K], BF16)
+        nc.sync.dma_start(out=w_nat[:], in_=coeff.rearrange("o d m -> o (d m)"))
+        bias_bf = const.tile([P, O], BF16)
+        nc.sync.dma_start(out=bias_bf[:], in_=bias.partition_broadcast(P))
         ident = const.tile([P, P], BF16)
         make_identity(nc, ident[:])
         identf = const.tile([P, P], F32)
         make_identity(nc, identf[:])
 
-        kn_bf = const.tile([P, 12], BF16)
-        nc.sync.dma_start(out=kn_bf[:], in_=knots.partition_broadcast(P))
-        kn = const.tile([P, 12], F32)
+        kn = const.tile([P, KN], F32)
         nc.vector.tensor_copy(out=kn[:], in_=kn_bf[:])
 
         def diff(a, b, nm):
@@ -46,77 +81,86 @@ def tile_kanlayerbspline_kernel(tc, x, coeff, bias, knots, out):
             nc.vector.tensor_sub(out=d[:], in0=kn[:, a:a + 8], in1=kn[:, b:b + 8])
             return d
 
-        d10 = diff(1, 0, "d10")
-        d20 = diff(2, 0, "d20")
-        d30 = diff(3, 0, "d30")
-        d40 = diff(4, 0, "d40")
-        d21 = diff(2, 1, "d21")
-        d31 = diff(3, 1, "d31")
-        d41 = diff(4, 1, "d41")
-        d32 = diff(3, 2, "d32")
-        d42 = diff(4, 2, "d42")
-        d43 = diff(4, 3, "d43")
+        def mul(a, b, nm):
+            d = const.tile([P, 8], F32, name=nm)
+            nc.vector.tensor_mul(out=d[:], in0=a[:], in1=b[:])
+            return d
 
-        def weight(factors, top, nm):
-            prod = const.tile([P, 8], F32, name=nm + "_p")
-            nc.vector.tensor_mul(out=prod[:], in0=factors[0][:], in1=factors[1][:])
-            for f in factors[2:]:
-                nc.vector.tensor_mul(out=prod[:], in0=prod[:], in1=f[:])
-            w = const.tile([P, 8], F32, name=nm)
-            nc.vector.reciprocal(out=w[:], in_=prod[:])
-            if top is not None:
-                nc.vector.tensor_mul(out=w[:], in0=w[:], in1=top[:])
-            return w
+        def inverse(a, nm):
+            d = const.tile([P, 8], F32, name=nm)
+            nc.vector.reciprocal(out=d[:], in_=a[:])
+            return d
 
-        w0 = weight([d10, d20, d30], None, "w0")
-        w4 = weight([d41, d42, d43], None, "w4")
-        w1 = weight([d10, d21, d31, d41], d40, "w1")
-        w3 = weight([d30, d31, d32, d43], d40, "w3")
-
-        wsig = const.tile([P, 12], F32)
-        nc.vector.tensor_copy(out=wsig[:, 0:8], in_=w0[:])
-        nc.vector.tensor_copy(out=wsig[:, 8:12], in_=w4[:, 4:8])
-        sig0 = const.tile([P, 12], F32)
-        nc.scalar.activation(out=sig0[:], in_=wsig[:], func=ACT.Sqrt)
-        sig = const.tile([P, 12], F32)
+        d20, d30, d40 = diff(2, 0, "d20"), diff(3, 0, "d30"), diff(4, 0, "d40")
+        d21, d31, d41 = diff(2, 1, "d21"), diff(3, 1, "d31"), diff(4, 1, "d41")
+        p20 = mul(d20, d30, "p20")
+        p21 = mul(mul(d21, d31, "p21a"), d41, "p21")
+        rise = mul(mul(d40, p20, "rise_a"), inverse(p21, "rise_b"), "rise")
+        ones = const.tile([P, 8], F32)
+        nc.vector.memset(ones[:], 1.0)
+        kap = const.tile([P, KN], F32)
+        nc.vector.memset(kap[:], 1.0)
+        nc.vector.tensor_tensor_scan(
+            out=kap[:, 1:9], data0=rise[:], data1=ones[:], initial=1.0, op0=ALU.mult, op1=ALU.mult
+        )
+        sig0 = const.tile([P, KN], F32)
+        nc.scalar.activation(out=sig0[:], in_=kap[:], func=ACT.Sqrt)
+        sig = const.tile([P, KN], F32)
         nc.vector.reciprocal(out=sig[:], in_=sig0[:])
-        nc.vector.tensor_mul(out=sig[:], in0=sig[:], in1=wsig[:])
+        nc.vector.tensor_mul(out=sig[:], in0=sig[:], in1=kap[:])
         nc.vector.tensor_add(out=sig[:], in0=sig[:], in1=sig0[:])
         nc.vector.tensor_scalar_mul(out=sig[:], in0=sig[:], scalar1=0.5)
-        beta = const.tile([P, 12], F32)
+        beta = const.tile([P, KN], F32)
         nc.vector.tensor_mul(out=beta[:], in0=sig[:], in1=kn[:])
         nc.vector.tensor_scalar_mul(out=beta[:], in0=beta[:], scalar1=-1.0)
-        rweff = const.tile([P, 12], F32)
-        nc.vector.tensor_mul(out=rweff[:], in0=sig[:], in1=sig[:])
-        nc.vector.reciprocal(out=rweff[:], in_=rweff[:])
-        rp_s = const.tile([P, 8], F32)
-        nc.vector.tensor_mul(out=rp_s[:], in0=w1[:], in1=rweff[:, 1:9])
-        nc.vector.tensor_scalar_mul(out=rp_s[:], in0=rp_s[:], scalar1=-1.0)
-        rm_s = const.tile([P, 8], F32)
-        nc.vector.tensor_mul(out=rm_s[:], in0=w3[:], in1=rweff[:, 3:11])
-        nc.vector.tensor_scalar_mul(out=rm_s[:], in0=rm_s[:], scalar1=-1.0)
-        a4_s = const.tile([P, 4], F32)
-        nc.vector.tensor_mul(out=a4_s[:], in0=w4[:, 0:4], in1=rweff[:, 4:8])
+        clip(0)
 
-        bias_f = const.tile([P, O], F32)
+        side_scale = const.tile([P, 2, 2], F32)
+        fall = const.tile([P, 8], F32)
         w_codes = const.tile([P, PASSES * O], U32, align_bytes=64)
         w_scales = const.tile([P, PASSES * O], U8, align_bytes=64)
+        bias_f = const.tile([P, O], F32)
 
-        with tc.tile_pool(name="prep", bufs=1) as prep:
-            w_nat = prep.tile([P, K], BF16)
-            nc.sync.dma_start(out=w_nat[:], in_=coeff.rearrange("o d m -> o (d m)"))
-            bias_bf = prep.tile([P, O], BF16)
-            nc.sync.dma_start(out=bias_bf[:], in_=bias.partition_broadcast(P))
+        def scales_of_the_sides():
+            d10, d32 = diff(1, 0, "d10"), diff(3, 2, "d32")
+            d42, d43 = diff(4, 2, "d42"), diff(4, 3, "d43")
+            p41 = mul(d41, d42, "p41")
+            ikap = const.tile([P, KN], F32, name="ikap")
+            nc.vector.reciprocal(out=ikap[:], in_=kap[:])
+            q = mul(mul(d30, d31, "q_a"), d32, "q_b")
+            t = mul(mul(d40, p41, "fall_a"), inverse(q, "fall_b"), "fall_c")
+            nc.vector.tensor_mul(out=t[:], in0=t[:], in1=kap[:, 4:12])
+            nc.vector.tensor_mul(out=t[:], in0=t[:], in1=ikap[:, 3:11])
+            nc.vector.tensor_scalar_mul(out=fall[:], in0=t[:], scalar1=-1.0)
+            w0 = inverse(mul(d10, p20, "p10"), "w0")
+            w4 = inverse(mul(p41, d43, "p43"), "w4")
+            nc.vector.tensor_mul(out=w0[:], in0=w0[:], in1=ikap[:, 0:8])
+            nc.vector.tensor_mul(out=w4[:], in0=w4[:], in1=ikap[:, 4:12])
+            nc.vector.tensor_scalar_mul(out=w4[:], in0=w4[:], scalar1=-1.0)
+            pick = const.tile([P, 4], F32, name="pick")
+            nc.vector.tensor_reduce(
+                out=pick[:], in_=identf[:].rearrange("p (x j l) -> p j x l", x=8, j=4, l=4),
+                op=ALU.add, axis=AX.XY,
+            )
+            for side, w in ((0, w0), (1, w4)):
+                wv = w[:].rearrange("p (h j) -> p h j", j=4)
+                nc.vector.tensor_mul(out=wv, in0=wv, in1=pick[:].unsqueeze(1).to_broadcast([P, 2, 4]))
+                nc.vector.tensor_reduce(out=side_scale[:, side, :], in_=wv, op=ALU.add, axis=AX.X)
+
+        def weights():
             nc.vector.tensor_copy(out=bias_f[:], in_=bias_bf[:])
-            w_perm = prep.tile([P, PASSES, 4, P], BF16)
-            wv = w_nat[:].rearrange("o (c q l h t) -> o c t q h l", c=PASSES, q=16, l=4, h=2, t=4)
+            w_perm = const.tile([P, PASSES, 4, P], BF16, name="w_perm")
+            wv = w_nat[:].rearrange("o (e v t q l h j) -> o e h t v q j l", e=2, v=2, t=4, q=4, l=4, h=2, j=4)
             for c in range(PASSES):
                 for t in range(4):
-                    nc.vector.tensor_copy(
-                        out=w_perm[:, c, t, :].rearrange("o (q h l) -> o q h l", q=16, h=2),
-                        in_=wv[:, c, t],
-                    )
-            w_grp = prep.tile([P, PASSES, O, 4], BF16, align_bytes=64)
+                    for v in range(2):
+                        nc.scalar.copy(
+                            out=w_perm[:, c, t, 64 * v:64 * v + 64].rearrange(
+                                "o (q j l) -> o q j l", q=4, j=4
+                            ),
+                            in_=wv[:, c // 2, c % 2, t, v],
+                        )
+            w_grp = const.tile([P, PASSES, O, 4], BF16, name="w_grp", align_bytes=64)
             for c in range(PASSES):
                 wT = ps_s.tile([P, 4, P], BF16, tag="L")
                 for t in range(4):
@@ -128,117 +172,87 @@ def tile_kanlayerbspline_kernel(tc, x, coeff, bias, knots, out):
                 in_=w_grp[:].rearrange("p c o t -> p (c o t)"),
             )
 
-        xin = ctx.enter_context(tc.tile_pool(name="xin", bufs=2))
-        cub = ctx.enter_context(tc.tile_pool(name="cub", bufs=2))
-        sets = ctx.enter_context(tc.tile_pool(name="sets", bufs=2))
-        work = ctx.enter_context(tc.tile_pool(name="work", bufs=3))
-        mxp = ctx.enter_context(tc.tile_pool(name="mxp", bufs=2))
-        ctx.enter_context(tc.manual_schedule())
-
-        def rows_of(r):
-            return slice(r * NT * P, (r + 1) * NT * P)
-
-        def plane(s, m):
-            return s[m % 4][:, :, m // 4, :]
-
-        xs = {}
         squares = {}
         cubes = {}
         relus = {}
+        banks = {}
         lefts = {}
         groups = {}
         coded = {}
         accs = {}
 
-        def load(r):
-            t = xin.tile([P, NT, D], BF16, name="x_nat")
-            nc.sync.dma_start(out=t[:], in_=x[rows_of(r), :].rearrange("(p n) d -> p n d", n=NT))
-            xs[r] = t
-
-        def clip(r):
-            nc.vector.tensor_scalar(
-                out=xs[r][:], in0=xs[r][:], scalar1=-1.0, scalar2=1.0, op0=ALU.max, op1=ALU.min
-            )
-
         def square(r, i):
             t = work.tile([P, N], F32, name="sq")
             nc.scalar.activation(
-                out=t[:], in_=xs[r][:].rearrange("p n d -> p (n d)"), func=ACT.Square,
+                out=t[:], in_=us[r][:].rearrange("p n d -> p (n d)"), func=ACT.Square,
                 bias=beta[:, i:i + 1], scale=sig[:, i:i + 1],
             )
             squares[i] = t
 
-        def open_cubes(r):
-            s_a = [cub.tile([P, G, 2, 4], F32, name="A%d" % t) for t in range(4)]
-            s_f = [cub.tile([P, G, 2, 4], F32, name="F%d" % t) for t in range(4)]
-            cubes[r] = (s_a, s_f)
+        def knot_plane(t, i):
+            return t[:, i // 4].rearrange("p g (j l) -> p g j l", l=4)[:, :, i % 4, :]
 
-        def cube_of(r, i):
-            s_a, s_f = cubes[r]
-            return plane(s_a, i) if i < 8 else plane(s_f, i - 4)
+        def half(h):
+            return slice((h % 2) * HG, (h % 2 + 1) * HG)
 
         def cube(r, i):
+            if i == 0:
+                cubes[r] = cub.tile([P, 3, G, 16], F32, name="cubes_t")
             nc.vector.scalar_tensor_tensor(
-                out=cube_of(r, i), in0=xs[r][:].rearrange("p n (g l) -> p (n g) l", l=4),
-                scalar=kn[:, i:i + 1], in1=squares[i][:].rearrange("p (g l) -> p g l", l=4),
+                out=knot_plane(cubes[r], i),
+                in0=us[r][:].rearrange("p n (g l) -> p (n g) l", l=4),
+                scalar=kn[:, i:i + 1],
+                in1=squares[i][:].rearrange("p (g l) -> p g l", l=4),
                 op0=ALU.subtract, op1=ALU.mult,
             )
 
-        def fall_lead(r, m, on_scalar):
-            dst = plane(cubes[r][1], m)
-            if on_scalar:
-                nc.scalar.activation(
-                    out=dst, in_=cube_of(r, m + 4), func=ACT.Copy, scale=a4_s[:, m:m + 1]
-                )
-            else:
-                nc.vector.tensor_scalar_mul(out=dst, in0=cube_of(r, m + 4), scalar1=a4_s[:, m:m + 1])
-
         def open_relus(h):
-            s_rp = [sets.tile([P, HG, 2, 4], F32, name="RP%d" % t) for t in range(4)]
-            s_rm = [sets.tile([P, HG, 2, 4], F32, name="RM%d" % t) for t in range(4)]
-            relus[h] = (s_rp, s_rm)
-
-        def half_of(h):
-            return h // 2, slice((h % 2) * HG, (h % 2 + 1) * HG)
-
-        def relu_rise(h, m):
-            r, gh = half_of(h)
-            nc.vector.tensor_scalar(
-                out=plane(relus[h][0], m), in0=cube_of(r, m + 1)[:, gh], scalar1=rp_s[:, m:m + 1],
-                scalar2=0.0, op0=ALU.mult, op1=ALU.min,
+            relus[h] = (
+                sets.tile([P, 2, HG, 16], F32, name="rp"), sets.tile([P, 2, HG, 16], F32, name="rm")
             )
+
+        def relu_rise(h, mh):
+            dst = relus[h][0][:, mh]
+            same, after = cubes[h // 2][:, mh, half(h)], cubes[h // 2][:, mh + 1, half(h)]
+            for o, i in ((dst[:, :, 0:12], same[:, :, 4:16]), (dst[:, :, 12:16], after[:, :, 0:4])):
+                nc.vector.tensor_scalar(
+                    out=o, in0=i, scalar1=-1.0, scalar2=0.0, op0=ALU.mult, op1=ALU.min
+                )
 
         def relu_fall(h, m):
-            r, gh = half_of(h)
             nc.scalar.activation(
-                out=plane(relus[h][1], m), in_=cube_of(r, m + 3)[:, gh], func=ACT.Relu,
-                scale=rm_s[:, m:m + 1],
+                out=knot_plane(relus[h][1], m), in_=knot_plane(cubes[h // 2], m + 3)[:, half(h)],
+                func=ACT.Relu, scale=fall[:, m:m + 1],
             )
 
-        banks = {}
-
         def sums(h, j):
-            r = h // 2
             c, n = j // HT, j % HT
-            g0 = n * 64 + c * 16
+            e, mh = c // 2, c % 2
             pair = []
             for side in range(2):
                 bank = ps_s.tile([P, 4, P], F32, tag="LR"[side], name="bank")
                 for t in range(4):
-                    for s, g, lead in (
-                        (cubes[r][side], (h % 2) * HG + g0, True), (relus[h][side], g0, False)
-                    ):
-                        nc.tensor.matmul(
-                            out=bank[:, t, :],
-                            lhsT=s[t][:, g:g + 16, :, :].rearrange("p g h l -> p (g h l)"),
-                            rhs=identf[:], is_transpose=True, start=lead, stop=not lead,
-                        )
+                    g = n * 64 + e * 32 + t * 8
+                    gc = (h % 2) * HG + g
+                    nc.tensor.matmul(
+                        out=bank[:, t, :],
+                        lhsT=cubes[h // 2][:, mh + side, gc:gc + 8, :].rearrange("p g z -> p (g z)"),
+                        rhs=identf[:], is_transpose=True, start=True, stop=False,
+                    )
+                    nc.tensor.matmul(
+                        out=bank[:, t, :],
+                        lhsT=relus[h][side][:, mh, g:g + 8, :].rearrange("p g z -> p (g z)"),
+                        rhs=identf[:], is_transpose=True, start=False, stop=True,
+                    )
                 pair.append(bank[:].rearrange("p t b -> p b t"))
             banks[(h, j)] = pair
 
         def read_left(h, j):
+            mh = j // HT % 2
             t = work.tile([P, P, 4], BF16, name="left")
-            nc.scalar.activation(out=t[:], in_=banks[(h, j)][0], func=ACT.Relu)
+            nc.scalar.activation(
+                out=t[:], in_=banks[(h, j)][0], func=ACT.Relu, scale=side_scale[:, 0, mh:mh + 1]
+            )
             lefts[(h, j)] = t
 
         def read_right(h, j):
@@ -246,8 +260,8 @@ def tile_kanlayerbspline_kernel(tc, x, coeff, bias, knots, out):
             if n == 0:
                 groups[(h, c)] = work.tile([P, HT, P, 4], BF16, name="grouped", align_bytes=64)
             nc.vector.scalar_tensor_tensor(
-                out=groups[(h, c)][:, n], in0=banks[(h, j)][1], scalar=-1.0, in1=lefts[(h, j)][:],
-                op0=ALU.mult, op1=ALU.max,
+                out=groups[(h, c)][:, n], in0=banks[(h, j)][1], scalar=side_scale[:, 1, c % 2:c % 2 + 1],
+                in1=lefts[(h, j)][:], op0=ALU.mult, op1=ALU.max,
             )
 
         def quantise(h, c):
@@ -290,8 +304,9 @@ def tile_kanlayerbspline_kernel(tc, x, coeff, bias, knots, out):
 
         CH = PASSES * HT
         halves = 2 * ROUNDS
-        load(0)
-        clip(0)
+        fall_plan = {0: (0,), 1: (1,), 2: (2,), 3: (3,), 4: (4,), 5: (5,), 6: (6, 7),
+                     9: (0,), 11: (1,), 13: (2, 3), 14: (4, 5), 15: (6, 7)}
+        rise_plan = {0: 0, 7: 1, 14: 0, 15: 1}
         for k in range(-1, ROUNDS + 1):
             nxt = k + 1
             more = nxt < ROUNDS
@@ -299,37 +314,27 @@ def tile_kanlayerbspline_kernel(tc, x, coeff, bias, knots, out):
                 load(nxt + 1)
             for s in range(2 * CH):
                 h, j = 2 * k + s // CH, s % CH
-                here = 0 <= h < halves
                 hp, jp = (h, j - 1) if j > 0 else (h - 1, CH - 1)
                 hq, jq = (h, j - 3) if j > 2 else (h - 1, j + CH - 3)
-                if here:
+                if 0 <= h < halves:
                     sums(h, j)
                 if 0 <= hp < halves:
                     read_left(hp, jp)
-                if j == 0 and 0 <= h + 1 < halves:
-                    open_relus(h + 1)
-                if 0 <= h + 1 < halves:
-                    relu_fall(h + 1, j)
+                ahead = 0 <= h + 1 < halves
+                if ahead:
+                    if j == 0:
+                        open_relus(h + 1)
+                    for m in fall_plan.get(s, ()):
+                        relu_fall(h + 1, m)
                 if more:
-                    if s == 1:
-                        open_cubes(nxt)
+                    if s <= 5 or 7 <= s <= 12:
+                        square(nxt, s if s <= 5 else s - 1)
                     if 1 <= s <= 6 or 8 <= s <= 13:
-                        square(nxt, s - 1 if s <= 6 else s - 2)
-                    if s == 7:
-                        fall_lead(nxt, 0, True)
-                    if s == 14:
-                        fall_lead(nxt, 2, True)
-                    if 2 <= s <= 7 or 9 <= s <= 14:
-                        cube(nxt, s - 2 if s <= 7 else s - 3)
-                if 0 <= h + 1 < halves:
-                    relu_rise(h + 1, j)
+                        cube(nxt, s - 1 if s <= 6 else s - 2)
                 if 0 <= hq < halves and jq % HT == HT - 1:
                     quantise(hq, jq // HT)
-                if more:
-                    if s == 8:
-                        fall_lead(nxt, 1, False)
-                    if s == 15:
-                        fall_lead(nxt, 3, False)
+                if ahead and s in rise_plan:
+                    relu_rise(h + 1, rise_plan[s])
                 if 0 <= hp < halves:
                     read_right(hp, jp)
                 if j == 3 and 0 <= h - 1 < halves:
@@ -338,3 +343,7 @@ def tile_kanlayerbspline_kernel(tc, x, coeff, bias, knots, out):
                     finish(h - 1)
                 if s == 15 and nxt + 1 < ROUNDS:
                     clip(nxt + 1)
+                if k == -1 and s == 8:
+                    scales_of_the_sides()
+                if k == -1 and s == 13:
+                    weights()

@@ -18,10 +18,8 @@ FLOPS = 2 * B * K * O
 P = 128
 PASSES = 4
 NT = 4
-HT = NT // 2
 N = NT * D
 G = N // 4
-HG = G // 2
 KN = 12
 ROUNDS = B // (NT * P)
 
@@ -34,7 +32,7 @@ def tile_kanlayerbspline_kernel(tc, x, coeff, bias, knots, out):
         cub = ctx.enter_context(tc.tile_pool(name="cub", bufs=2))
         sets = ctx.enter_context(tc.tile_pool(name="sets", bufs=2))
         work = ctx.enter_context(tc.tile_pool(name="work", bufs=3))
-        mxp = ctx.enter_context(tc.tile_pool(name="mxp", bufs=2))
+        mxp = ctx.enter_context(tc.tile_pool(name="mxp", bufs=1))
         ps_s = ctx.enter_context(tc.psum_pool(name="ps_s", bufs=3))
         ps_o = ctx.enter_context(tc.psum_pool(name="ps_o", bufs=2))
         ctx.enter_context(tc.manual_schedule())
@@ -190,65 +188,59 @@ def tile_kanlayerbspline_kernel(tc, x, coeff, bias, knots, out):
             squares[i] = t
 
         def knot_plane(t, i):
-            return t[:, i // 4].rearrange("p g (j l) -> p g j l", l=4)[:, :, i % 4, :]
-
-        def half(h):
-            return slice((h % 2) * HG, (h % 2 + 1) * HG)
+            return t[:].rearrange("p g (j l) -> p g j l", l=4)[:, :, i % 4, :]
 
         def cube(r, i):
-            if i == 0:
-                cubes[r] = cub.tile([P, 3, G, 16], F32, name="cubes_t")
+            key = (r, i // 4)
+            if key not in cubes:
+                cubes[key] = cub.tile([P, G, 16], F32, name="cubes%d" % (i // 4))
             nc.vector.scalar_tensor_tensor(
-                out=knot_plane(cubes[r], i),
+                out=knot_plane(cubes[key], i),
                 in0=us[r][:].rearrange("p n (g l) -> p (n g) l", l=4),
                 scalar=kn[:, i:i + 1],
                 in1=squares[i][:].rearrange("p (g l) -> p g l", l=4),
                 op0=ALU.subtract, op1=ALU.mult,
             )
 
-        def open_relus(h):
-            relus[h] = (
-                sets.tile([P, 2, HG, 16], F32, name="rp"), sets.tile([P, 2, HG, 16], F32, name="rm")
-            )
+        def relus_of(h):
+            if h not in relus:
+                relus[h] = (sets.tile([P, G, 16], F32, name="rp"), sets.tile([P, G, 16], F32, name="rm"))
+            return relus[h]
 
-        def relu_rise(h, mh):
-            dst = relus[h][0][:, mh]
-            same, after = cubes[h // 2][:, mh, half(h)], cubes[h // 2][:, mh + 1, half(h)]
-            for o, i in ((dst[:, :, 0:12], same[:, :, 4:16]), (dst[:, :, 12:16], after[:, :, 0:4])):
-                nc.vector.tensor_scalar(
-                    out=o, in0=i, scalar1=-1.0, scalar2=0.0, op0=ALU.mult, op1=ALU.min
-                )
+        def relu_rise(h, last):
+            r, mh = h // 2, h % 2
+            dst = relus_of(h)[0]
+            if last:
+                o, i = dst[:, :, 12:16], cubes[(r, mh + 1)][:, :, 0:4]
+            else:
+                o, i = dst[:, :, 0:12], cubes[(r, mh)][:, :, 4:16]
+            nc.vector.tensor_scalar(out=o, in0=i, scalar1=-1.0, scalar2=0.0, op0=ALU.mult, op1=ALU.min)
 
-        def relu_fall(h, m):
+        def relu_fall(h, j):
+            m = 4 * (h % 2) + j
             nc.scalar.activation(
-                out=knot_plane(relus[h][1], m), in_=knot_plane(cubes[h // 2], m + 3)[:, half(h)],
+                out=knot_plane(relus_of(h)[1], j), in_=knot_plane(cubes[(h // 2, (m + 3) // 4)], m + 3),
                 func=ACT.Relu, scale=fall[:, m:m + 1],
             )
 
         def sums(h, j):
-            c, n = j // HT, j % HT
-            e, mh = c // 2, c % 2
+            e, n = j // NT, j % NT
+            r, mh = h // 2, h % 2
             pair = []
             for side in range(2):
                 bank = ps_s.tile([P, 4, P], F32, tag="LR"[side], name="bank")
                 for t in range(4):
                     g = n * 64 + e * 32 + t * 8
-                    gc = (h % 2) * HG + g
-                    nc.tensor.matmul(
-                        out=bank[:, t, :],
-                        lhsT=cubes[h // 2][:, mh + side, gc:gc + 8, :].rearrange("p g z -> p (g z)"),
-                        rhs=identf[:], is_transpose=True, start=True, stop=False,
-                    )
-                    nc.tensor.matmul(
-                        out=bank[:, t, :],
-                        lhsT=relus[h][side][:, mh, g:g + 8, :].rearrange("p g z -> p (g z)"),
-                        rhs=identf[:], is_transpose=True, start=False, stop=True,
-                    )
+                    for s, lead in ((cubes[(r, mh + side)], True), (relus[h][side], False)):
+                        nc.tensor.matmul(
+                            out=bank[:, t, :], lhsT=s[:, g:g + 8, :].rearrange("p g z -> p (g z)"),
+                            rhs=identf[:], is_transpose=True, start=lead, stop=not lead,
+                        )
                 pair.append(bank[:].rearrange("p t b -> p b t"))
             banks[(h, j)] = pair
 
         def read_left(h, j):
-            mh = j // HT % 2
+            mh = h % 2
             t = work.tile([P, P, 4], BF16, name="left")
             nc.scalar.activation(
                 out=t[:], in_=banks[(h, j)][0], func=ACT.Relu, scale=side_scale[:, 0, mh:mh + 1]
@@ -256,29 +248,32 @@ def tile_kanlayerbspline_kernel(tc, x, coeff, bias, knots, out):
             lefts[(h, j)] = t
 
         def read_right(h, j):
-            c, n = j // HT, j % HT
+            e, n = j // NT, j % NT
+            mh = h % 2
             if n == 0:
-                groups[(h, c)] = work.tile([P, HT, P, 4], BF16, name="grouped", align_bytes=64)
+                groups[(h, e)] = work.tile([P, NT, P, 4], BF16, name="grouped", align_bytes=64)
             nc.vector.scalar_tensor_tensor(
-                out=groups[(h, c)][:, n], in0=banks[(h, j)][1], scalar=side_scale[:, 1, c % 2:c % 2 + 1],
+                out=groups[(h, e)][:, n], in0=banks[(h, j)][1], scalar=side_scale[:, 1, mh:mh + 1],
                 in1=lefts[(h, j)][:], op0=ALU.mult, op1=ALU.max,
             )
 
-        def quantise(h, c):
+        def quantise(h, e):
+            r, c = h // 2, 2 * e + h % 2
             if c == 0:
-                codes = mxp.tile([P, PASSES, HT * P], U32, name="codes", align_bytes=64)
-                scales = mxp.tile([P, PASSES, HT * P], U8, name="scales", align_bytes=64)
-                coded[h] = (codes, scales)
-            codes, scales = coded[h]
+                coded[r] = (
+                    mxp.tile([P, PASSES, NT * P], U32, name="codes", align_bytes=64),
+                    mxp.tile([P, PASSES, NT * P], U8, name="scales", align_bytes=64),
+                )
+            codes, scales = coded[r]
             nc.vector.quantize_mx(
                 out=codes[:, c, :].bitcast(FP8X4), scales=scales[:, c, :],
-                in_=groups[(h, c)][:].rearrange("p n b t -> p (n b t)"),
+                in_=groups[(h, e)][:].rearrange("p n b t -> p (n b t)"),
             )
 
-        def multiply(h):
-            codes, scales = coded[h]
-            acc = ps_o.tile([P, HT, O], F32, name="acc")
-            for n in range(HT):
+        def multiply(r):
+            codes, scales = coded[r]
+            acc = ps_o.tile([P, NT, O], F32, name="acc")
+            for n in range(NT):
                 cols = slice(n * P, (n + 1) * P)
                 for c in range(PASSES):
                     nc.tensor.matmul_mx(
@@ -288,62 +283,65 @@ def tile_kanlayerbspline_kernel(tc, x, coeff, bias, knots, out):
                         rhs_scale=w_scales[:, c * O:(c + 1) * O],
                         start=(c == 0), stop=(c == PASSES - 1),
                     )
-            accs[h] = acc
+            accs[r] = acc
 
-        def finish(h):
-            out_sb = xin.tile([P, HT, O], F32, name="out_sb")
+        def finish(r):
+            out_sb = xin.tile([P, NT, O], F32, name="out_sb")
             nc.vector.tensor_tensor(
-                out=out_sb[:], in0=accs[h][:], in1=bias_f[:].unsqueeze(1).to_broadcast([P, HT, O]),
+                out=out_sb[:], in0=accs[r][:], in1=bias_f[:].unsqueeze(1).to_broadcast([P, NT, O]),
                 op=ALU.add,
             )
-            n0 = (h % 2) * HT
-            nc.sync.dma_start(
-                out=out[rows_of(h // 2), :].rearrange("(p n) o -> p n o", n=NT)[:, n0:n0 + HT, :],
-                in_=out_sb[:],
-            )
+            nc.sync.dma_start(out=out[rows_of(r), :].rearrange("(p n) o -> p n o", n=NT), in_=out_sb[:])
 
-        CH = PASSES * HT
+        SLOTS = 2 * NT
+        square_plan = (
+            {0: (9, 0), 1: (10, 0), 2: (11, 0), 4: (4, 1), 5: (5, 1), 7: (3, 1)},
+            {0: (6, 1), 1: (2, 1), 2: (1, 1), 4: (7, 1), 5: (0, 1), 7: (8, 1)},
+        )
+        cube_plan = (
+            {0: (8, 0), 1: (9, 0), 2: (10, 0), 3: (11, 0), 5: (4, 1), 6: (5, 1)},
+            {0: (3, 1), 1: (6, 1), 2: (2, 1), 3: (1, 1), 5: (7, 1), 6: (0, 1)},
+        )
+        fall_plan = ({3: 0, 5: 1, 6: 2, 7: 3}, {3: 1, 5: 2, 6: 0, 7: 3})
+        rise_plan = {4: False, 7: True}
         halves = 2 * ROUNDS
-        fall_plan = {0: (0,), 1: (1,), 2: (2,), 3: (3,), 4: (4,), 5: (5,), 6: (6, 7),
-                     9: (0,), 11: (1,), 13: (2, 3), 14: (4, 5), 15: (6, 7)}
-        rise_plan = {0: 0, 7: 1, 14: 0, 15: 1}
-        for k in range(-1, ROUNDS + 1):
-            nxt = k + 1
-            more = nxt < ROUNDS
-            if nxt + 1 < ROUNDS:
-                load(nxt + 1)
-            for s in range(2 * CH):
-                h, j = 2 * k + s // CH, s % CH
-                hp, jp = (h, j - 1) if j > 0 else (h - 1, CH - 1)
-                hq, jq = (h, j - 3) if j > 2 else (h - 1, j + CH - 3)
+        for h in range(-2, halves + 1):
+            r, mh = h // 2, h % 2
+            if mh == 0 and 1 <= r + 2 < ROUNDS:
+                load(r + 2)
+            for s in range(SLOTS):
+                hp, sp = (h, s - 1) if s > 0 else (h - 1, SLOTS - 1)
                 if 0 <= h < halves:
-                    sums(h, j)
+                    sums(h, s)
                 if 0 <= hp < halves:
-                    read_left(hp, jp)
+                    read_left(hp, sp)
                 ahead = 0 <= h + 1 < halves
-                if ahead:
-                    if j == 0:
-                        open_relus(h + 1)
-                    for m in fall_plan.get(s, ()):
-                        relu_fall(h + 1, m)
-                if more:
-                    if s <= 5 or 7 <= s <= 12:
-                        square(nxt, s if s <= 5 else s - 1)
-                    if 1 <= s <= 6 or 8 <= s <= 13:
-                        cube(nxt, s - 1 if s <= 6 else s - 2)
-                if 0 <= hq < halves and jq % HT == HT - 1:
-                    quantise(hq, jq // HT)
+                if ahead and s in fall_plan[mh]:
+                    relu_fall(h + 1, fall_plan[mh][s])
+                if s in square_plan[mh]:
+                    i, later = square_plan[mh][s]
+                    if 0 <= r + later < ROUNDS:
+                        square(r + later, i)
+                if s in cube_plan[mh]:
+                    i, later = cube_plan[mh][s]
+                    if 0 <= r + later < ROUNDS:
+                        cube(r + later, i)
                 if ahead and s in rise_plan:
                     relu_rise(h + 1, rise_plan[s])
                 if 0 <= hp < halves:
-                    read_right(hp, jp)
-                if j == 3 and 0 <= h - 1 < halves:
-                    multiply(h - 1)
-                if j == 5 and 0 <= h - 1 < halves:
-                    finish(h - 1)
-                if s == 15 and nxt + 1 < ROUNDS:
-                    clip(nxt + 1)
-                if k == -1 and s == 8:
+                    read_right(hp, sp)
+                if s == 7 and 0 <= h < halves:
+                    quantise(h, 0)
+                if s == 2 and 0 <= h - 1 < halves:
+                    quantise(h - 1, 1)
+                if mh == 0 and 0 <= r - 1:
+                    if s == 4:
+                        multiply(r - 1)
+                    if s == 6:
+                        finish(r - 1)
+                if mh == 1 and s == 6 and r + 2 < ROUNDS:
+                    clip(r + 2)
+                if h == -2 and s == 7:
                     scales_of_the_sides()
-                if k == -1 and s == 13:
+                if h == -1 and s == 6:
                     weights()

@@ -218,6 +218,12 @@ def tile_kanlayerbspline_kernel(tc, x, coeff, bias, knots, out):
 
         def relu_fall(h, j):
             m = 4 * (h % 2) + j
+            if m == 5:
+                nc.vector.tensor_scalar(
+                    out=knot_plane(relus_of(h)[1], j), in0=knot_plane(cubes[(h // 2, 2)], m + 3),
+                    scalar1=fall[:, m:m + 1], scalar2=0.0, op0=ALU.mult, op1=ALU.max,
+                )
+                return
             nc.scalar.activation(
                 out=knot_plane(relus_of(h)[1], j), in_=knot_plane(cubes[(h // 2, (m + 3) // 4)], m + 3),
                 func=ACT.Relu, scale=fall[:, m:m + 1],

@@ -34,7 +34,7 @@ def tile_kanlayerbspline_kernel(tc, x, coeff, bias, knots, out):
         work = ctx.enter_context(tc.tile_pool(name="work", bufs=3))
         mxp = ctx.enter_context(tc.tile_pool(name="mxp", bufs=1))
         ps_s = ctx.enter_context(tc.psum_pool(name="ps_s", bufs=3))
-        ps_o = ctx.enter_context(tc.psum_pool(name="ps_o", bufs=2))
+        ps_o = ctx.enter_context(tc.psum_pool(name="ps_o", bufs=1))
         ctx.enter_context(tc.manual_schedule())
 
         def rows_of(r):
@@ -170,6 +170,7 @@ def tile_kanlayerbspline_kernel(tc, x, coeff, bias, knots, out):
                 in_=w_grp[:].rearrange("p c o t -> p (c o t)"),
             )
 
+        unread = ps_o.tile([P, PASSES * O], F32, name="unread")
         squares = {}
         cubes = {}
         relus = {}
@@ -244,6 +245,10 @@ def tile_kanlayerbspline_kernel(tc, x, coeff, bias, knots, out):
                         )
                 pair.append(bank[:].rearrange("p t b -> p b t"))
             banks[(h, j)] = pair
+            nc.tensor.matmul_mx(
+                out=unread[:], lhsT=w_codes[:, 0:P].bitcast(FP8X4), lhsT_scale=w_scales[:, 0:P],
+                rhs=w_codes[:].bitcast(FP8X4), rhs_scale=w_scales[:], start=True, stop=True,
+            )
 
         def read_left(h, j):
             mh = h % 2

@@ -19,9 +19,12 @@ P = 128
 PASSES = 4
 NT = 4
 N = NT * D
+HALF = N // 2
 G = N // 4
+GH = G // 2
 KN = 12
 ROUNDS = B // (NT * P)
+SLOTS = 8
 
 
 def tile_kanlayerbspline_kernel(tc, x, coeff, bias, knots, out):
@@ -31,9 +34,10 @@ def tile_kanlayerbspline_kernel(tc, x, coeff, bias, knots, out):
         xin = ctx.enter_context(tc.tile_pool(name="xin", bufs=2))
         cub = ctx.enter_context(tc.tile_pool(name="cub", bufs=2))
         sets = ctx.enter_context(tc.tile_pool(name="sets", bufs=2))
-        work = ctx.enter_context(tc.tile_pool(name="work", bufs=3))
-        mxp = ctx.enter_context(tc.tile_pool(name="mxp", bufs=1))
-        ps_s = ctx.enter_context(tc.psum_pool(name="ps_s", bufs=3))
+        one = ctx.enter_context(tc.tile_pool(name="one", bufs=1))
+        work = ctx.enter_context(tc.tile_pool(name="work", bufs=4))
+        ps_q = ctx.enter_context(tc.psum_pool(name="ps_q", bufs=4))
+        ps_t = ctx.enter_context(tc.psum_pool(name="ps_t", bufs=3))
         ps_o = ctx.enter_context(tc.psum_pool(name="ps_o", bufs=1))
         ctx.enter_context(tc.manual_schedule())
 
@@ -49,14 +53,15 @@ def tile_kanlayerbspline_kernel(tc, x, coeff, bias, knots, out):
             xs[r] = t
 
         def clip(r):
-            t = xin.tile([P, NT, D], BF16, name="u")
-            dst = t[:].rearrange("p n (e t v z) -> p (n e) t v z", e=2, t=4, v=2)
-            src = xs[r][:].rearrange("p n (e v t z) -> p (n e) v t z", e=2, v=2, t=4)
-            for v in range(2):
-                nc.vector.tensor_scalar(
-                    out=dst[:, :, :, v, :], in0=src[:, :, v], scalar1=-1.0, scalar2=1.0,
-                    op0=ALU.max, op1=ALU.min,
-                )
+            t = xin.tile([P, N], BF16, name="u")
+            dst = t[:].rearrange("p (e n t v z) -> p e n t v z", e=2, n=NT, t=4, v=2)
+            src = xs[r][:].rearrange("p n (e v t z) -> p n e v t z", e=2, v=2, t=4)
+            for e in range(2):
+                for v in range(2):
+                    nc.vector.tensor_scalar(
+                        out=dst[:, e, :, :, v, :], in0=src[:, :, e, v], scalar1=-1.0, scalar2=1.0,
+                        op0=ALU.max, op1=ALU.min,
+                    )
             us[r] = t
 
         kn_bf = const.tile([P, KN], BF16)
@@ -79,9 +84,12 @@ def tile_kanlayerbspline_kernel(tc, x, coeff, bias, knots, out):
             nc.vector.tensor_sub(out=d[:], in0=kn[:, a:a + 8], in1=kn[:, b:b + 8])
             return d
 
-        def mul(a, b, nm):
-            d = const.tile([P, 8], F32, name=nm)
-            nc.vector.tensor_mul(out=d[:], in0=a[:], in1=b[:])
+        def product(factors, nm):
+            d = factors[0]
+            for i, f in enumerate(factors[1:]):
+                p = const.tile([P, 8], F32, name="%s_%d" % (nm, i))
+                nc.vector.tensor_mul(out=p[:], in0=d[:], in1=f[:])
+                d = p
             return d
 
         def inverse(a, nm):
@@ -89,17 +97,20 @@ def tile_kanlayerbspline_kernel(tc, x, coeff, bias, knots, out):
             nc.vector.reciprocal(out=d[:], in_=a[:])
             return d
 
-        d20, d30, d40 = diff(2, 0, "d20"), diff(3, 0, "d30"), diff(4, 0, "d40")
+        d10, d20, d30, d40 = diff(1, 0, "d10"), diff(2, 0, "d20"), diff(3, 0, "d30"), diff(4, 0, "d40")
         d21, d31, d41 = diff(2, 1, "d21"), diff(3, 1, "d31"), diff(4, 1, "d41")
-        p20 = mul(d20, d30, "p20")
-        p21 = mul(mul(d21, d31, "p21a"), d41, "p21")
-        rise = mul(mul(d40, p20, "rise_a"), inverse(p21, "rise_b"), "rise")
+        d42, d43 = diff(4, 2, "d42"), diff(4, 3, "d43")
+        w0 = inverse(product([d10, d20, d30], "p0"), "w0")
+        w4 = inverse(product([d41, d42, d43], "p4"), "w4")
+        rise = product([d40, d20, d30, inverse(product([d21, d31, d41], "p1"), "i1")], "rise")
         ones = const.tile([P, 8], F32)
         nc.vector.memset(ones[:], 1.0)
         kap = const.tile([P, KN], F32)
         nc.vector.memset(kap[:], 1.0)
+        nc.vector.tensor_copy(out=kap[:, 0:4], in_=w0[:, 0:4])
+        nc.vector.tensor_copy(out=kap[:, 9:12], in_=w4[:, 5:8])
         nc.vector.tensor_tensor_scan(
-            out=kap[:, 1:9], data0=rise[:], data1=ones[:], initial=1.0, op0=ALU.mult, op1=ALU.mult
+            out=kap[:, 5:9], data0=rise[:, 4:8], data1=ones[:, 4:8], initial=1.0, op0=ALU.mult, op1=ALU.mult
         )
         sig0 = const.tile([P, KN], F32)
         nc.scalar.activation(out=sig0[:], in_=kap[:], func=ACT.Sqrt)
@@ -108,42 +119,51 @@ def tile_kanlayerbspline_kernel(tc, x, coeff, bias, knots, out):
         nc.vector.tensor_mul(out=sig[:], in0=sig[:], in1=kap[:])
         nc.vector.tensor_add(out=sig[:], in0=sig[:], in1=sig0[:])
         nc.vector.tensor_scalar_mul(out=sig[:], in0=sig[:], scalar1=0.5)
+        beta_neg = const.tile([P, KN], F32)
+        nc.vector.tensor_mul(out=beta_neg[:], in0=sig[:], in1=kn[:])
         beta = const.tile([P, KN], F32)
-        nc.vector.tensor_mul(out=beta[:], in0=sig[:], in1=kn[:])
-        nc.vector.tensor_scalar_mul(out=beta[:], in0=beta[:], scalar1=-1.0)
+        nc.vector.tensor_scalar_mul(out=beta[:], in0=beta_neg[:], scalar1=-1.0)
+        kn_neg = const.tile([P, KN], F32)
+        nc.vector.tensor_scalar_mul(out=kn_neg[:], in0=kn[:], scalar1=-1.0)
         clip(0)
 
-        side_scale = const.tile([P, 2, 2], F32)
-        fall = const.tile([P, 8], F32)
+        side_scale = const.tile([P, 2], F32)
+        tail8 = const.tile([P, 1], F32)
+        fall3 = const.tile([P, 8], F32)
+        fall2 = const.tile([P, 8], F32)
+        rise2 = const.tile([P, 8], F32)
         w_codes = const.tile([P, PASSES * O], U32, align_bytes=64)
         w_scales = const.tile([P, PASSES * O], U8, align_bytes=64)
         bias_f = const.tile([P, O], F32)
 
-        def scales_of_the_sides():
-            d10, d32 = diff(1, 0, "d10"), diff(3, 2, "d32")
-            d42, d43 = diff(4, 2, "d42"), diff(4, 3, "d43")
-            p41 = mul(d41, d42, "p41")
+        def weights_of_the_terms():
+            d32 = diff(3, 2, "d32")
             ikap = const.tile([P, KN], F32, name="ikap")
             nc.vector.reciprocal(out=ikap[:], in_=kap[:])
-            q = mul(mul(d30, d31, "q_a"), d32, "q_b")
-            t = mul(mul(d40, p41, "fall_a"), inverse(q, "fall_b"), "fall_c")
-            nc.vector.tensor_mul(out=t[:], in0=t[:], in1=kap[:, 4:12])
-            nc.vector.tensor_mul(out=t[:], in0=t[:], in1=ikap[:, 3:11])
-            nc.vector.tensor_scalar_mul(out=fall[:], in0=t[:], scalar1=-1.0)
-            w0 = inverse(mul(d10, p20, "p10"), "w0")
-            w4 = inverse(mul(p41, d43, "p43"), "w4")
-            nc.vector.tensor_mul(out=w0[:], in0=w0[:], in1=ikap[:, 0:8])
-            nc.vector.tensor_mul(out=w4[:], in0=w4[:], in1=ikap[:, 4:12])
-            nc.vector.tensor_scalar_mul(out=w4[:], in0=w4[:], scalar1=-1.0)
+            q = product([d40, d41, d42, inverse(product([d30, d31, d32], "p3"), "i3")], "f3")
+            nc.vector.tensor_mul(out=q[:], in0=q[:], in1=kap[:, 4:12])
+            nc.vector.tensor_mul(out=q[:], in0=q[:], in1=ikap[:, 3:11])
+            nc.vector.tensor_scalar_mul(out=fall3[:], in0=q[:], scalar1=-1.0)
+            q = product([d40, d41, d43, inverse(product([d20, d21, d32], "p2"), "i2")], "f2")
+            nc.vector.tensor_mul(out=q[:], in0=q[:], in1=kap[:, 4:12])
+            nc.vector.tensor_mul(out=fall2[:], in0=q[:], in1=ikap[:, 2:10])
+            q = product([d40, d10, d30, inverse(product([d21, d32, d42], "p5"), "i5")], "r2")
+            nc.vector.tensor_mul(out=q[:], in0=q[:], in1=kap[:, 0:8])
+            nc.vector.tensor_mul(out=rise2[:], in0=q[:], in1=ikap[:, 2:10])
+            nc.vector.tensor_mul(out=tail8[:], in0=w4[:, 4:5], in1=ikap[:, 8:9])
+            nc.vector.tensor_scalar_mul(out=tail8[:], in0=tail8[:], scalar1=-1.0)
             pick = const.tile([P, 4], F32, name="pick")
             nc.vector.tensor_reduce(
                 out=pick[:], in_=identf[:].rearrange("p (x j l) -> p j x l", x=8, j=4, l=4),
                 op=ALU.add, axis=AX.XY,
             )
-            for side, w in ((0, w0), (1, w4)):
-                wv = w[:].rearrange("p (h j) -> p h j", j=4)
-                nc.vector.tensor_mul(out=wv, in0=wv, in1=pick[:].unsqueeze(1).to_broadcast([P, 2, 4]))
-                nc.vector.tensor_reduce(out=side_scale[:, side, :], in_=wv, op=ALU.add, axis=AX.X)
+            s = const.tile([P, 2, 4], F32, name="s")
+            nc.vector.tensor_scalar_mul(out=s[:, 0, :], in0=w4[:, 0:4], scalar1=-1.0)
+            nc.vector.tensor_copy(out=s[:, 1, :], in_=w0[:, 4:8])
+            for h in range(2):
+                nc.vector.tensor_mul(out=s[:, h, :], in0=s[:, h, :], in1=ikap[:, 4:8])
+                nc.vector.tensor_mul(out=s[:, h, :], in0=s[:, h, :], in1=pick[:])
+            nc.vector.tensor_reduce(out=side_scale[:], in_=s[:], op=ALU.add, axis=AX.X)
 
         def weights():
             nc.vector.tensor_copy(out=bias_f[:], in_=bias_bf[:])
@@ -160,7 +180,7 @@ def tile_kanlayerbspline_kernel(tc, x, coeff, bias, knots, out):
                         )
             w_grp = const.tile([P, PASSES, O, 4], BF16, name="w_grp", align_bytes=64)
             for c in range(PASSES):
-                wT = ps_s.tile([P, 4, P], BF16, tag="L")
+                wT = ps_q.tile([P, 4, P], BF16, tag="Q")
                 for t in range(4):
                     nc.tensor.transpose(wT[:, t, :], w_perm[:, c, t, :], ident[:])
                 nc.vector.tensor_copy(out=w_grp[:, c, :, :], in_=wT[:].rearrange("p t o -> p o t"))
@@ -170,126 +190,195 @@ def tile_kanlayerbspline_kernel(tc, x, coeff, bias, knots, out):
                 in_=w_grp[:].rearrange("p c o t -> p (c o t)"),
             )
 
-        unread = ps_o.tile([P, PASSES * O], F32, name="unread")
         squares = {}
-        cubes = {}
-        relus = {}
-        banks = {}
-        lefts = {}
-        groups = {}
+        clamped = {}
+        paired = {}
+        mids = {}
+        outer = {}
+        tails = {}
+        terms = {}
+        q_banks = {}
+        t_banks = {}
+        grouped = {}
         coded = {}
         accs = {}
 
+        def pair(r):
+            t = one.tile([P, N], BF16, name="paired")
+            nc.vector.tensor_copy(
+                out=t[:].rearrange("p (a c s) -> p a c s", s=2, c=32),
+                in_=us[r][:].rearrange("p (a s c) -> p a c s", s=2, c=32),
+            )
+            paired[r] = t
+
+        def clamp(r, i):
+            t = work.tile([P, N // 8, 8], BF16, name="z")
+            dst = t[:].rearrange("p a z -> p (a z)")
+            src = paired[r][:]
+            if i < 4:
+                nc.vector.tensor_scalar(out=dst, in0=src, scalar1=kn[:, i:i + 1], scalar2=None, op0=ALU.max)
+            else:
+                nc.vector.tensor_scalar(
+                    out=dst, in0=src, scalar1=-1.0, scalar2=kn_neg[:, i:i + 1], op0=ALU.mult, op1=ALU.max
+                )
+            clamped[i] = t
+
         def square(r, i):
             t = work.tile([P, N], F32, name="sq")
+            if i in (0, 1, 10, 11):
+                src = clamped[i][:].rearrange("p a z -> p (a z)")
+                b = beta if i < 4 else beta_neg
+            else:
+                src, b = us[r][:], beta
             nc.scalar.activation(
-                out=t[:], in_=us[r][:].rearrange("p n d -> p (n d)"), func=ACT.Square,
-                bias=beta[:, i:i + 1], scale=sig[:, i:i + 1],
+                out=t[:], in_=src, func=ACT.Square, bias=b[:, i:i + 1], scale=sig[:, i:i + 1],
             )
             squares[i] = t
 
-        def knot_plane(t, i):
-            return t[:].rearrange("p g (j l) -> p g j l", l=4)[:, :, i % 4, :]
+        def knot_plane(t, j):
+            return t.rearrange("p g (j l) -> p g j l", l=4)[:, :, j, :]
+
+        def tails_of(r):
+            if r not in tails:
+                tails[r] = cub.tile([P, 2, N // 8, 32], BF16, name="tails")
+            return tails[r]
 
         def cube(r, i):
-            key = (r, i // 4)
-            if key not in cubes:
-                cubes[key] = cub.tile([P, G, 16], F32, name="cubes%d" % (i // 4))
-            nc.vector.scalar_tensor_tensor(
-                out=knot_plane(cubes[key], i),
-                in0=us[r][:].rearrange("p n (g l) -> p (n g) l", l=4),
-                scalar=kn[:, i:i + 1],
-                in1=squares[i][:].rearrange("p (g l) -> p g l", l=4),
-                op0=ALU.subtract, op1=ALU.mult,
-            )
-
-        def relus_of(h):
-            if h not in relus:
-                relus[h] = (sets.tile([P, G, 16], F32, name="rp"), sets.tile([P, G, 16], F32, name="rm"))
-            return relus[h]
-
-        def relu_rise(h, last):
-            r, mh = h // 2, h % 2
-            dst = relus_of(h)[0]
-            if last:
-                o, i = dst[:, :, 12:16], cubes[(r, mh + 1)][:, :, 0:4]
-            else:
-                o, i = dst[:, :, 0:12], cubes[(r, mh)][:, :, 4:16]
-            nc.vector.tensor_scalar(out=o, in0=i, scalar1=-1.0, scalar2=0.0, op0=ALU.mult, op1=ALU.min)
-
-        def relu_fall(h, j):
-            m = 4 * (h % 2) + j
-            if m == 5:
-                nc.vector.tensor_scalar(
-                    out=knot_plane(relus_of(h)[1], j), in0=knot_plane(cubes[(h // 2, 2)], m + 3),
-                    scalar1=fall[:, m:m + 1], scalar2=0.0, op0=ALU.mult, op1=ALU.max,
+            if i in (0, 1, 10, 11):
+                k = kn if i < 4 else kn_neg
+                j = i % 4
+                nc.vector.scalar_tensor_tensor(
+                    out=tails_of(r)[:, i // 8, :, 8 * j:8 * j + 8], in0=clamped[i][:], scalar=k[:, i:i + 1],
+                    in1=squares[i][:].rearrange("p (a z) -> p a z", z=8), op0=ALU.subtract, op1=ALU.mult,
                 )
                 return
-            nc.scalar.activation(
-                out=knot_plane(relus_of(h)[1], j), in_=knot_plane(cubes[(h // 2, (m + 3) // 4)], m + 3),
-                func=ACT.Relu, scale=fall[:, m:m + 1],
-            )
-
-        def sums(h, j):
-            e, n = j // NT, j % NT
-            r, mh = h // 2, h % 2
-            pair = []
-            for side in range(2):
-                bank = ps_s.tile([P, 4, P], F32, tag="LR"[side], name="bank")
-                for t in range(4):
-                    g = n * 64 + e * 32 + t * 8
-                    for s, lead in ((cubes[(r, mh + side)], True), (relus[h][side], False)):
-                        nc.tensor.matmul(
-                            out=bank[:, t, :], lhsT=s[:, g:g + 8, :].rearrange("p g z -> p (g z)"),
-                            rhs=identf[:], is_transpose=True, start=lead, stop=not lead,
-                        )
-                pair.append(bank[:].rearrange("p t b -> p b t"))
-            banks[(h, j)] = pair
-            nc.tensor.matmul_mx(
-                out=unread[:], lhsT=w_codes[:, 0:P].bitcast(FP8X4), lhsT_scale=w_scales[:, 0:P],
-                rhs=w_codes[:].bitcast(FP8X4), rhs_scale=w_scales[:], start=True, stop=True,
-            )
-
-        def read_left(h, j):
-            mh = h % 2
-            t = work.tile([P, P, 4], BF16, name="left")
-            nc.scalar.activation(
-                out=t[:], in_=banks[(h, j)][0], func=ACT.Relu, scale=side_scale[:, 0, mh:mh + 1]
-            )
-            lefts[(h, j)] = t
-
-        def read_right(h, j):
-            e, n = j // NT, j % NT
-            mh = h % 2
-            if n == 0:
-                groups[(h, e)] = work.tile([P, NT, P, 4], BF16, name="grouped", align_bytes=64)
+            if 4 <= i < 8:
+                if r not in mids:
+                    mids[r] = cub.tile([P, G, 16], F32, name="mids")
+                dst = knot_plane(mids[r][:], i - 4)
+            else:
+                pool = cub if i in (3, 8) else one
+                outer[(r, i)] = pool.tile([P, N], F32, name="outer%d" % i)
+                dst = outer[(r, i)][:].rearrange("p (g l) -> p g l", l=4)
             nc.vector.scalar_tensor_tensor(
-                out=groups[(h, e)][:, n], in0=banks[(h, j)][1], scalar=side_scale[:, 1, mh:mh + 1],
-                in1=lefts[(h, j)][:], op0=ALU.mult, op1=ALU.max,
+                out=dst, in0=us[r][:].rearrange("p (g l) -> p g l", l=4), scalar=kn[:, i:i + 1],
+                in1=squares[i][:].rearrange("p (g l) -> p g l", l=4), op0=ALU.subtract, op1=ALU.mult,
             )
 
-        def quantise(h, e):
-            r, c = h // 2, 2 * e + h % 2
-            if c == 0:
-                coded[r] = (
-                    mxp.tile([P, PASSES, NT * P], U32, name="codes", align_bytes=64),
-                    mxp.tile([P, PASSES, NT * P], U8, name="scales", align_bytes=64),
+        def outer_tail(r, i):
+            src = outer[(r, i)][:].rearrange("p (a s v l) -> p a s v l", s=2, v=8, l=4)
+            j = i % 4
+            dst = tails_of(r)[:, i // 8, :, 8 * j:8 * j + 8].rearrange("p (a v) (l s) -> p a v l s", v=8, s=2)
+            factor = {2: 1.0, 3: 1.0, 8: tail8[:, 0:1], 9: -1.0}[i]
+            for s in range(2):
+                nc.vector.tensor_scalar(
+                    out=dst[:, :, :, :, s], in0=src[:, :, s], scalar1=factor, scalar2=0.0,
+                    op0=ALU.mult, op1=ALU.max,
                 )
-            codes, scales = coded[r]
-            nc.vector.quantize_mx(
-                out=codes[:, c, :].bitcast(FP8X4), scales=scales[:, c, :],
-                in_=groups[(h, e)][:].rearrange("p n b t -> p (n b t)"),
+
+        def terms_of(k):
+            if k not in terms:
+                terms[k] = {
+                    nm: sets.tile([P, GH, 16], F32, name=nm) for nm in ("right5", "right6", "left3", "left2")
+                }
+            return terms[k]
+
+        def knot_half(k, i):
+            r, e = k // 2, k % 2
+            if 4 <= i < 8:
+                return knot_plane(mids[r][:, e * GH:(e + 1) * GH, :], i - 4)
+            return outer[(r, i)][:, e * HALF:(e + 1) * HALF].rearrange("p (g l) -> p g l", l=4)
+
+        def right5(k, last):
+            dst = terms_of(k)["right5"]
+            r, e = k // 2, k % 2
+            if last:
+                o, i = dst[:, :, 12:16], knot_half(k, 8)
+            else:
+                o, i = dst[:, :, 0:12], mids[r][:, e * GH:(e + 1) * GH, 4:16]
+            nc.vector.tensor_scalar(out=o, in0=i, scalar1=-1.0, scalar2=0.0, op0=ALU.mult, op1=ALU.min)
+
+        def right6(k, j):
+            nc.scalar.activation(
+                out=knot_plane(terms_of(k)["right6"][:], j), in_=knot_half(k, j + 6), func=ACT.Relu,
+                scale=rise2[:, 4 + j:5 + j],
             )
+
+        def left3(k, j):
+            nc.scalar.activation(
+                out=knot_plane(terms_of(k)["left3"][:], j), in_=knot_half(k, j + 3), func=ACT.Relu,
+                scale=fall3[:, j:j + 1],
+            )
+
+        def left2(k, j):
+            nc.vector.tensor_scalar(
+                out=knot_plane(terms_of(k)["left2"][:], j), in0=knot_half(k, j + 2),
+                scalar1=fall2[:, j:j + 1], scalar2=0.0, op0=ALU.mult, op1=ALU.min,
+            )
+
+        def sums(r, s):
+            e, n = s // NT, s % NT
+            k = 2 * r + e
+            bank = ps_q.tile([P, 4, P], F32, tag="Q", name="q_bank")
+            tm = terms_of(k)
+            for t in range(4):
+                g = n * 32 + t * 8
+                parts = [mids[r][:, e * GH + g:e * GH + g + 8, :]]
+                parts += [tm[nm][:, g:g + 8, :] for nm in ("right5", "right6", "left3", "left2")]
+                for i, part in enumerate(parts):
+                    nc.tensor.matmul(
+                        out=bank[:, t, :], lhsT=part.rearrange("p g z -> p (g z)"), rhs=identf[:],
+                        is_transpose=True, start=(i == 0), stop=(i == len(parts) - 1),
+                    )
+            q_banks[(r, s)] = bank
+
+        def turn_tails(r, s):
+            bank = ps_t.tile([P, 2, P, 2], F32, name="t_bank")
+            words = tails[r][:].rearrange("p h a z -> p h (a z)").bitcast(F32)
+            for h in range(2):
+                for u in range(2):
+                    a = (s * 2 + u) * P
+                    nc.tensor.matmul(
+                        out=bank[:, h, :, u], lhsT=words[:, h, a:a + P], rhs=identf[:],
+                        is_transpose=True, start=True, stop=True,
+                    )
+            t_banks[(r, s)] = bank
+
+        def read_sums(r, s):
+            e, n = s // NT, s % NT
+            if n == 0:
+                grouped[(r, e)] = xin.tile([P, NT, 2, P, 4], BF16, name="grouped", align_bytes=64)
+            for h in range(2):
+                nc.scalar.activation(
+                    out=grouped[(r, e)][:, n, h], in_=q_banks[(r, s)][:].rearrange("p t b -> p b t"),
+                    func=ACT.Relu, scale=side_scale[:, h:h + 1],
+                )
+
+        def take_tails(r, s):
+            e, n = s // NT, s % NT
+            o = grouped[(r, e)][:, n].rearrange("p h b t -> p (h b t)")
+            nc.vector.tensor_tensor(
+                out=o, in0=t_banks[(r, s)][:].rearrange("p h b u -> p (h b u)").bitcast(BF16), in1=o, op=ALU.min
+            )
+
+        def quantise(r, e):
+            codes = one.tile([P, NT, 2, P], U32, name="codes%d" % e, align_bytes=64)
+            scales = one.tile([P, NT, 2, P], U8, name="scales%d" % e, align_bytes=64)
+            nc.vector.quantize_mx(
+                out=codes[:].rearrange("p n h b -> p (n h b)").bitcast(FP8X4),
+                scales=scales[:].rearrange("p n h b -> p (n h b)"),
+                in_=grouped[(r, e)][:].rearrange("p n h b t -> p (n h b t)"),
+            )
+            coded[(r, e)] = (codes, scales)
 
         def multiply(r):
-            codes, scales = coded[r]
             acc = ps_o.tile([P, NT, O], F32, name="acc")
             for n in range(NT):
-                cols = slice(n * P, (n + 1) * P)
                 for c in range(PASSES):
+                    codes, scales = coded[(r, c // 2)]
                     nc.tensor.matmul_mx(
                         out=acc[:, n, :],
-                        lhsT=codes[:, c, cols].bitcast(FP8X4), lhsT_scale=scales[:, c, cols],
+                        lhsT=codes[:, n, c % 2, :].bitcast(FP8X4), lhsT_scale=scales[:, n, c % 2, :],
                         rhs=w_codes[:, c * O:(c + 1) * O].bitcast(FP8X4),
                         rhs_scale=w_scales[:, c * O:(c + 1) * O],
                         start=(c == 0), stop=(c == PASSES - 1),
@@ -304,55 +393,66 @@ def tile_kanlayerbspline_kernel(tc, x, coeff, bias, knots, out):
             )
             nc.sync.dma_start(out=out[rows_of(r), :].rearrange("(p n) o -> p n o", n=NT), in_=out_sb[:])
 
-        SLOTS = 2 * NT
-        square_plan = (
-            {0: (9, 0), 1: (10, 0), 2: (11, 0), 4: (4, 1), 5: (5, 1), 7: (3, 1)},
-            {0: (6, 1), 1: (2, 1), 2: (1, 1), 4: (7, 1), 5: (0, 1), 7: (8, 1)},
-        )
-        cube_plan = (
-            {0: (8, 0), 1: (9, 0), 2: (10, 0), 3: (11, 0), 5: (4, 1), 6: (5, 1)},
-            {0: (3, 1), 1: (6, 1), 2: (2, 1), 3: (1, 1), 5: (7, 1), 6: (0, 1)},
-        )
-        fall_plan = ({3: 0, 5: 1, 6: 2, 7: 3}, {3: 1, 5: 2, 6: 0, 7: 3})
-        rise_plan = {4: False, 7: True}
-        halves = 2 * ROUNDS
-        for h in range(-2, halves + 1):
-            r, mh = h // 2, h % 2
-            if mh == 0 and 1 <= r + 2 < ROUNDS:
+        square_plan = ((4,), (5, 6), (7,), (9, 2), (0,), (1, 10), (11,), (8, 3))
+        cube_plan = ((8, 3), (4,), (5, 6), (7,), (9, 2), (0,), (1, 10), (11,))
+        clamp_plan = {3: (0,), 4: (1, 10), 5: (11,)}
+        outer_tail_plan = {1: 8, 3: 3, 6: 2, 7: 9}
+
+        def live(r):
+            return 0 <= r < ROUNDS
+
+        for r in range(-2, ROUNDS + 1):
+            if 1 <= r + 2 < ROUNDS:
                 load(r + 2)
             for s in range(SLOTS):
-                hp, sp = (h, s - 1) if s > 0 else (h - 1, SLOTS - 1)
-                if 0 <= h < halves:
-                    sums(h, s)
-                if 0 <= hp < halves:
-                    read_left(hp, sp)
-                ahead = 0 <= h + 1 < halves
-                if ahead and s in fall_plan[mh]:
-                    relu_fall(h + 1, fall_plan[mh][s])
-                if s in square_plan[mh]:
-                    i, later = square_plan[mh][s]
-                    if 0 <= r + later < ROUNDS:
-                        square(r + later, i)
-                if s in cube_plan[mh]:
-                    i, later = cube_plan[mh][s]
-                    if 0 <= r + later < ROUNDS:
-                        cube(r + later, i)
-                if ahead and s in rise_plan:
-                    relu_rise(h + 1, rise_plan[s])
-                if 0 <= hp < halves:
-                    read_right(hp, sp)
-                if s == 7 and 0 <= h < halves:
-                    quantise(h, 0)
-                if s == 2 and 0 <= h - 1 < halves:
-                    quantise(h - 1, 1)
-                if mh == 0 and 0 <= r - 1:
-                    if s == 4:
-                        multiply(r - 1)
-                    if s == 6:
-                        finish(r - 1)
-                if mh == 1 and s == 6 and r + 2 < ROUNDS:
+                prev = (r, s - 1) if s > 0 else (r - 1, SLOTS - 1)
+                i = s % 4
+                k = 2 * r + (1 if s < 4 else 2)
+                if live(r):
+                    sums(r, s)
+                if live(prev[0]):
+                    turn_tails(*prev)
+                    read_sums(*prev)
+                later = r + 2 if s == 7 else r + 1
+                for knot in square_plan[s]:
+                    if live(later):
+                        square(later, knot)
+                if live(k // 2):
+                    left3(k, i)
+                    right6(k, i)
+                for knot in cube_plan[s]:
+                    if live(r + 1):
+                        cube(r + 1, knot)
+                if live(k // 2):
+                    if i == 1:
+                        right5(k, False)
+                        right5(k, True)
+                    if i == 2:
+                        left2(k, 1)
+                    if i == 3:
+                        left2(k, 0)
+                        left2(k, 2)
+                        left2(k, 3)
+                if live(r + 1):
+                    if s == 1:
+                        pair(r + 1)
+                    for knot in clamp_plan.get(s, ()):
+                        clamp(r + 1, knot)
+                    if s in outer_tail_plan:
+                        outer_tail(r + 1, outer_tail_plan[s])
+                if live(prev[0]):
+                    take_tails(*prev)
+                if s == 5 and live(r):
+                    quantise(r, 0)
+                if s == 2 and live(r - 1):
+                    quantise(r - 1, 1)
+                if s == 4 and live(r - 1):
+                    multiply(r - 1)
+                if s == 6 and live(r - 1):
+                    finish(r - 1)
+                if s == 5 and 1 <= r + 2 < ROUNDS:
                     clip(r + 2)
-                if h == -2 and s == 7:
-                    scales_of_the_sides()
-                if h == -1 and s == 6:
+                if r == -2 and s == 7:
+                    weights_of_the_terms()
+                if r == -1 and s == 6:
                     weights()

@@ -36,8 +36,8 @@ def tile_kanlayerbspline_kernel(tc, x, coeff, bias, knots, out):
         sets = ctx.enter_context(tc.tile_pool(name="sets", bufs=2))
         one = ctx.enter_context(tc.tile_pool(name="one", bufs=1))
         work = ctx.enter_context(tc.tile_pool(name="work", bufs=4))
-        ps_q = ctx.enter_context(tc.psum_pool(name="ps_q", bufs=4))
-        ps_t = ctx.enter_context(tc.psum_pool(name="ps_t", bufs=3))
+        ps_q = ctx.enter_context(tc.psum_pool(name="ps_q", bufs=3))
+        ps_t = ctx.enter_context(tc.psum_pool(name="ps_t", bufs=2))
         ps_o = ctx.enter_context(tc.psum_pool(name="ps_o", bufs=1))
         ctx.enter_context(tc.manual_schedule())
 
@@ -132,6 +132,8 @@ def tile_kanlayerbspline_kernel(tc, x, coeff, bias, knots, out):
         fall3 = const.tile([P, 8], F32)
         fall2 = const.tile([P, 8], F32)
         rise2 = const.tile([P, 8], F32)
+        again6 = const.tile([P, 4], F32)
+        again2 = const.tile([P, 4], F32)
         w_codes = const.tile([P, PASSES * O], U32, align_bytes=64)
         w_scales = const.tile([P, PASSES * O], U8, align_bytes=64)
         bias_f = const.tile([P, O], F32)
@@ -150,6 +152,10 @@ def tile_kanlayerbspline_kernel(tc, x, coeff, bias, knots, out):
             q = product([d40, d10, d30, inverse(product([d21, d32, d42], "p5"), "i5")], "r2")
             nc.vector.tensor_mul(out=q[:], in0=q[:], in1=kap[:, 0:8])
             nc.vector.tensor_mul(out=rise2[:], in0=q[:], in1=ikap[:, 2:10])
+            nc.vector.tensor_scalar_mul(out=again6[:], in0=rise2[:, 4:8], scalar1=-1.0)
+            nc.vector.memset(again2[:], 0.0)
+            nc.vector.reciprocal(out=again2[:, 1:4], in_=fall3[:, 0:3])
+            nc.vector.tensor_mul(out=again2[:, 1:4], in0=again2[:, 1:4], in1=fall2[:, 1:4])
             nc.vector.tensor_mul(out=tail8[:], in0=w4[:, 4:5], in1=ikap[:, 8:9])
             nc.vector.tensor_scalar_mul(out=tail8[:], in0=tail8[:], scalar1=-1.0)
             pick = const.tile([P, 4], F32, name="pick")
@@ -167,7 +173,7 @@ def tile_kanlayerbspline_kernel(tc, x, coeff, bias, knots, out):
 
         def weights():
             nc.vector.tensor_copy(out=bias_f[:], in_=bias_bf[:])
-            w_perm = const.tile([P, PASSES, 4, P], BF16, name="w_perm")
+            w_perm = xin.tile([P, PASSES, 4, P], BF16, tag="grouped", name="w_perm", align_bytes=64)
             wv = w_nat[:].rearrange("o (e v t q l h j) -> o e h t v q j l", e=2, v=2, t=4, q=4, l=4, h=2, j=4)
             for c in range(PASSES):
                 for t in range(4):
@@ -178,7 +184,7 @@ def tile_kanlayerbspline_kernel(tc, x, coeff, bias, knots, out):
                             ),
                             in_=wv[:, c // 2, c % 2, t, v],
                         )
-            w_grp = const.tile([P, PASSES, O, 4], BF16, name="w_grp", align_bytes=64)
+            w_grp = xin.tile([P, PASSES, O, 4], BF16, tag="grouped", name="w_grp", align_bytes=64)
             for c in range(PASSES):
                 wT = ps_q.tile([P, 4, P], BF16, tag="Q")
                 for t in range(4):
@@ -193,6 +199,8 @@ def tile_kanlayerbspline_kernel(tc, x, coeff, bias, knots, out):
         squares = {}
         clamped = {}
         paired = {}
+        turned = {}
+        u_psum = {}
         mids = {}
         outer = {}
         tails = {}
@@ -202,6 +210,23 @@ def tile_kanlayerbspline_kernel(tc, x, coeff, bias, knots, out):
         grouped = {}
         coded = {}
         accs = {}
+
+        def turn_u(r):
+            t = ps_o.tile([P, N // P, P], BF16, name="u_turned")
+            for a in range(N // P):
+                nc.tensor.transpose(t[:, a, :], us[r][:, a * P:(a + 1) * P], ident[:])
+            turned[r] = t
+
+        def copy_u(r):
+            t = one.tile([P, N // P, P], BF16, name="u_across")
+            nc.scalar.copy(out=t[:], in_=turned[r][:])
+            turned[r] = t
+
+        def return_u(r):
+            t = ps_o.tile([P, N], BF16, name="u_psum")
+            for a in range(N // P):
+                nc.tensor.transpose(t[:, a * P:(a + 1) * P], turned[r][:, a, :], ident[:])
+            u_psum[r] = t
 
         def pair(r):
             t = one.tile([P, N], BF16, name="paired")
@@ -261,7 +286,7 @@ def tile_kanlayerbspline_kernel(tc, x, coeff, bias, knots, out):
                 outer[(r, i)] = pool.tile([P, N], F32, name="outer%d" % i)
                 dst = outer[(r, i)][:].rearrange("p (g l) -> p g l", l=4)
             nc.vector.scalar_tensor_tensor(
-                out=dst, in0=us[r][:].rearrange("p (g l) -> p g l", l=4), scalar=kn[:, i:i + 1],
+                out=dst, in0=u_psum[r][:].rearrange("p (g l) -> p g l", l=4), scalar=kn[:, i:i + 1],
                 in1=squares[i][:].rearrange("p (g l) -> p g l", l=4), op0=ALU.subtract, op1=ALU.mult,
             )
 
@@ -299,9 +324,15 @@ def tile_kanlayerbspline_kernel(tc, x, coeff, bias, knots, out):
             nc.vector.tensor_scalar(out=o, in0=i, scalar1=-1.0, scalar2=0.0, op0=ALU.mult, op1=ALU.min)
 
         def right6(k, j):
-            nc.scalar.activation(
-                out=knot_plane(terms_of(k)["right6"][:], j), in_=knot_half(k, j + 6), func=ACT.Relu,
-                scale=rise2[:, 4 + j:5 + j],
+            if j == 3:
+                nc.scalar.activation(
+                    out=knot_plane(terms_of(k)["right6"][:], j), in_=knot_half(k, j + 6), func=ACT.Relu,
+                    scale=rise2[:, 4 + j:5 + j],
+                )
+                return
+            nc.gpsimd.tensor_scalar(
+                out=knot_plane(terms_of(k)["right6"][:], j), in0=knot_plane(terms_of(k)["right5"][:], j + 1),
+                scalar1=again6[:, j:j + 1], scalar2=0.0, op0=ALU.mult, op1=ALU.add,
             )
 
         def left3(k, j):
@@ -311,6 +342,12 @@ def tile_kanlayerbspline_kernel(tc, x, coeff, bias, knots, out):
             )
 
         def left2(k, j):
+            if j >= 2:
+                nc.gpsimd.tensor_scalar(
+                    out=knot_plane(terms_of(k)["left2"][:], j), in0=knot_plane(terms_of(k)["left3"][:], j - 1),
+                    scalar1=again2[:, j:j + 1], scalar2=0.0, op0=ALU.mult, op1=ALU.add,
+                )
+                return
             nc.vector.tensor_scalar(
                 out=knot_plane(terms_of(k)["left2"][:], j), in0=knot_half(k, j + 2),
                 scalar1=fall2[:, j:j + 1], scalar2=0.0, op0=ALU.mult, op1=ALU.min,
@@ -347,7 +384,7 @@ def tile_kanlayerbspline_kernel(tc, x, coeff, bias, knots, out):
         def read_sums(r, s):
             e, n = s // NT, s % NT
             if n == 0:
-                grouped[(r, e)] = xin.tile([P, NT, 2, P, 4], BF16, name="grouped", align_bytes=64)
+                grouped[(r, e)] = xin.tile([P, NT, 2, P, 4], BF16, tag="grouped", name="grouped", align_bytes=64)
             for h in range(2):
                 nc.scalar.activation(
                     out=grouped[(r, e)][:, n, h], in_=q_banks[(r, s)][:].rearrange("p t b -> p b t"),
@@ -412,27 +449,38 @@ def tile_kanlayerbspline_kernel(tc, x, coeff, bias, knots, out):
                     sums(r, s)
                 if live(prev[0]):
                     turn_tails(*prev)
+                if s == 5 and 1 <= r + 2 < ROUNDS:
+                    turn_u(r + 2)
+                if s == 7 and 1 <= r + 2 < ROUNDS:
+                    return_u(r + 2)
+                if live(prev[0]):
                     read_sums(*prev)
+                if s == 6 and 1 <= r + 2 < ROUNDS:
+                    copy_u(r + 2)
                 later = r + 2 if s == 7 else r + 1
                 for knot in square_plan[s]:
                     if live(later):
                         square(later, knot)
                 if live(k // 2):
-                    left3(k, i)
-                    right6(k, i)
+                    for j in ((0, 1), (2,), (3,), ())[i]:
+                        left3(k, j)
+                    if i == 3:
+                        right6(k, 3)
                 for knot in cube_plan[s]:
                     if live(r + 1):
                         cube(r + 1, knot)
                 if live(k // 2):
-                    if i == 1:
+                    if i == 0:
                         right5(k, False)
+                    if i == 1:
                         right5(k, True)
-                    if i == 2:
                         left2(k, 1)
                     if i == 3:
                         left2(k, 0)
-                        left2(k, 2)
-                        left2(k, 3)
+                    for j in ((), (0,), (1,), (2,))[i]:
+                        right6(k, j)
+                    for j in ((), (), (2,), (3,))[i]:
+                        left2(k, j)
                 if live(r + 1):
                     if s == 1:
                         pair(r + 1)
@@ -450,9 +498,12 @@ def tile_kanlayerbspline_kernel(tc, x, coeff, bias, knots, out):
                     multiply(r - 1)
                 if s == 6 and live(r - 1):
                     finish(r - 1)
-                if s == 5 and 1 <= r + 2 < ROUNDS:
+                if s == 3 and 1 <= r + 2 < ROUNDS:
                     clip(r + 2)
                 if r == -2 and s == 7:
+                    turn_u(0)
+                    copy_u(0)
+                    return_u(0)
                     weights_of_the_terms()
                 if r == -1 and s == 6:
                     weights()

@@ -78,6 +78,14 @@ def tile_kanlayerbspline_kernel(tc, x, coeff, bias, knots, out):
 
         kn = const.tile([P, KN], F32)
         nc.vector.tensor_copy(out=kn[:], in_=kn_bf[:])
+        kn_neg = const.tile([P, KN], F32)
+        nc.vector.tensor_scalar_mul(out=kn_neg[:], in0=kn[:], scalar1=-1.0)
+        ident_pair = const.tile([P, P], BF16)
+        nc.vector.tensor_copy(
+            out=ident_pair[:].rearrange("p (u c s) -> p u c s", u=2, s=2),
+            in_=ident[:].rearrange("p (u s c) -> p u c s", u=2, s=2),
+        )
+        clip(0)
 
         def diff(a, b, nm):
             d = const.tile([P, 8], F32, name=nm)
@@ -107,8 +115,8 @@ def tile_kanlayerbspline_kernel(tc, x, coeff, bias, knots, out):
         nc.vector.memset(ones[:], 1.0)
         kap = const.tile([P, KN], F32)
         nc.vector.memset(kap[:], 1.0)
-        nc.vector.tensor_copy(out=kap[:, 0:4], in_=w0[:, 0:4])
-        nc.vector.tensor_copy(out=kap[:, 9:12], in_=w4[:, 5:8])
+        nc.vector.tensor_copy(out=kap[:, 0:2], in_=w0[:, 0:2])
+        nc.vector.tensor_copy(out=kap[:, 10:12], in_=w4[:, 6:8])
         nc.vector.tensor_tensor_scan(
             out=kap[:, 5:9], data0=rise[:, 4:8], data1=ones[:, 4:8], initial=1.0, op0=ALU.mult, op1=ALU.mult
         )
@@ -123,12 +131,9 @@ def tile_kanlayerbspline_kernel(tc, x, coeff, bias, knots, out):
         nc.vector.tensor_mul(out=beta_neg[:], in0=sig[:], in1=kn[:])
         beta = const.tile([P, KN], F32)
         nc.vector.tensor_scalar_mul(out=beta[:], in0=beta_neg[:], scalar1=-1.0)
-        kn_neg = const.tile([P, KN], F32)
-        nc.vector.tensor_scalar_mul(out=kn_neg[:], in0=kn[:], scalar1=-1.0)
-        clip(0)
 
         side_scale = const.tile([P, 2], F32)
-        tail8 = const.tile([P, 1], F32)
+        tail_factor = const.tile([P, 4], F32)
         fall3 = const.tile([P, 8], F32)
         fall2 = const.tile([P, 8], F32)
         rise2 = const.tile([P, 8], F32)
@@ -153,11 +158,12 @@ def tile_kanlayerbspline_kernel(tc, x, coeff, bias, knots, out):
             nc.vector.tensor_mul(out=q[:], in0=q[:], in1=kap[:, 0:8])
             nc.vector.tensor_mul(out=rise2[:], in0=q[:], in1=ikap[:, 2:10])
             nc.vector.tensor_scalar_mul(out=again6[:], in0=rise2[:, 4:8], scalar1=-1.0)
-            nc.vector.memset(again2[:], 0.0)
             nc.vector.reciprocal(out=again2[:, 1:4], in_=fall3[:, 0:3])
             nc.vector.tensor_mul(out=again2[:, 1:4], in0=again2[:, 1:4], in1=fall2[:, 1:4])
-            nc.vector.tensor_mul(out=tail8[:], in0=w4[:, 4:5], in1=ikap[:, 8:9])
-            nc.vector.tensor_scalar_mul(out=tail8[:], in0=tail8[:], scalar1=-1.0)
+            nc.vector.tensor_copy(out=tail_factor[:, 0:2], in_=w0[:, 2:4])
+            nc.vector.tensor_mul(out=tail_factor[:, 2:4], in0=w4[:, 4:6], in1=ikap[:, 8:10])
+            nc.vector.tensor_scalar_mul(out=tail_factor[:, 2:4], in0=tail_factor[:, 2:4], scalar1=-1.0)
+            nc.vector.tensor_scalar_mul(out=again2[:, 0:1], in0=fall2[:, 0:1], scalar1=-1.0)
             pick = const.tile([P, 4], F32, name="pick")
             nc.vector.tensor_reduce(
                 out=pick[:], in_=identf[:].rearrange("p (x j l) -> p j x l", x=8, j=4, l=4),
@@ -201,6 +207,7 @@ def tile_kanlayerbspline_kernel(tc, x, coeff, bias, knots, out):
         paired = {}
         turned = {}
         u_psum = {}
+        below = {}
         mids = {}
         outer = {}
         tails = {}
@@ -212,7 +219,7 @@ def tile_kanlayerbspline_kernel(tc, x, coeff, bias, knots, out):
         accs = {}
 
         def turn_u(r):
-            t = ps_o.tile([P, N // P, P], BF16, name="u_turned")
+            t = ps_o.tile([P, N // P, P], BF16, tag="acc", name="u_turned")
             for a in range(N // P):
                 nc.tensor.transpose(t[:, a, :], us[r][:, a * P:(a + 1) * P], ident[:])
             turned[r] = t
@@ -222,11 +229,11 @@ def tile_kanlayerbspline_kernel(tc, x, coeff, bias, knots, out):
             nc.scalar.copy(out=t[:], in_=turned[r][:])
             turned[r] = t
 
-        def return_u(r):
-            t = ps_o.tile([P, N], BF16, name="u_psum")
+        def return_u(r, nm, order):
+            t = ps_o.tile([P, N], BF16, name=nm)
             for a in range(N // P):
-                nc.tensor.transpose(t[:, a * P:(a + 1) * P], turned[r][:, a, :], ident[:])
-            u_psum[r] = t
+                nc.tensor.transpose(t[:, a * P:(a + 1) * P], turned[r][:, a, :], order[:])
+            u_psum[(r, nm)] = t
 
         def pair(r):
             t = one.tile([P, N], BF16, name="paired")
@@ -250,14 +257,20 @@ def tile_kanlayerbspline_kernel(tc, x, coeff, bias, knots, out):
 
         def square(r, i):
             t = work.tile([P, N], F32, name="sq")
+            b, a = beta[:, i:i + 1], sig[:, i:i + 1]
             if i in (0, 1, 10, 11):
                 src = clamped[i][:].rearrange("p a z -> p (a z)")
-                b = beta if i < 4 else beta_neg
+                if i > 4:
+                    b = beta_neg[:, i:i + 1]
+            elif i in (2, 3, 9):
+                src, b, a = paired[r][:], kn_neg[:, i:i + 1], 1.0
+            elif i == 8:
+                src = paired[r][:]
             else:
-                src, b = us[r][:], beta
-            nc.scalar.activation(
-                out=t[:], in_=src, func=ACT.Square, bias=b[:, i:i + 1], scale=sig[:, i:i + 1],
-            )
+                src = us[r][:]
+                if i == 4:
+                    b, a = kn_neg[:, i:i + 1], 1.0
+            nc.scalar.activation(out=t[:], in_=src, func=ACT.Square, bias=b, scale=a)
             squares[i] = t
 
         def knot_plane(t, j):
@@ -280,26 +293,27 @@ def tile_kanlayerbspline_kernel(tc, x, coeff, bias, knots, out):
             if 4 <= i < 8:
                 if r not in mids:
                     mids[r] = cub.tile([P, G, 16], F32, name="mids")
-                dst = knot_plane(mids[r][:], i - 4)
-            else:
-                pool = cub if i in (3, 8) else one
-                outer[(r, i)] = pool.tile([P, N], F32, name="outer%d" % i)
-                dst = outer[(r, i)][:].rearrange("p (g l) -> p g l", l=4)
+                nc.vector.scalar_tensor_tensor(
+                    out=knot_plane(mids[r][:], i - 4), in0=u_psum[(r, "u_own")][:].rearrange("p (g l) -> p g l", l=4),
+                    scalar=kn[:, i:i + 1], in1=squares[i][:].rearrange("p (g l) -> p g l", l=4),
+                    op0=ALU.subtract, op1=ALU.mult,
+                )
+                return
+            pool = cub if i in (3, 8) else one
+            outer[(r, i)] = pool.tile([P, N], F32, name="outer%d" % i)
             nc.vector.scalar_tensor_tensor(
-                out=dst, in0=u_psum[r][:].rearrange("p (g l) -> p g l", l=4), scalar=kn[:, i:i + 1],
-                in1=squares[i][:].rearrange("p (g l) -> p g l", l=4), op0=ALU.subtract, op1=ALU.mult,
+                out=outer[(r, i)][:], in0=u_psum[(r, "u_paired")][:], scalar=kn[:, i:i + 1], in1=squares[i][:],
+                op0=ALU.subtract, op1=ALU.mult,
             )
 
         def outer_tail(r, i):
-            src = outer[(r, i)][:].rearrange("p (a s v l) -> p a s v l", s=2, v=8, l=4)
             j = i % 4
-            dst = tails_of(r)[:, i // 8, :, 8 * j:8 * j + 8].rearrange("p (a v) (l s) -> p a v l s", v=8, s=2)
-            factor = {2: 1.0, 3: 1.0, 8: tail8[:, 0:1], 9: -1.0}[i]
-            for s in range(2):
-                nc.vector.tensor_scalar(
-                    out=dst[:, :, :, :, s], in0=src[:, :, s], scalar1=factor, scalar2=0.0,
-                    op0=ALU.mult, op1=ALU.max,
-                )
+            nc.vector.tensor_scalar(
+                out=tails_of(r)[:, i // 8, :, 8 * j:8 * j + 8],
+                in0=outer[(r, i)][:].rearrange("p (a z) -> p a z", z=8),
+                scalar1=tail_factor[:, {2: 0, 3: 1, 8: 2, 9: 3}[i]:{2: 1, 3: 2, 8: 3, 9: 4}[i]], scalar2=0.0,
+                op0=ALU.mult, op1=ALU.max,
+            )
 
         def terms_of(k):
             if k not in terms:
@@ -308,27 +322,28 @@ def tile_kanlayerbspline_kernel(tc, x, coeff, bias, knots, out):
                 }
             return terms[k]
 
-        def knot_half(k, i):
+        def plane_parts(k, nm, j, i):
             r, e = k // 2, k % 2
+            dst = terms_of(k)[nm][:]
             if 4 <= i < 8:
-                return knot_plane(mids[r][:, e * GH:(e + 1) * GH, :], i - 4)
-            return outer[(r, i)][:, e * HALF:(e + 1) * HALF].rearrange("p (g l) -> p g l", l=4)
+                return [(knot_plane(dst, j), knot_plane(mids[r][:, e * GH:(e + 1) * GH, :], i - 4))]
+            src = outer[(r, i)][:, e * HALF:(e + 1) * HALF].rearrange("p (a v l s) -> p a v l s", v=8, l=4, s=2)
+            dst = dst.rearrange("p (a s v) (j l) -> p a s v j l", s=2, v=8, l=4)
+            return [(dst[:, :, s, :, j, :], src[:, :, :, :, s]) for s in range(2)]
 
         def right5(k, last):
-            dst = terms_of(k)["right5"]
             r, e = k // 2, k % 2
             if last:
-                o, i = dst[:, :, 12:16], knot_half(k, 8)
+                parts = plane_parts(k, "right5", 3, 8)
             else:
-                o, i = dst[:, :, 0:12], mids[r][:, e * GH:(e + 1) * GH, 4:16]
-            nc.vector.tensor_scalar(out=o, in0=i, scalar1=-1.0, scalar2=0.0, op0=ALU.mult, op1=ALU.min)
+                parts = [(terms_of(k)["right5"][:, :, 0:12], mids[r][:, e * GH:(e + 1) * GH, 4:16])]
+            for o, i in parts:
+                nc.vector.tensor_scalar(out=o, in0=i, scalar1=-1.0, scalar2=0.0, op0=ALU.mult, op1=ALU.min)
 
         def right6(k, j):
             if j == 3:
-                nc.scalar.activation(
-                    out=knot_plane(terms_of(k)["right6"][:], j), in_=knot_half(k, j + 6), func=ACT.Relu,
-                    scale=rise2[:, 4 + j:5 + j],
-                )
+                for o, i in plane_parts(k, "right6", 3, 9):
+                    nc.scalar.activation(out=o, in_=i, func=ACT.Relu, scale=rise2[:, 7:8])
                 return
             nc.gpsimd.tensor_scalar(
                 out=knot_plane(terms_of(k)["right6"][:], j), in0=knot_plane(terms_of(k)["right5"][:], j + 1),
@@ -336,22 +351,33 @@ def tile_kanlayerbspline_kernel(tc, x, coeff, bias, knots, out):
             )
 
         def left3(k, j):
+            for o, i in plane_parts(k, "left3", j, j + 3):
+                if j == 3:
+                    nc.vector.tensor_scalar(
+                        out=o, in0=i, scalar1=fall3[:, j:j + 1], scalar2=0.0, op0=ALU.mult, op1=ALU.max
+                    )
+                else:
+                    nc.scalar.activation(out=o, in_=i, func=ACT.Relu, scale=fall3[:, j:j + 1])
+
+        def below2(k):
+            r, e = k // 2, k % 2
+            t = sets.tile([P, HALF], F32, name="below")
             nc.scalar.activation(
-                out=knot_plane(terms_of(k)["left3"][:], j), in_=knot_half(k, j + 3), func=ACT.Relu,
-                scale=fall3[:, j:j + 1],
+                out=t[:], in_=outer[(r, 2)][:, e * HALF:(e + 1) * HALF], func=ACT.Relu, scale=-1.0
             )
+            below[k] = t
 
         def left2(k, j):
-            if j >= 2:
+            if j == 0:
+                src = below[k][:].rearrange("p (a v l s) -> p a v l s", v=8, l=4, s=2)
+                dst = terms_of(k)["left2"][:].rearrange("p (a s v) (j l) -> p a s v j l", s=2, v=8, l=4)
+                parts = [(dst[:, :, s, :, 0, :], src[:, :, :, :, s]) for s in range(2)]
+            else:
+                parts = [(knot_plane(terms_of(k)["left2"][:], j), knot_plane(terms_of(k)["left3"][:], j - 1))]
+            for o, i in parts:
                 nc.gpsimd.tensor_scalar(
-                    out=knot_plane(terms_of(k)["left2"][:], j), in0=knot_plane(terms_of(k)["left3"][:], j - 1),
-                    scalar1=again2[:, j:j + 1], scalar2=0.0, op0=ALU.mult, op1=ALU.add,
+                    out=o, in0=i, scalar1=again2[:, j:j + 1], scalar2=0.0, op0=ALU.mult, op1=ALU.add,
                 )
-                return
-            nc.vector.tensor_scalar(
-                out=knot_plane(terms_of(k)["left2"][:], j), in0=knot_half(k, j + 2),
-                scalar1=fall2[:, j:j + 1], scalar2=0.0, op0=ALU.mult, op1=ALU.min,
-            )
 
         def sums(r, s):
             e, n = s // NT, s % NT
@@ -409,7 +435,7 @@ def tile_kanlayerbspline_kernel(tc, x, coeff, bias, knots, out):
             coded[(r, e)] = (codes, scales)
 
         def multiply(r):
-            acc = ps_o.tile([P, NT, O], F32, name="acc")
+            acc = ps_o.tile([P, NT, O], F32, tag="acc", name="acc")
             for n in range(NT):
                 for c in range(PASSES):
                     codes, scales = coded[(r, c // 2)]
@@ -430,8 +456,8 @@ def tile_kanlayerbspline_kernel(tc, x, coeff, bias, knots, out):
             )
             nc.sync.dma_start(out=out[rows_of(r), :].rearrange("(p n) o -> p n o", n=NT), in_=out_sb[:])
 
-        square_plan = ((4,), (5, 6), (7,), (9, 2), (0,), (1, 10), (11,), (8, 3))
-        cube_plan = ((8, 3), (4,), (5, 6), (7,), (9, 2), (0,), (1, 10), (11,))
+        square_plan = ((4,), (5, 6), (7,), (9, 2), (0,), (1, 10), (11,), (3, 8))
+        cube_plan = ((3, 8), (4,), (5, 6), (7,), (9, 2), (0,), (1, 10), (11,))
         clamp_plan = {3: (0,), 4: (1, 10), 5: (11,)}
         outer_tail_plan = {1: 8, 3: 3, 6: 2, 7: 9}
 
@@ -449,21 +475,28 @@ def tile_kanlayerbspline_kernel(tc, x, coeff, bias, knots, out):
                     sums(r, s)
                 if live(prev[0]):
                     turn_tails(*prev)
-                if s == 5 and 1 <= r + 2 < ROUNDS:
-                    turn_u(r + 2)
-                if s == 7 and 1 <= r + 2 < ROUNDS:
-                    return_u(r + 2)
+                if live(r + 2):
+                    if s == 3:
+                        turn_u(r + 2)
+                    if s == 6:
+                        return_u(r + 2, "u_paired", ident_pair)
+                    if s == 7:
+                        return_u(r + 2, "u_own", ident)
+                if s == 5 and live(r - 1):
+                    multiply(r - 1)
                 if live(prev[0]):
                     read_sums(*prev)
-                if s == 6 and 1 <= r + 2 < ROUNDS:
+                if s == 4 and live(r + 2):
                     copy_u(r + 2)
                 later = r + 2 if s == 7 else r + 1
                 for knot in square_plan[s]:
                     if live(later):
                         square(later, knot)
                 if live(k // 2):
-                    for j in ((0, 1), (2,), (3,), ())[i]:
+                    for j in ((0, 1), (2,), (), ())[i]:
                         left3(k, j)
+                    if i == 2:
+                        below2(k)
                     if i == 3:
                         right6(k, 3)
                 for knot in cube_plan[s]:
@@ -474,36 +507,30 @@ def tile_kanlayerbspline_kernel(tc, x, coeff, bias, knots, out):
                         right5(k, False)
                     if i == 1:
                         right5(k, True)
-                        left2(k, 1)
-                    if i == 3:
-                        left2(k, 0)
+                    if i == 2:
+                        left3(k, 3)
                     for j in ((), (0,), (1,), (2,))[i]:
                         right6(k, j)
-                    for j in ((), (), (2,), (3,))[i]:
+                    for j in ((), (1,), (2,), (3, 0))[i]:
                         left2(k, j)
+                if r == -1 and s == 1:
+                    weights_of_the_terms()
                 if live(r + 1):
-                    if s == 1:
-                        pair(r + 1)
                     for knot in clamp_plan.get(s, ()):
                         clamp(r + 1, knot)
                     if s in outer_tail_plan:
                         outer_tail(r + 1, outer_tail_plan[s])
                 if live(prev[0]):
                     take_tails(*prev)
-                if s == 5 and live(r):
+                if s == 6 and live(r):
                     quantise(r, 0)
                 if s == 2 and live(r - 1):
                     quantise(r - 1, 1)
-                if s == 4 and live(r - 1):
-                    multiply(r - 1)
-                if s == 6 and live(r - 1):
+                if s == 7 and live(r - 1):
                     finish(r - 1)
-                if s == 3 and 1 <= r + 2 < ROUNDS:
+                if s == 2 and 1 <= r + 2 < ROUNDS:
                     clip(r + 2)
-                if r == -2 and s == 7:
-                    turn_u(0)
-                    copy_u(0)
-                    return_u(0)
-                    weights_of_the_terms()
+                if s == 6 and live(r + 2):
+                    pair(r + 2)
                 if r == -1 and s == 6:
                     weights()

@@ -493,11 +493,13 @@ def tile_kanlayerbspline_kernel(tc, x, coeff, bias, knots, out):
                     if live(later):
                         square(later, knot)
                 if live(k // 2):
-                    for j in ((0, 1), (2,), (), ())[i]:
-                        left3(k, j)
-                    if i == 2:
+                    if i == 0:
+                        left3(k, 0)
+                        left3(k, 1)
+                        left3(k, 2)
+                    if i == 1:
                         below2(k)
-                    if i == 3:
+                    if i == 2:
                         right6(k, 3)
                 for knot in cube_plan[s]:
                     if live(r + 1):
@@ -505,13 +507,12 @@ def tile_kanlayerbspline_kernel(tc, x, coeff, bias, knots, out):
                 if live(k // 2):
                     if i == 0:
                         right5(k, False)
-                    if i == 1:
                         right5(k, True)
-                    if i == 2:
+                    if i == 1:
                         left3(k, 3)
-                    for j in ((), (0,), (1,), (2,))[i]:
+                    for j in ((0, 1), (2,), (), ())[i]:
                         right6(k, j)
-                    for j in ((), (1,), (2,), (3, 0))[i]:
+                    for j in ((), (1, 2), (3, 0), ())[i]:
                         left2(k, j)
                 if r == -1 and s == 1:
                     weights_of_the_terms()

from contextlib import ExitStack

import concourse.mybir as mybir
from concourse.masks import make_identity

F32 = mybir.dt.float32
BF16 = mybir.dt.bfloat16
U32 = mybir.dt.uint32
U8 = mybir.dt.uint8
FP8X4 = mybir.dt.float8_e4m3fn_x4
ALU = mybir.AluOpType
ACT = mybir.ActivationFunctionType
AX = mybir.AxisListType

B, D, O, NC = 16384, 256, 128, 8
K = D * NC
FLOPS = 2 * B * K * O
P = 128
PASSES = 4
NT = 4
N = NT * D
HALF = N // 2
G = N // 4
GH = G // 2
KN = 12
ROUNDS = B // (NT * P)
SLOTS = 8


def tile_kanlayerbspline_kernel(tc, x, coeff, bias, knots, out):
    nc = tc.nc
    with ExitStack() as ctx:
        const = ctx.enter_context(tc.tile_pool(name="const", bufs=1))
        xin = ctx.enter_context(tc.tile_pool(name="xin", bufs=2))
        cub = ctx.enter_context(tc.tile_pool(name="cub", bufs=2))
        sets = ctx.enter_context(tc.tile_pool(name="sets", bufs=2))
        one = ctx.enter_context(tc.tile_pool(name="one", bufs=1))
        work = ctx.enter_context(tc.tile_pool(name="work", bufs=4))
        ps_q = ctx.enter_context(tc.psum_pool(name="ps_q", bufs=3))
        ps_t = ctx.enter_context(tc.psum_pool(name="ps_t", bufs=2))
        ps_o = ctx.enter_context(tc.psum_pool(name="ps_o", bufs=1))
        ctx.enter_context(tc.manual_schedule())

        def rows_of(r):
            return slice(r * NT * P, (r + 1) * NT * P)

        xs = {}
        us = {}

        def load(r):
            t = xin.tile([P, NT, D], BF16, name="x_nat")
            nc.sync.dma_start(out=t[:], in_=x[rows_of(r), :].rearrange("(p n) d -> p n d", n=NT))
            xs[r] = t

        def clip(r):
            t = xin.tile([P, N], BF16, name="u")
            dst = t[:].rearrange("p (e n t v z) -> p e n t v z", e=2, n=NT, t=4, v=2)
            src = xs[r][:].rearrange("p n (e v t z) -> p n e v t z", e=2, v=2, t=4)
            for e in range(2):
                for v in range(2):
                    nc.vector.tensor_scalar(
                        out=dst[:, e, :, :, v, :], in0=src[:, :, e, v], scalar1=-1.0, scalar2=1.0,
                        op0=ALU.max, op1=ALU.min,
                    )
            us[r] = t

        kn_bf = const.tile([P, KN], BF16)
        nc.sync.dma_start(out=kn_bf[:], in_=knots.partition_broadcast(P))
        load(0)
        w_nat = const.tile([P, K], BF16)
        nc.sync.dma_start(out=w_nat[:], in_=coeff.rearrange("o d m -> o (d m)"))
        bias_bf = const.tile([P, O], BF16)
        nc.sync.dma_start(out=bias_bf[:], in_=bias.partition_broadcast(P))
        ident = const.tile([P, P], BF16)
        make_identity(nc, ident[:])
        identf = const.tile([P, P], F32)
        make_identity(nc, identf[:])

        kn = const.tile([P, KN], F32)
        nc.vector.tensor_copy(out=kn[:], in_=kn_bf[:])
        kn_neg = const.tile([P, KN], F32)
        nc.vector.tensor_scalar_mul(out=kn_neg[:], in0=kn[:], scalar1=-1.0)
        ident_pair = const.tile([P, P], BF16)
        nc.vector.tensor_copy(
            out=ident_pair[:].rearrange("p (u c s) -> p u c s", u=2, s=2),
            in_=ident[:].rearrange("p (u s c) -> p u c s", u=2, s=2),
        )
        clip(0)

        def diff(a, b, nm):
            d = const.tile([P, 8], F32, name=nm)
            nc.vector.tensor_sub(out=d[:], in0=kn[:, a:a + 8], in1=kn[:, b:b + 8])
            return d

        def product(factors, nm):
            d = factors[0]
            for i, f in enumerate(factors[1:]):
                p = const.tile([P, 8], F32, name="%s_%d" % (nm, i))
                nc.vector.tensor_mul(out=p[:], in0=d[:], in1=f[:])
                d = p
            return d

        def inverse(a, nm):
            d = const.tile([P, 8], F32, name=nm)
            nc.vector.reciprocal(out=d[:], in_=a[:])
            return d

        d10, d20, d30, d40 = diff(1, 0, "d10"), diff(2, 0, "d20"), diff(3, 0, "d30"), diff(4, 0, "d40")
        d21, d31, d41 = diff(2, 1, "d21"), diff(3, 1, "d31"), diff(4, 1, "d41")
        d42, d43 = diff(4, 2, "d42"), diff(4, 3, "d43")
        w0 = inverse(product([d10, d20, d30], "p0"), "w0")
        w4 = inverse(product([d41, d42, d43], "p4"), "w4")
        rise = product([d40, d20, d30, inverse(product([d21, d31, d41], "p1"), "i1")], "rise")
        ones = const.tile([P, 8], F32)
        nc.vector.memset(ones[:], 1.0)
        kap = const.tile([P, KN], F32)
        nc.vector.memset(kap[:], 1.0)
        nc.vector.tensor_copy(out=kap[:, 0:2], in_=w0[:, 0:2])
        nc.vector.tensor_copy(out=kap[:, 10:12], in_=w4[:, 6:8])
        nc.vector.tensor_tensor_scan(
            out=kap[:, 5:9], data0=rise[:, 4:8], data1=ones[:, 4:8], initial=1.0, op0=ALU.mult, op1=ALU.mult
        )
        sig0 = const.tile([P, KN], F32)
        nc.scalar.activation(out=sig0[:], in_=kap[:], func=ACT.Sqrt)
        sig = const.tile([P, KN], F32)
        nc.vector.reciprocal(out=sig[:], in_=sig0[:])
        nc.vector.tensor_mul(out=sig[:], in0=sig[:], in1=kap[:])
        nc.vector.tensor_add(out=sig[:], in0=sig[:], in1=sig0[:])
        nc.vector.tensor_scalar_mul(out=sig[:], in0=sig[:], scalar1=0.5)
        beta_neg = const.tile([P, KN], F32)
        nc.vector.tensor_mul(out=beta_neg[:], in0=sig[:], in1=kn[:])
        beta = const.tile([P, KN], F32)
        nc.vector.tensor_scalar_mul(out=beta[:], in0=beta_neg[:], scalar1=-1.0)

        side_scale = const.tile([P, 2], F32)
        tail_factor = const.tile([P, 4], F32)
        fall3 = const.tile([P, 8], F32)
        fall2 = const.tile([P, 8], F32)
        rise2 = const.tile([P, 8], F32)
        again6 = const.tile([P, 4], F32)
        again2 = const.tile([P, 4], F32)
        w_codes = const.tile([P, PASSES * O], U32, align_bytes=64)
        w_scales = const.tile([P, PASSES * O], U8, align_bytes=64)
        bias_f = const.tile([P, O], F32)

        def weights_of_the_terms():
            d32 = diff(3, 2, "d32")
            ikap = const.tile([P, KN], F32, name="ikap")
            nc.vector.reciprocal(out=ikap[:], in_=kap[:])
            q = product([d40, d41, d42, inverse(product([d30, d31, d32], "p3"), "i3")], "f3")
            nc.vector.tensor_mul(out=q[:], in0=q[:], in1=kap[:, 4:12])
            nc.vector.tensor_mul(out=q[:], in0=q[:], in1=ikap[:, 3:11])
            nc.vector.tensor_scalar_mul(out=fall3[:], in0=q[:], scalar1=-1.0)
            q = product([d40, d41, d43, inverse(product([d20, d21, d32], "p2"), "i2")], "f2")
            nc.vector.tensor_mul(out=q[:], in0=q[:], in1=kap[:, 4:12])
            nc.vector.tensor_mul(out=fall2[:], in0=q[:], in1=ikap[:, 2:10])
            q = product([d40, d10, d30, inverse(product([d21, d32, d42], "p5"), "i5")], "r2")
            nc.vector.tensor_mul(out=q[:], in0=q[:], in1=kap[:, 0:8])
            nc.vector.tensor_mul(out=rise2[:], in0=q[:], in1=ikap[:, 2:10])
            nc.vector.tensor_scalar_mul(out=again6[:], in0=rise2[:, 4:8], scalar1=-1.0)
            nc.vector.reciprocal(out=again2[:, 1:4], in_=fall3[:, 0:3])
            nc.vector.tensor_mul(out=again2[:, 1:4], in0=again2[:, 1:4], in1=fall2[:, 1:4])
            nc.vector.tensor_copy(out=tail_factor[:, 0:2], in_=w0[:, 2:4])
            nc.vector.tensor_mul(out=tail_factor[:, 2:4], in0=w4[:, 4:6], in1=ikap[:, 8:10])
            nc.vector.tensor_scalar_mul(out=tail_factor[:, 2:4], in0=tail_factor[:, 2:4], scalar1=-1.0)
            nc.vector.tensor_scalar_mul(out=again2[:, 0:1], in0=fall2[:, 0:1], scalar1=-1.0)
            pick = const.tile([P, 4], F32, name="pick")
            nc.vector.tensor_reduce(
                out=pick[:], in_=identf[:].rearrange("p (x j l) -> p j x l", x=8, j=4, l=4),
                op=ALU.add, axis=AX.XY,
            )
            s = const.tile([P, 2, 4], F32, name="s")
            nc.vector.tensor_scalar_mul(out=s[:, 0, :], in0=w4[:, 0:4], scalar1=-1.0)
            nc.vector.tensor_copy(out=s[:, 1, :], in_=w0[:, 4:8])
            for h in range(2):
                nc.vector.tensor_mul(out=s[:, h, :], in0=s[:, h, :], in1=ikap[:, 4:8])
                nc.vector.tensor_mul(out=s[:, h, :], in0=s[:, h, :], in1=pick[:])
            nc.vector.tensor_reduce(out=side_scale[:], in_=s[:], op=ALU.add, axis=AX.X)

        def weights():
            nc.vector.tensor_copy(out=bias_f[:], in_=bias_bf[:])
            w_perm = xin.tile([P, PASSES, 4, P], BF16, tag="grouped", name="w_perm", align_bytes=64)
            wv = w_nat[:].rearrange("o (e v t q l h j) -> o e h t v q j l", e=2, v=2, t=4, q=4, l=4, h=2, j=4)
            for c in range(PASSES):
                for t in range(4):
                    for v in range(2):
                        nc.scalar.copy(
                            out=w_perm[:, c, t, 64 * v:64 * v + 64].rearrange(
                                "o (q j l) -> o q j l", q=4, j=4
                            ),
                            in_=wv[:, c // 2, c % 2, t, v],
                        )
            w_grp = xin.tile([P, PASSES, O, 4], BF16, tag="grouped", name="w_grp", align_bytes=64)
            for c in range(PASSES):
                wT = ps_q.tile([P, 4, P], BF16, tag="Q")
                for t in range(4):
                    nc.tensor.transpose(wT[:, t, :], w_perm[:, c, t, :], ident[:])
                nc.vector.tensor_copy(out=w_grp[:, c, :, :], in_=wT[:].rearrange("p t o -> p o t"))
            nc.vector.quantize_mx(
                out=w_codes[:].bitcast(FP8X4),
                scales=w_scales[:],
                in_=w_grp[:].rearrange("p c o t -> p (c o t)"),
            )

        squares = {}
        clamped = {}
        paired = {}
        turned = {}
        u_psum = {}
        below = {}
        mids = {}
        outer = {}
        tails = {}
        terms = {}
        q_banks = {}
        t_banks = {}
        grouped = {}
        coded = {}
        accs = {}

        def turn_u(r):
            t = ps_o.tile([P, N // P, P], BF16, tag="acc", name="u_turned")
            for a in range(N // P):
                nc.tensor.transpose(t[:, a, :], us[r][:, a * P:(a + 1) * P], ident[:])
            turned[r] = t

        def copy_u(r):
            t = one.tile([P, N // P, P], BF16, name="u_across")
            nc.scalar.copy(out=t[:], in_=turned[r][:])
            turned[r] = t

        def return_u(r, nm, order):
            t = ps_o.tile([P, N], BF16, name=nm)
            for a in range(N // P):
                nc.tensor.transpose(t[:, a * P:(a + 1) * P], turned[r][:, a, :], order[:])
            u_psum[(r, nm)] = t

        def pair(r):
            t = one.tile([P, N], BF16, name="paired")
            nc.vector.tensor_copy(
                out=t[:].rearrange("p (a c s) -> p a c s", s=2, c=32),
                in_=us[r][:].rearrange("p (a s c) -> p a c s", s=2, c=32),
            )
            paired[r] = t

        def clamp(r, i):
            t = work.tile([P, N // 8, 8], BF16, name="z")
            dst = t[:].rearrange("p a z -> p (a z)")
            src = paired[r][:]
            if i < 4:
                nc.vector.tensor_scalar(out=dst, in0=src, scalar1=kn[:, i:i + 1], scalar2=None, op0=ALU.max)
            else:
                nc.vector.tensor_scalar(
                    out=dst, in0=src, scalar1=-1.0, scalar2=kn_neg[:, i:i + 1], op0=ALU.mult, op1=ALU.max
                )
            clamped[i] = t

        def square(r, i):
            t = work.tile([P, N], F32, name="sq")
            b, a = beta[:, i:i + 1], sig[:, i:i + 1]
            if i in (0, 1, 10, 11):
                src = clamped[i][:].rearrange("p a z -> p (a z)")
                if i > 4:
                    b = beta_neg[:, i:i + 1]
            elif i in (2, 3, 9):
                src, b, a = paired[r][:], kn_neg[:, i:i + 1], 1.0
            elif i == 8:
                src = paired[r][:]
            else:
                src = us[r][:]
                if i == 4:
                    b, a = kn_neg[:, i:i + 1], 1.0
            nc.scalar.activation(out=t[:], in_=src, func=ACT.Square, bias=b, scale=a)
            squares[i] = t

        def knot_plane(t, j):
            return t.rearrange("p g (j l) -> p g j l", l=4)[:, :, j, :]

        def tails_of(r):
            if r not in tails:
                tails[r] = cub.tile([P, 2, N // 8, 32], BF16, name="tails")
            return tails[r]

        def cube(r, i):
            if i in (0, 1, 10, 11):
                k = kn if i < 4 else kn_neg
                j = i % 4
                nc.vector.scalar_tensor_tensor(
                    out=tails_of(r)[:, i // 8, :, 8 * j:8 * j + 8], in0=clamped[i][:], scalar=k[:, i:i + 1],
                    in1=squares[i][:].rearrange("p (a z) -> p a z", z=8), op0=ALU.subtract, op1=ALU.mult,
                )
                return
            if 4 <= i < 8:
                if r not in mids:
                    mids[r] = cub.tile([P, G, 16], F32, name="mids")
                nc.vector.scalar_tensor_tensor(
                    out=knot_plane(mids[r][:], i - 4), in0=u_psum[(r, "u_own")][:].rearrange("p (g l) -> p g l", l=4),
                    scalar=kn[:, i:i + 1], in1=squares[i][:].rearrange("p (g l) -> p g l", l=4),
                    op0=ALU.subtract, op1=ALU.mult,
                )
                return
            pool = cub if i in (3, 8) else one
            outer[(r, i)] = pool.tile([P, N], F32, name="outer%d" % i)
            nc.vector.scalar_tensor_tensor(
                out=outer[(r, i)][:], in0=u_psum[(r, "u_paired")][:], scalar=kn[:, i:i + 1], in1=squares[i][:],
                op0=ALU.subtract, op1=ALU.mult,
            )

        def outer_tail(r, i):
            j = i % 4
            nc.vector.tensor_scalar(
                out=tails_of(r)[:, i // 8, :, 8 * j:8 * j + 8],
                in0=outer[(r, i)][:].rearrange("p (a z) -> p a z", z=8),
                scalar1=tail_factor[:, {2: 0, 3: 1, 8: 2, 9: 3}[i]:{2: 1, 3: 2, 8: 3, 9: 4}[i]], scalar2=0.0,
                op0=ALU.mult, op1=ALU.max,
            )

        def terms_of(k):
            if k not in terms:
                terms[k] = {
                    nm: sets.tile([P, GH, 16], F32, name=nm) for nm in ("right5", "right6", "left3", "left2")
                }
            return terms[k]

        def plane_parts(k, nm, j, i):
            r, e = k // 2, k % 2
            dst = terms_of(k)[nm][:]
            if 4 <= i < 8:
                return [(knot_plane(dst, j), knot_plane(mids[r][:, e * GH:(e + 1) * GH, :], i - 4))]
            src = outer[(r, i)][:, e * HALF:(e + 1) * HALF].rearrange("p (a v l s) -> p a v l s", v=8, l=4, s=2)
            dst = dst.rearrange("p (a s v) (j l) -> p a s v j l", s=2, v=8, l=4)
            return [(dst[:, :, s, :, j, :], src[:, :, :, :, s]) for s in range(2)]

        def right5(k, last):
            r, e = k // 2, k % 2
            if last:
                parts = plane_parts(k, "right5", 3, 8)
            else:
                parts = [(terms_of(k)["right5"][:, :, 0:12], mids[r][:, e * GH:(e + 1) * GH, 4:16])]
            for o, i in parts:
                nc.vector.tensor_scalar(out=o, in0=i, scalar1=-1.0, scalar2=0.0, op0=ALU.mult, op1=ALU.min)

        def right6(k, j):
            if j == 3:
                for o, i in plane_parts(k, "right6", 3, 9):
                    nc.scalar.activation(out=o, in_=i, func=ACT.Relu, scale=rise2[:, 7:8])
                return
            nc.gpsimd.tensor_scalar(
                out=knot_plane(terms_of(k)["right6"][:], j), in0=knot_plane(terms_of(k)["right5"][:], j + 1),
                scalar1=again6[:, j:j + 1], scalar2=0.0, op0=ALU.mult, op1=ALU.add,
            )

        def left3(k, j):
            for o, i in plane_parts(k, "left3", j, j + 3):
                if j == 3:
                    nc.vector.tensor_scalar(
                        out=o, in0=i, scalar1=fall3[:, j:j + 1], scalar2=0.0, op0=ALU.mult, op1=ALU.max
                    )
                else:
                    nc.scalar.activation(out=o, in_=i, func=ACT.Relu, scale=fall3[:, j:j + 1])

        def below2(k):
            r, e = k // 2, k % 2
            t = sets.tile([P, HALF], F32, name="below")
            nc.scalar.activation(
                out=t[:], in_=outer[(r, 2)][:, e * HALF:(e + 1) * HALF], func=ACT.Relu, scale=-1.0
            )
            below[k] = t

        def left2(k, j):
            if j == 0:
                src = below[k][:].rearrange("p (a v l s) -> p a v l s", v=8, l=4, s=2)
                dst = terms_of(k)["left2"][:].rearrange("p (a s v) (j l) -> p a s v j l", s=2, v=8, l=4)
                parts = [(dst[:, :, s, :, 0, :], src[:, :, :, :, s]) for s in range(2)]
            else:
                parts = [(knot_plane(terms_of(k)["left2"][:], j), knot_plane(terms_of(k)["left3"][:], j - 1))]
            for o, i in parts:
                nc.gpsimd.tensor_scalar(
                    out=o, in0=i, scalar1=again2[:, j:j + 1], scalar2=0.0, op0=ALU.mult, op1=ALU.add,
                )

        def sums(r, s):
            e, n = s // NT, s % NT
            k = 2 * r + e
            bank = ps_q.tile([P, 4, P], F32, tag="Q", name="q_bank")
            tm = terms_of(k)
            for t in range(4):
                g = n * 32 + t * 8
                parts = [mids[r][:, e * GH + g:e * GH + g + 8, :]]
                parts += [tm[nm][:, g:g + 8, :] for nm in ("right5", "right6", "left3", "left2")]
                for i, part in enumerate(parts):
                    nc.tensor.matmul(
                        out=bank[:, t, :], lhsT=part.rearrange("p g z -> p (g z)"), rhs=identf[:],
                        is_transpose=True, start=(i == 0), stop=(i == len(parts) - 1),
                    )
            q_banks[(r, s)] = bank

        def turn_tails(r, s):
            bank = ps_t.tile([P, 2, P, 2], F32, name="t_bank")
            words = tails[r][:].rearrange("p h a z -> p h (a z)").bitcast(F32)
            for h in range(2):
                for u in range(2):
                    a = (s * 2 + u) * P
                    nc.tensor.matmul(
                        out=bank[:, h, :, u], lhsT=words[:, h, a:a + P], rhs=identf[:],
                        is_transpose=True, start=True, stop=True,
                    )
            t_banks[(r, s)] = bank

        def read_sums(r, s):
            e, n = s // NT, s % NT
            if n == 0:
                grouped[(r, e)] = xin.tile([P, NT, 2, P, 4], BF16, tag="grouped", name="grouped", align_bytes=64)
            for h in range(2):
                nc.scalar.activation(
                    out=grouped[(r, e)][:, n, h], in_=q_banks[(r, s)][:].rearrange("p t b -> p b t"),
                    func=ACT.Relu, scale=side_scale[:, h:h + 1],
                )

        def take_tails(r, s):
            e, n = s // NT, s % NT
            o = grouped[(r, e)][:, n].rearrange("p h b t -> p (h b t)")
            nc.vector.tensor_tensor(
                out=o, in0=t_banks[(r, s)][:].rearrange("p h b u -> p (h b u)").bitcast(BF16), in1=o, op=ALU.min
            )

        def quantise(r, e):
            codes = one.tile([P, NT, 2, P], U32, name="codes%d" % e, align_bytes=64)
            scales = one.tile([P, NT, 2, P], U8, name="scales%d" % e, align_bytes=64)
            nc.vector.quantize_mx(
                out=codes[:].rearrange("p n h b -> p (n h b)").bitcast(FP8X4),
                scales=scales[:].rearrange("p n h b -> p (n h b)"),
                in_=grouped[(r, e)][:].rearrange("p n h b t -> p (n h b t)"),
            )
            coded[(r, e)] = (codes, scales)

        def multiply(r):
            acc = ps_o.tile([P, NT, O], F32, tag="acc", name="acc")
            for n in range(NT):
                for c in range(PASSES):
                    codes, scales = coded[(r, c // 2)]
                    nc.tensor.matmul_mx(
                        out=acc[:, n, :],
                        lhsT=codes[:, n, c % 2, :].bitcast(FP8X4), lhsT_scale=scales[:, n, c % 2, :],
                        rhs=w_codes[:, c * O:(c + 1) * O].bitcast(FP8X4),
                        rhs_scale=w_scales[:, c * O:(c + 1) * O],
                        start=(c == 0), stop=(c == PASSES - 1),
                    )
            accs[r] = acc

        def finish(r):
            out_sb = xin.tile([P, NT, O], F32, name="out_sb")
            nc.vector.tensor_tensor(
                out=out_sb[:], in0=accs[r][:], in1=bias_f[:].unsqueeze(1).to_broadcast([P, NT, O]),
                op=ALU.add,
            )
            nc.sync.dma_start(out=out[rows_of(r), :].rearrange("(p n) o -> p n o", n=NT), in_=out_sb[:])

        square_plan = ((4,), (5, 6), (7,), (9, 2), (0,), (1, 10), (11,), (3, 8))
        cube_plan = ((3, 8), (4,), (5, 6), (7,), (9, 2), (0,), (1, 10), (11,))
        clamp_plan = {3: (0,), 4: (1, 10), 5: (11,)}
        outer_tail_plan = {1: 8, 3: 3, 6: 2, 7: 9}

        def live(r):
            return 0 <= r < ROUNDS

        for r in range(-2, ROUNDS + 1):
            if 1 <= r + 2 < ROUNDS:
                load(r + 2)
            for s in range(SLOTS):
                prev = (r, s - 1) if s > 0 else (r - 1, SLOTS - 1)
                i = s % 4
                k = 2 * r + (1 if s < 4 else 2)
                if live(r):
                    sums(r, s)
                if live(prev[0]):
                    turn_tails(*prev)
                if live(r + 2):
                    if s == 3:
                        turn_u(r + 2)
                    if s == 6:
                        return_u(r + 2, "u_paired", ident_pair)
                    if s == 7:
                        return_u(r + 2, "u_own", ident)
                if s == 5 and live(r - 1):
                    multiply(r - 1)
                if live(prev[0]):
                    read_sums(*prev)
                if s == 4 and live(r + 2):
                    copy_u(r + 2)
                later = r + 2 if s == 7 else r + 1
                for knot in square_plan[s]:
                    if live(later):
                        square(later, knot)
                if live(k // 2):
                    if i == 0:
                        left3(k, 0)
                        left3(k, 1)
                        left3(k, 2)
                    if i == 1:
                        below2(k)
                    if i == 2:
                        right6(k, 3)
                for knot in cube_plan[s]:
                    if live(r + 1):
                        cube(r + 1, knot)
                if live(k // 2):
                    if i == 0:
                        right5(k, False)
                        right5(k, True)
                    if i == 1:
                        left3(k, 3)
                    for j in ((0, 1), (2,), (), ())[i]:
                        right6(k, j)
                    for j in ((), (1, 2), (3, 0), ())[i]:
                        left2(k, j)
                if r == -1 and s == 1:
                    weights_of_the_terms()
                if live(r + 1):
                    for knot in clamp_plan.get(s, ()):
                        clamp(r + 1, knot)
                    if s in outer_tail_plan:
                        outer_tail(r + 1, outer_tail_plan[s])
                if live(prev[0]):
                    take_tails(*prev)
                if s == 6 and live(r):
                    quantise(r, 0)
                if s == 2 and live(r - 1):
                    quantise(r - 1, 1)
                if s == 7 and live(r - 1):
                    finish(r - 1)
                if s == 2 and 1 <= r + 2 < ROUNDS:
                    clip(r + 2)
                if s == 6 and live(r + 2):
                    pair(r + 2)
                if r == -1 and s == 6:
                    weights()
